import numpy as np
import ml_dtypes


def mxq(x, axis, fmt="e4m3"):
    dtype, down = {"e4m3": (ml_dtypes.float8_e4m3fn, 7), "e5m2": (ml_dtypes.float8_e5m2, 14)}[fmt]
    v = np.moveaxis(np.asarray(x, np.float32).astype(ml_dtypes.bfloat16).astype(np.float64), axis, -1)
    blocks = v.reshape(v.shape[:-1] + (-1, 32))
    amax = np.abs(blocks).max(-1, keepdims=True)
    byte = np.maximum(np.where(amax > 0, np.frexp(amax)[1] - 1 + 127, 0) - down, 1)
    scale = np.exp2(byte - 127.0)
    codes = (blocks / scale).astype(np.float32).astype(dtype).astype(np.float64)
    return np.moveaxis((codes * scale).reshape(v.shape), -1, axis)


WIDE = False


def mx_kscale(k):
    if not WIDE:
        return np.ones(k)
    levels = np.array([10, -10, 5, -5, 0])
    if k % 512:
        return np.exp2(np.random.permutation(np.resize(levels, k // 32))).repeat(32)
    a = np.empty((k // 512, 16))
    for p in range(k // 512):
        a[p, :8] = np.random.permutation(np.resize(levels, 8))
        for g in range(8):
            far = levels[np.abs(levels - a[p, g]) >= 10]
            a[p, g + 8] = far[np.random.randint(len(far))]
    return np.exp2(a.ravel()).repeat(32)


BF16 = ml_dtypes.bfloat16


def bf(x):
    return np.asarray(x, np.float32).astype(BF16)


def f64(x):
    return np.asarray(x).astype(np.float64)


E2M1 = np.array([0.0, 0.5, 1.0, 1.5, 2.0, 3.0, 4.0, 6.0, -0.0, -0.5, -1.0, -1.5, -2.0, -3.0, -4.0, -6.0])


def pack_weight(w, fmt):
    k, n = w.shape
    w = f64(bf(w)).reshape(k // 32, 32, n)
    amax = np.abs(w).max(1)
    if fmt == "e4m3":
        byte = np.frexp(amax)[1] - 1 + 127 - 7
    else:
        mant, ex = np.frexp(amax / 6.0)
        byte = np.where(mant > 0.5, ex, ex - 1) + 127
    byte = np.clip(np.where(amax > 0, byte, 1), 1, 254)
    scaled = (w * np.exp2(127.0 - byte)[:, None, :]).reshape(k, n).astype(np.float32)
    by_word = np.ascontiguousarray(scaled.reshape(k // 512, 128, 4, n).transpose(0, 1, 3, 2))
    if fmt == "e4m3":
        words = by_word.astype(ml_dtypes.float8_e4m3fn).view(np.uint8)
    else:
        c = by_word.astype(ml_dtypes.float4_e2m1fn).view(np.uint8) & 0xF
        words = c[..., 0::2] | (c[..., 1::2] << 4)
    return np.ascontiguousarray(words), np.ascontiguousarray(byte.astype(np.uint8).reshape(k // 512, 16, n))


def unpack_weight(words, scales, fmt):
    g, p, n, _ = words.shape
    if fmt == "e4m3":
        vals = np.ascontiguousarray(words).view(ml_dtypes.float8_e4m3fn).astype(np.float64)
    else:
        nib = np.empty((g, p, n, 4), np.uint8)
        nib[..., 0::2] = words & 0xF
        nib[..., 1::2] = words >> 4
        vals = E2M1[nib]
    vals = vals * np.repeat(np.exp2(scales.astype(np.float64) - 127.0), 8, axis=1)[..., None]
    return vals.transpose(0, 1, 3, 2).reshape(g * 512, n)
def pack4(w):
    words, scales = pack_weight(w, "e2m1")
    return words.reshape(words.shape[0], 128, -1), scales


def unpack4(words, scales):
    return unpack_weight(words.reshape(words.shape[0], 128, -1, 2), scales, "e2m1")


B, N, D, H, DH = 2, 512, 1024, 16, 64
INNER = H * DH
S = 2 * DH


def dpfp(u):
    u2 = np.concatenate([np.maximum(u, 0.0), np.maximum(-u, 0.0)], axis=-1)
    return u2 * np.roll(u2, 1, axis=-1)


def draw0():
    s, t = mx_kscale(D), mx_kscale(N)
    f = dpfp(np.random.standard_normal((B, H, N, DH)))
    x = bf(np.random.standard_normal((B, N, D)) * s)
    words, scales = pack4(np.random.standard_normal((D, INNER)) / np.sqrt(D) / s[:, None])
    return {"x": x,
            "wv_words": words,
            "wv_scales": scales,
            "beta": bf(np.random.standard_normal((B, H, N)) * t),
            "vo": bf(np.random.standard_normal((B, H, N, DH)) * 0.3),
            "k_phi": bf(f / f.sum(-1, keepdims=True) / t[:, None]),
            "W": bf(np.random.standard_normal((B, H, S, DH)))}


def core(x, wv_words, wv_scales, beta, vo, k_phi, W):
    v = mxq(f64(x), 2, "e4m3") @ unpack4(wv_words, wv_scales)
    v = v.reshape(B, N, H, DH).transpose(0, 2, 1, 3)
    dv = f64(beta)[..., None] * (v - f64(vo))
    return f64(W) + (mxq(f64(k_phi).transpose(0, 1, 3, 2), 3, "e4m3") @ mxq(dv, 2, "e4m3"))


def e4m3fn_bytes(y):
    return np.clip(np.asarray(y, np.float64), -448.0, 448.0).astype(np.float32).astype(ml_dtypes.float8_e4m3fn).view(np.uint8)


def e4m3fn_values(b):
    return np.asarray(b, np.uint8).view(ml_dtypes.float8_e4m3fn).astype(np.float64)


def setup_inputs():
    d = draw0()
    x0 = np.asarray(d['k_phi']).astype(np.float64)
    s = (np.max(np.abs(x0), axis=(0, 1, 3), keepdims=True) / 448.0).astype(np.float32)
    out = {}
    for k, v in d.items():
        if k == 'k_phi':
            out['k_phi_bytes'] = e4m3fn_bytes(x0 / s.astype(np.float64))
            out['k_phi_scale'] = s
        else:
            out[k] = v
    return out


def reference(x, wv_words, wv_scales, beta, vo, k_phi_bytes, k_phi_scale, W):
    return core(x, wv_words, wv_scales, beta, vo, e4m3fn_values(k_phi_bytes) * k_phi_scale.astype(np.float64), W)

@@ -1,0 +1,406 @@
+from contextlib import ExitStack
+
+import concourse.mybir as mybir
+from concourse.masks import make_identity
+
+F32 = mybir.dt.float32
+BF16 = mybir.dt.bfloat16
+I32 = mybir.dt.int32
+U32 = mybir.dt.uint32
+U8 = mybir.dt.uint8
+FP8 = mybir.dt.float8_e4m3fn
+E4M3X4 = mybir.dt.float8_e4m3fn_x4
+E2M1X4 = mybir.dt.float4_e2m1fn_x4
+ALU = mybir.AluOpType
+ACT = mybir.ActivationFunctionType
+
+B, N, D, H, DH = 2, 512, 1024, 16, 64
+S = 2 * DH
+P = 128
+PACK = 4
+RUN = 4
+FLOPS = 2 * B * N * D * H * DH + 2 * B * H * N * S * DH
+
+WIDEN_ON_VECTOR = ((0, 0), (0, 2), (0, 4), (0, 8), (0, 10))
+INTERLEAVE_ON_VECTOR = ((0, 0), (0, 2), (0, 4), (0, 8), (0, 10))
+
+
+def tile_dpfpattention_pb_w4_kernel(tc, x, wv_words, wv_scales, beta, vo, k_phi_bytes, k_phi_scale, W, out):
+    nc = tc.nc
+    with ExitStack() as ctx:
+        keep = ctx.enter_context(tc.tile_pool(name="keep", bufs=1))
+        work = ctx.enter_context(tc.tile_pool(name="work", bufs=4))
+        psum = ctx.enter_context(tc.psum_pool(name="psum", bufs=2))
+
+        ident = keep.tile([P, P], F32, name="ident")
+        make_identity(nc, ident[:])
+        warm = keep.tile([P, 1], F32, name="warm")
+        nc.vector.memset(warm[:], 0.0)
+        nc.scalar.activation(out=warm[:], in_=warm[:], func=ACT.Copy)
+        wsc = keep.tile([P, 2, D], U8, align_bytes=64, name="wsc")
+        nc.vector.memset(wsc[:].rearrange("p g n -> p (g n)").bitcast(I32), 0)
+        beta_rows = keep.tile([P, N], BF16, align_bytes=64, name="beta_rows")
+        nc.vector.memset(beta_rows[:], 0.0)
+        nc.gpsimd.dma_start(out=beta_rows[0 : B * H, :], in_=beta.rearrange("b h n -> (b h) n"))
+        kscale = keep.tile([P, PACK], F32, name="kscale")
+        nc.sync.dma_start(out=kscale[:], in_=k_phi_scale.rearrange("a c (p t) f -> p (a c t f)", t=PACK))
+        kb, xs, vos, ws = {}, {}, {}, {}
+
+        def load_kphi(b, h0, nh):
+            kbt = keep.tile([P, nh, PACK * S], U8, align_bytes=64, name=f"kb_{b}_{h0}")
+            nc.sync.dma_start(out=kbt[:], in_=k_phi_bytes[b, h0 : h0 + nh].rearrange("h (p t) s -> p h (t s)", t=PACK))
+            for h in range(nh):
+                kb[b, h0 + h] = kbt[:, h, :]
+
+        def load_x(b, t0, nt):
+            xt = keep.tile([P, nt, D], BF16, align_bytes=64, name=f"x_{b}_{t0}")
+            nc.sync.dma_start(out=xt[:], in_=x[b].rearrange("(p t) k -> p t k", t=PACK)[:, t0 : t0 + nt, :])
+            for t in range(nt):
+                xs[b, t0 + t] = xt[:, t, :]
+
+        def load_vo(b, u):
+            v = keep.tile([P, 8, PACK, DH], BF16, align_bytes=64, name=f"vo_{b}_{u}")
+            nc.sync.dma_start(
+                out=v[:].rearrange("p h t d -> p h (t d)"),
+                in_=vo[b, 8 * u : 8 * u + 8].rearrange("h (p t) d -> p h (t d)", t=PACK),
+            )
+            vos[b, u] = v
+
+        def load_W(b):
+            w = keep.tile([P, H, DH], BF16, align_bytes=64, name=f"W_{b}")
+            nc.sync.dma_start(out=w[:], in_=W[b].rearrange("h s d -> s h d"))
+            ws[b] = w
+
+        ww = keep.tile([P, 2, 2 * D], U8, align_bytes=64, name="ww")
+
+        def load_weight_scales():
+            for q in range(4):
+                nc.sync.dma_start(
+                    out=wsc[32 * q : 32 * q + 4, :, :].bitcast(I32),
+                    in_=wv_scales[:, 4 * q : 4 * q + 4, :].rearrange("g q n -> q g n").bitcast(I32),
+                )
+
+        def load_weight():
+            nc.sync.dma_start(out=ww[:], in_=wv_words.rearrange("g p n -> p g n"))
+
+        load_kphi(0,0,2)
+        load_kphi(0,6,2)
+        load_kphi(0,2,2)
+        load_x(0,0,2)
+        load_kphi(0,4,2)
+        load_kphi(0,12,2)
+        load_x(0,2,2)
+        load_weight_scales()
+        load_kphi(0,8,2)
+        load_kphi(0,14,2)
+        load_weight()
+        load_kphi(0,10,2)
+        load_vo(0,0)
+        load_kphi(1,0,4)
+        load_vo(0,1)
+        load_x(1,0,4)
+        load_kphi(1,4,4)
+        load_W(0)
+        load_vo(1,0)
+        load_kphi(1,8,4)
+        load_kphi(1,12,4)
+        load_vo(1,1)
+        load_W(1)
+
+        beta_t = keep.tile([P, B * H, PACK, RUN], BF16, align_bytes=64, name="beta_t")
+
+        betas = []
+
+        def turn_beta():
+            bt = psum.tile([P, 2, P], F32, name="turn", bufs=2)
+            words = beta_rows[:].bitcast(F32)
+            for u in range(2):
+                nc.tensor.transpose(bt[:, u, :], words[:, u : 2 * P : 2], ident[:])
+            betas.append(bt)
+
+        def copy_beta():
+            for u in range(2):
+                pair = betas[0][:, u, 0 : B * H].bitcast(BF16).rearrange("p (r e) -> p r e", e=2)
+                nc.scalar.copy(
+                    out=beta_t[:, :, 2 * u : 2 * u + 2, :],
+                    in_=pair.unsqueeze(3).to_broadcast([P, B * H, 2, RUN]),
+                )
+
+        xp, xg, xc = {}, {}, {}
+
+        def turn_x(b, t):
+            ps = psum.tile([P, 2, 2, P], F32, name="turn", bufs=2)
+            words = xs[b, t].bitcast(F32)
+            for g in range(2):
+                for u in range(2):
+                    nc.tensor.transpose(ps[:, g, u, :], words[:, 256 * g + u : 256 * (g + 1) : 2], ident[:])
+            xp[b, t] = ps
+
+        def copy_x(b, t):
+            ps = xp[b, t]
+            gt = work.tile([P, 2 * P * PACK], BF16, align_bytes=64, name="xg", bufs=8)
+            nc.scalar.copy(
+                out=gt[:].bitcast(F32).rearrange("p (g r u) -> p g r u", g=2, u=2),
+                in_=ps[:].rearrange("p g u r -> p g r u"),
+            )
+            xg[b, t] = gt
+
+        def quant_x(b, t):
+            codes = keep.tile([P, 2, P], U32, align_bytes=64, name=f"xc_{b}_{t}")
+            scales = keep.tile([P, 2, P], U8, align_bytes=64, name=f"xsc_{b}_{t}")
+            nc.vector.quantize_mx(
+                out=codes[:].rearrange("p g r -> p (g r)").bitcast(E4M3X4),
+                scales=scales[:].rearrange("p g r -> p (g r)"),
+                in_=xg[b, t][:],
+            )
+            xc[b, t] = (codes, scales)
+
+        planes, inter, kc = {}, {}, {}
+
+        def widen(b, h):
+            pl = work.tile([P, 2, PACK, S], BF16, align_bytes=64, name="planes", bufs=16)
+            for i in range(2):
+                for t in range(PACK):
+                    src = kb[b, h + i][:, S * t : S * (t + 1)].bitcast(FP8)
+                    if (b, h) in WIDEN_ON_VECTOR:
+                        nc.vector.tensor_scalar(out=pl[:, i, t, :], in0=src, scalar1=kscale[:, t : t + 1], scalar2=None, op0=ALU.mult)
+                    else:
+                        nc.scalar.activation(out=pl[:, i, t, :], in_=src, func=ACT.Copy, scale=kscale[:, t : t + 1])
+            planes[b, h] = pl
+
+        def interleave(b, h):
+            pl = planes[b, h]
+            it = work.tile([P, 2, S, PACK], BF16, align_bytes=64, name="inter", bufs=16)
+            copy = nc.vector.tensor_copy if (b, h) in INTERLEAVE_ON_VECTOR else nc.scalar.copy
+            for i in range(2):
+                copy(
+                    out=it[:, i, :, :].rearrange("p (c i) t -> p c t i", i=RUN),
+                    in_=pl[:, i, :, :].rearrange("p t (c i) -> p c t i", i=RUN),
+                )
+            inter[b, h] = it
+
+        def quant_k(b, h):
+            codes = keep.tile([P, 2, S], U32, align_bytes=64, name=f"kc_{b}_{h}")
+            scales = keep.tile([P, 2, S], U8, align_bytes=64, name=f"ksc_{b}_{h}")
+            nc.vector.quantize_mx(
+                out=codes[:].rearrange("p h s -> p (h s)").bitcast(E4M3X4),
+                scales=scales[:].rearrange("p h s -> p (h s)"),
+                in_=inter[b, h][:].rearrange("p h s t -> p (h s t)"),
+            )
+            for i in range(2):
+                kc[b, h + i] = (codes[:, i, :], scales[:, i, :])
+
+        vps, t1s, dvg, dvc = {}, {}, {}, {}
+
+        def values(b, u, t):
+            ps = psum.tile([P, 512], F32, name="v", bufs=4)
+            codes, scales = xc[b, t]
+            for g in range(2):
+                nc.tensor.matmul_mx(
+                    out=ps[:],
+                    lhsT=codes[:, g, :].bitcast(E4M3X4),
+                    lhsT_scale=scales[:, g, :],
+                    rhs=ww[:, g, 1024 * u : 1024 * (u + 1)].bitcast(E2M1X4),
+                    rhs_scale=wsc[:, g, 512 * u : 512 * (u + 1)],
+                    start=(g == 0),
+                    stop=(g == 1),
+                )
+            vps[b, u, t] = ps
+
+        def subtract(b, u, t):
+            if (b, u) not in t1s:
+                t1 = work.tile([P, 8, DH // RUN, PACK, RUN], F32, align_bytes=64, name="t1", bufs=3)
+                t1s[b, u] = t1
+            nc.vector.tensor_tensor(
+                out=t1s[b, u][:, :, :, t, :],
+                in0=vps[b, u, t][:].rearrange("p (h c i) -> p h c i", h=8, i=RUN),
+                in1=vos[b, u][:, :, t, :].rearrange("p h (c i) -> p h c i", i=RUN),
+                op=ALU.subtract,
+            )
+
+        def scale_dv(b, u, j):
+            name = "dvg_last" if (b, u, j) == (1, 1, 1) else "dvg"
+            dg = work.tile([P, 4, DH, PACK], BF16, align_bytes=64, name="dvg", tag=name, bufs=1)
+            engine = nc.gpsimd if j == 1 and (b, u) != (1, 1) else nc.vector
+            r0 = 16 * b + 8 * u + 4 * j
+            engine.tensor_tensor(
+                out=dg[:].rearrange("p h (c i) t -> p h c t i", i=RUN),
+                in0=t1s[b, u][:, 4 * j : 4 * j + 4, :, :, :],
+                in1=beta_t[:, r0 : r0 + 4, :, :].unsqueeze(2).to_broadcast([P, 4, DH // RUN, PACK, RUN]),
+                op=ALU.mult,
+            )
+            dvg[b, u, j] = dg
+
+        def quant_dv(b, u, j):
+            codes = work.tile([P, 4, DH], U32, align_bytes=64, name="dvc", bufs=4)
+            scales = work.tile([P, 4, DH], U8, align_bytes=64, name="dvsc", bufs=4)
+            nc.vector.quantize_mx(
+                out=codes[:].rearrange("p h d -> p (h d)").bitcast(E4M3X4),
+                scales=scales[:].rearrange("p h d -> p (h d)"),
+                in_=dvg[b, u, j][:].rearrange("p h d t -> p (h d t)"),
+            )
+            dvc[b, u, j] = (codes, scales)
+
+        ops = {}
+
+        def update(b, u, j):
+            ps = psum.tile([P, 4, DH], F32, name="o", bufs=2)
+            dcodes, dscales = dvc[b, u, j]
+            for i in range(4):
+                kcodes, kscales = kc[b, 8 * u + 4 * j + i // 2 * 2 + i % 2]
+                nc.tensor.matmul_mx(
+                    out=ps[:, i, :],
+                    lhsT=kcodes.bitcast(E4M3X4),
+                    lhsT_scale=kscales,
+                    rhs=dcodes[:, i, :].bitcast(E4M3X4),
+                    rhs_scale=dscales[:, i, :],
+                    start=True,
+                    stop=True,
+                )
+            ops[b, u, j] = ps
+
+        def finish(b, u, j):
+            h0 = 8 * u + 4 * j
+            ot = work.tile([P, 4, DH], F32, align_bytes=64, name="ot", bufs=4)
+            nc.vector.tensor_tensor(out=ot[:], in0=ops[b, u, j][:], in1=ws[b][:, h0 : h0 + 4, :], op=ALU.add)
+            nc.sync.dma_start(out=out[b, h0 : h0 + 4].rearrange("h s d -> s h d"), in_=ot[:])
+
+        with tc.manual_schedule():
+            widen(0, 0)
+            widen(0, 6)
+            widen(0, 2)
+            interleave(0, 0)
+            widen(0, 4)
+            interleave(0, 2)
+            quant_k(0, 0)
+            turn_x(0, 0)
+            copy_x(0, 0)
+            turn_x(0, 1)
+            interleave(0, 6)
+            copy_x(0, 1)
+            widen(0, 12)
+            interleave(0, 4)
+            quant_k(0, 2)
+            quant_x(0, 0)
+            quant_x(0, 1)
+            turn_x(0, 2)
+            copy_x(0, 2)
+            turn_x(0, 3)
+            copy_x(0, 3)
+            quant_k(0, 4)
+            widen(0, 8)
+            quant_x(0, 2)
+            quant_x(0, 3)
+            turn_beta()
+            copy_beta()
+            widen(0, 14)
+            interleave(0, 12)
+            values(0, 0, 0)
+            values(0, 0, 1)
+            values(0, 0, 2)
+            values(0, 0, 3)
+            widen(0, 10)
+            interleave(0, 8)
+            quant_k(0, 6)
+            interleave(0, 10)
+            quant_k(0, 8)
+            subtract(0, 0, 0)
+            subtract(0, 0, 1)
+            subtract(0, 0, 2)
+            subtract(0, 0, 3)
+            values(0, 1, 0)
+            values(0, 1, 1)
+            values(0, 1, 2)
+            values(0, 1, 3)
+            quant_k(0, 10)
+            scale_dv(0, 0, 0)
+            quant_k(0, 12)
+            quant_dv(0, 0, 0)
+            widen(1, 0)
+            interleave(0, 14)
+            widen(1, 2)
+            interleave(1, 0)
+            turn_x(1, 0)
+            copy_x(1, 0)
+            turn_x(1, 1)
+            copy_x(1, 1)
+            update(0, 0, 0)
+            scale_dv(0, 0, 1)
+            subtract(0, 1, 0)
+            subtract(0, 1, 1)
+            subtract(0, 1, 2)
+            subtract(0, 1, 3)
+            quant_dv(0, 0, 1)
+            quant_k(0, 14)
+            turn_x(1, 2)
+            copy_x(1, 2)
+            turn_x(1, 3)
+            copy_x(1, 3)
+            interleave(1, 2)
+            update(0, 0, 1)
+            scale_dv(0, 1, 0)
+            quant_x(1, 0)
+            quant_x(1, 1)
+            quant_x(1, 2)
+            quant_x(1, 3)
+            values(1, 0, 0)
+            values(1, 0, 1)
+            values(1, 0, 2)
+            values(1, 0, 3)
+            finish(0, 0, 0)
+            quant_dv(0, 1, 0)
+            update(0, 1, 0)
+            widen(1, 4)
+            widen(1, 6)
+            interleave(1, 4)
+            scale_dv(0, 1, 1)
+            subtract(1, 0, 0)
+            subtract(1, 0, 1)
+            subtract(1, 0, 2)
+            subtract(1, 0, 3)
+            values(1, 1, 0)
+            values(1, 1, 1)
+            values(1, 1, 2)
+            values(1, 1, 3)
+            finish(0, 0, 1)
+            finish(0, 1, 0)
+            widen(1, 8)
+            interleave(1, 6)
+            quant_dv(0, 1, 1)
+            quant_k(1, 0)
+            update(0, 1, 1)
+            quant_k(1, 2)
+            scale_dv(1, 0, 0)
+            quant_k(1, 4)
+            quant_dv(1, 0, 0)
+            update(1, 0, 0)
+            widen(1, 10)
+            interleave(1, 8)
+            widen(1, 12)
+            interleave(1, 10)
+            widen(1, 14)
+            interleave(1, 12)
+            interleave(1, 14)
+            scale_dv(1, 0, 1)
+            subtract(1, 1, 0)
+            subtract(1, 1, 1)
+            subtract(1, 1, 2)
+            subtract(1, 1, 3)
+            finish(0, 1, 1)
+            finish(1, 0, 0)
+            quant_dv(1, 0, 1)
+            quant_k(1, 6)
+            update(1, 0, 1)
+            scale_dv(1, 1, 0)
+            quant_k(1, 8)
+            scale_dv(1, 1, 1)
+            quant_dv(1, 1, 0)
+            finish(1, 0, 1)
+            quant_k(1, 10)
+            update(1, 1, 0)
+            quant_dv(1, 1, 1)
+            quant_k(1, 12)
+            finish(1, 1, 0)
+            quant_k(1, 14)
+            update(1, 1, 1)
+            finish(1, 1, 1)

@@ -19,10 +19,14 @@ S = 2 * DH
 P = 128
 PACK = 4
 RUN = 4
+PAIRS = B * H // 2
+QUADS = PAIRS // 2
 FLOPS = 2 * B * N * D * H * DH + 2 * B * H * N * S * DH
 
-WIDEN_ON_VECTOR = ((0, 0), (0, 2), (0, 4), (0, 8), (0, 10))
-INTERLEAVE_ON_VECTOR = ((0, 0), (0, 2), (0, 4), (0, 8), (0, 10))
+WIDEN_ON_VECTOR = (0, 2, 4)
+INTERLEAVE_ON_SCALAR = (15,)
+WIDEN_IN = ((6,), (7,), (8, 9), (10, 11), (12, 13), (14,), (15,))
+ON_SIDE = (15,)
 
 
 def tile_dpfpattention_pb_w4_kernel(tc, x, wv_words, wv_scales, beta, vo, k_phi_bytes, k_phi_scale, W, out):
@@ -31,47 +35,46 @@ def tile_dpfpattention_pb_w4_kernel(tc, x, wv_words, wv_scales, beta, vo, k_phi_
         keep = ctx.enter_context(tc.tile_pool(name="keep", bufs=1))
         work = ctx.enter_context(tc.tile_pool(name="work", bufs=4))
         psum = ctx.enter_context(tc.psum_pool(name="psum", bufs=2))
+        ctx.enter_context(tc.manual_schedule())
 
         ident = keep.tile([P, P], F32, name="ident")
         make_identity(nc, ident[:])
-        warm = keep.tile([P, 1], F32, name="warm")
-        nc.vector.memset(warm[:], 0.0)
-        nc.scalar.activation(out=warm[:], in_=warm[:], func=ACT.Copy)
+        minus_ident = keep.tile([P, P], BF16, name="minus_ident")
+        nc.scalar.activation(out=minus_ident[:], in_=ident[:], func=ACT.Copy, scale=-1.0)
         wsc = keep.tile([P, 2, D], U8, align_bytes=64, name="wsc")
-        nc.vector.memset(wsc[:].rearrange("p g n -> p (g n)").bitcast(I32), 0)
+        nc.gpsimd.memset(wsc[:].rearrange("p g n -> p (g n)").bitcast(I32), 0)
         beta_rows = keep.tile([P, N], BF16, align_bytes=64, name="beta_rows")
-        nc.vector.memset(beta_rows[:], 0.0)
+        nc.gpsimd.memset(beta_rows[:].bitcast(I32), 0)
         nc.gpsimd.dma_start(out=beta_rows[0 : B * H, :], in_=beta.rearrange("b h n -> (b h) n"))
         kscale = keep.tile([P, PACK], F32, name="kscale")
-        nc.sync.dma_start(out=kscale[:], in_=k_phi_scale.rearrange("a c (p t) f -> p (a c t f)", t=PACK))
+        ww = keep.tile([P, 2, 2 * D], U8, align_bytes=64, name="ww")
         kb, xs, vos, ws = {}, {}, {}, {}
 
-        def load_kphi(b, h0, nh):
-            kbt = keep.tile([P, nh, PACK * S], U8, align_bytes=64, name=f"kb_{b}_{h0}")
-            nc.sync.dma_start(out=kbt[:], in_=k_phi_bytes[b, h0 : h0 + nh].rearrange("h (p t) s -> p h (t s)", t=PACK))
-            for h in range(nh):
-                kb[b, h0 + h] = kbt[:, h, :]
+        def load_kphi(q0, nq):
+            b, h0 = divmod(2 * q0, H)
+            kbt = keep.tile([P, 2 * nq, PACK * S], U8, align_bytes=64, name=f"kb_{q0}")
+            nc.sync.dma_start(out=kbt[:], in_=k_phi_bytes[b, h0 : h0 + 2 * nq].rearrange("h (p t) s -> p h (t s)", t=PACK))
+            for q in range(nq):
+                kb[q0 + q] = kbt[:, 2 * q : 2 * q + 2, :]
 
-        def load_x(b, t0, nt):
-            xt = keep.tile([P, nt, D], BF16, align_bytes=64, name=f"x_{b}_{t0}")
-            nc.sync.dma_start(out=xt[:], in_=x[b].rearrange("(p t) k -> p t k", t=PACK)[:, t0 : t0 + nt, :])
-            for t in range(nt):
-                xs[b, t0 + t] = xt[:, t, :]
+        def load_x(b, tp):
+            xt = keep.tile([P, 2, D], BF16, align_bytes=64, name=f"x_{b}_{tp}")
+            nc.sync.dma_start(out=xt[:], in_=x[b].rearrange("(p t) k -> p t k", t=PACK)[:, 2 * tp : 2 * tp + 2, :])
+            xs[b, tp] = xt
 
-        def load_vo(b, u):
-            v = keep.tile([P, 8, PACK, DH], BF16, align_bytes=64, name=f"vo_{b}_{u}")
+        def load_vo(r):
+            b, h0 = divmod(4 * r, H)
+            v = keep.tile([P, 4, PACK, DH], BF16, align_bytes=64, name=f"vo_{r}")
             nc.sync.dma_start(
                 out=v[:].rearrange("p h t d -> p h (t d)"),
-                in_=vo[b, 8 * u : 8 * u + 8].rearrange("h (p t) d -> p h (t d)", t=PACK),
+                in_=vo[b, h0 : h0 + 4].rearrange("h (p t) d -> p h (t d)", t=PACK),
             )
-            vos[b, u] = v
+            vos[r] = v
 
         def load_W(b):
             w = keep.tile([P, H, DH], BF16, align_bytes=64, name=f"W_{b}")
             nc.sync.dma_start(out=w[:], in_=W[b].rearrange("h s d -> s h d"))
             ws[b] = w
-
-        ww = keep.tile([P, 2, 2 * D], U8, align_bytes=64, name="ww")
 
         def load_weight_scales():
             for q in range(4):
@@ -80,327 +83,338 @@ def tile_dpfpattention_pb_w4_kernel(tc, x, wv_words, wv_scales, beta, vo, k_phi_
                     in_=wv_scales[:, 4 * q : 4 * q + 4, :].rearrange("g q n -> q g n").bitcast(I32),
                 )
 
-        def load_weight():
-            nc.sync.dma_start(out=ww[:], in_=wv_words.rearrange("g p n -> p g n"))
-
-        load_kphi(0,0,2)
-        load_kphi(0,6,2)
-        load_kphi(0,2,2)
-        load_x(0,0,2)
-        load_kphi(0,4,2)
-        load_kphi(0,12,2)
-        load_x(0,2,2)
+        nc.sync.dma_start(out=kscale[:], in_=k_phi_scale.rearrange("a c (p t) f -> p (a c t f)", t=PACK))
+        load_kphi(0, 1)
+        load_kphi(1, 1)
+        load_x(0, 0)
+        load_kphi(2, 1)
+        load_x(0, 1)
+        load_kphi(3, 1)
         load_weight_scales()
-        load_kphi(0,8,2)
-        load_kphi(0,14,2)
-        load_weight()
-        load_kphi(0,10,2)
-        load_vo(0,0)
-        load_kphi(1,0,4)
-        load_vo(0,1)
-        load_x(1,0,4)
-        load_kphi(1,4,4)
+        nc.sync.dma_start(out=ww[:], in_=wv_words.rearrange("g p n -> p g n"))
+        load_kphi(4, 2)
+        load_vo(0)
+        load_vo(1)
+        load_x(1, 0)
+        load_kphi(6, 2)
+        load_x(1, 1)
+        load_vo(2)
         load_W(0)
-        load_vo(1,0)
-        load_kphi(1,8,4)
-        load_kphi(1,12,4)
-        load_vo(1,1)
+        load_kphi(8, 2)
+        load_vo(3)
+        load_kphi(10, 2)
+        load_vo(4)
+        load_kphi(12, 2)
         load_W(1)
+        load_vo(5)
+        load_kphi(14, 2)
+        load_vo(6)
+        load_vo(7)
 
-        beta_t = keep.tile([P, B * H, PACK, RUN], BF16, align_bytes=64, name="beta_t")
-
-        betas = []
+        beta2 = keep.tile([P, B * H, PACK, 2], BF16, align_bytes=64, name="beta2")
+        beta4 = keep.tile([P, 4, PACK, RUN], BF16, align_bytes=64, name="beta4")
+        turned = {}
 
         def turn_beta():
-            bt = psum.tile([P, 2, P], F32, name="turn", bufs=2)
+            bt = psum.tile([P, 2, P], F32, name="turn", bufs=3)
             words = beta_rows[:].bitcast(F32)
             for u in range(2):
                 nc.tensor.transpose(bt[:, u, :], words[:, u : 2 * P : 2], ident[:])
-            betas.append(bt)
+            turned["beta"] = bt
 
         def copy_beta():
-            for u in range(2):
-                pair = betas[0][:, u, 0 : B * H].bitcast(BF16).rearrange("p (r e) -> p r e", e=2)
-                nc.scalar.copy(
-                    out=beta_t[:, :, 2 * u : 2 * u + 2, :],
-                    in_=pair.unsqueeze(3).to_broadcast([P, B * H, 2, RUN]),
-                )
+            by_slot = turned["beta"][:, :, 0 : B * H].bitcast(BF16).rearrange("p u (r e) -> p r u e", e=2)
+            nc.scalar.copy(
+                out=beta4[:].rearrange("p r (u e) i -> p r u e i", e=2),
+                in_=by_slot[:, 0:4].unsqueeze(4).to_broadcast([P, 4, 2, 2, RUN]),
+            )
+            nc.scalar.copy(
+                out=beta2[:].rearrange("p r (u e) i -> p r u e i", e=2),
+                in_=by_slot.unsqueeze(4).to_broadcast([P, B * H, 2, 2, 2]),
+            )
 
-        xp, xg, xc = {}, {}, {}
-
-        def turn_x(b, t):
-            ps = psum.tile([P, 2, 2, P], F32, name="turn", bufs=2)
-            words = xs[b, t].bitcast(F32)
+        xg, xcodes, xscales = {}, {}, {}
+        for b in range(B):
             for g in range(2):
-                for u in range(2):
-                    nc.tensor.transpose(ps[:, g, u, :], words[:, 256 * g + u : 256 * (g + 1) : 2], ident[:])
-            xp[b, t] = ps
+                xcodes[b, g] = keep.tile([P, N], U32, align_bytes=64, name=f"xc_{b}_{g}")
+                xscales[b, g] = keep.tile([P, N], U8, align_bytes=64, name=f"xsc_{b}_{g}")
 
-        def copy_x(b, t):
-            ps = xp[b, t]
+        def turn_x(b, tp, g):
+            ps = psum.tile([P, 2, 2, P], F32, name="turn", bufs=3)
+            for t in range(2):
+                words = xs[b, tp][:, t, :].bitcast(F32)
+                for u in range(2):
+                    nc.tensor.transpose(ps[:, t, u, :], words[:, 256 * g + u : 256 * (g + 1) : 2], ident[:])
+            turned[b, tp, g] = ps
+
+        def copy_x(b, tp, g):
             gt = work.tile([P, 2 * P * PACK], BF16, align_bytes=64, name="xg", bufs=8)
             nc.scalar.copy(
-                out=gt[:].bitcast(F32).rearrange("p (g r u) -> p g r u", g=2, u=2),
-                in_=ps[:].rearrange("p g u r -> p g r u"),
+                out=gt[:].bitcast(F32).rearrange("p (t r u) -> p t r u", t=2, u=2),
+                in_=turned[b, tp, g][:].rearrange("p t u r -> p t r u"),
             )
-            xg[b, t] = gt
+            xg[b, tp, g] = gt
 
-        def quant_x(b, t):
-            codes = keep.tile([P, 2, P], U32, align_bytes=64, name=f"xc_{b}_{t}")
-            scales = keep.tile([P, 2, P], U8, align_bytes=64, name=f"xsc_{b}_{t}")
-            nc.vector.quantize_mx(
-                out=codes[:].rearrange("p g r -> p (g r)").bitcast(E4M3X4),
-                scales=scales[:].rearrange("p g r -> p (g r)"),
-                in_=xg[b, t][:],
-            )
-            xc[b, t] = (codes, scales)
+        def quant_x(b, tp, g):
+            cols = slice(2 * P * tp, 2 * P * (tp + 1))
+            nc.vector.quantize_mx(out=xcodes[b, g][:, cols].bitcast(E4M3X4), scales=xscales[b, g][:, cols], in_=xg[b, tp, g][:])
 
         planes, inter, kc = {}, {}, {}
 
-        def widen(b, h):
-            pl = work.tile([P, 2, PACK, S], BF16, align_bytes=64, name="planes", bufs=16)
-            for i in range(2):
+        def widen(q, heads=(0, 1)):
+            if q not in planes:
+                planes[q] = work.tile([P, PACK, 2, S], BF16, align_bytes=64, name="planes", bufs=16)
+            pl = planes[q]
+            for i in heads:
                 for t in range(PACK):
-                    src = kb[b, h + i][:, S * t : S * (t + 1)].bitcast(FP8)
-                    if (b, h) in WIDEN_ON_VECTOR:
-                        nc.vector.tensor_scalar(out=pl[:, i, t, :], in0=src, scalar1=kscale[:, t : t + 1], scalar2=None, op0=ALU.mult)
+                    src = kb[q][:, i, S * t : S * (t + 1)].bitcast(FP8)
+                    if q in WIDEN_ON_VECTOR:
+                        nc.vector.tensor_scalar(out=pl[:, t, i, :], in0=src, scalar1=kscale[:, t : t + 1], scalar2=None, op0=ALU.mult)
                     else:
-                        nc.scalar.activation(out=pl[:, i, t, :], in_=src, func=ACT.Copy, scale=kscale[:, t : t + 1])
-            planes[b, h] = pl
+                        nc.scalar.activation(out=pl[:, t, i, :], in_=src, func=ACT.Copy, scale=kscale[:, t : t + 1])
 
-        def interleave(b, h):
-            pl = planes[b, h]
-            it = work.tile([P, 2, S, PACK], BF16, align_bytes=64, name="inter", bufs=16)
-            copy = nc.vector.tensor_copy if (b, h) in INTERLEAVE_ON_VECTOR else nc.scalar.copy
-            for i in range(2):
-                copy(
-                    out=it[:, i, :, :].rearrange("p (c i) t -> p c t i", i=RUN),
-                    in_=pl[:, i, :, :].rearrange("p t (c i) -> p c t i", i=RUN),
+        def interleave(q):
+            it = work.tile([P, 2 * S, PACK], BF16, align_bytes=64, name="inter", bufs=8)
+            dst = it[:].rearrange("p (c i) t -> p c t i", i=RUN)
+            src = planes[q][:].rearrange("p t h (c i) -> p (h c) t i", i=RUN)
+            if q in INTERLEAVE_ON_SCALAR:
+                nc.scalar.copy(out=dst, in_=src)
+            else:
+                nc.vector.tensor_copy(out=dst, in_=src)
+            inter[q] = it
+
+        def quant_k(q):
+            codes = keep.tile([P, 2 * S], U32, align_bytes=64, name=f"kc_{q}")
+            scales = keep.tile([P, 2 * S], U8, align_bytes=64, name=f"ksc_{q}")
+            nc.vector.quantize_mx(out=codes[:].bitcast(E4M3X4), scales=scales[:], in_=inter[q][:].rearrange("p c t -> p (c t)"))
+            kc[q] = (codes, scales)
+
+        vps, vts, diffs, dvg, dvc, ops = {}, {}, {}, {}, {}, {}
+
+        def first_values(tp):
+            ps = psum.tile([P, 2, 4 * DH], F32, name="diff", bufs=3)
+            for t in range(2):
+                cols = slice(P * (2 * tp + t), P * (2 * tp + t + 1))
+                for g in range(2):
+                    nc.tensor.matmul_mx(
+                        out=ps[:, t, :],
+                        lhsT=xcodes[0, g][:, cols].bitcast(E4M3X4),
+                        lhsT_scale=xscales[0, g][:, cols],
+                        rhs=ww[:, g, 0 : 8 * DH].bitcast(E2M1X4),
+                        rhs_scale=wsc[:, g, 0 : 4 * DH],
+                        start=(g == 0),
+                        stop=(g == 1),
+                    )
+            vps["first", tp] = ps
+
+        first_diff = keep.tile([P, 4, DH // RUN, PACK, RUN], F32, align_bytes=64, name="first_diff")
+
+        def first_subtract(tp):
+            for t in range(2):
+                nc.vector.tensor_tensor(
+                    out=first_diff[:, :, :, 2 * tp + t, :],
+                    in0=vps["first", tp][:, t, :].rearrange("p (h c i) -> p h c i", h=4, i=RUN),
+                    in1=vos[0][:, :, 2 * tp + t, :].rearrange("p h (c i) -> p h c i", i=RUN),
+                    op=ALU.subtract,
                 )
-            inter[b, h] = it
 
-        def quant_k(b, h):
-            codes = keep.tile([P, 2, S], U32, align_bytes=64, name=f"kc_{b}_{h}")
-            scales = keep.tile([P, 2, S], U8, align_bytes=64, name=f"ksc_{b}_{h}")
-            nc.vector.quantize_mx(
-                out=codes[:].rearrange("p h s -> p (h s)").bitcast(E4M3X4),
-                scales=scales[:].rearrange("p h s -> p (h s)"),
-                in_=inter[b, h][:].rearrange("p h s t -> p (h s t)"),
+        def first_scale():
+            dg = work.tile([P, 4, DH, PACK], BF16, align_bytes=64, name="dvg", bufs=3)
+            nc.vector.tensor_tensor(
+                out=dg[:].rearrange("p h (c i) t -> p h c t i", i=RUN),
+                in0=first_diff[:],
+                in1=beta4[:].unsqueeze(2).to_broadcast([P, 4, DH // RUN, PACK, RUN]),
+                op=ALU.mult,
             )
-            for i in range(2):
-                kc[b, h + i] = (codes[:, i, :], scales[:, i, :])
+            dvg[0] = dg
 
-        vps, t1s, dvg, dvc = {}, {}, {}, {}
-
-        def values(b, u, t):
-            ps = psum.tile([P, 512], F32, name="v", bufs=4)
-            codes, scales = xc[b, t]
+        def values(q):
+            b, j = divmod(q, H // 2)
+            ps = psum.tile([P, N], F32, name="turn", bufs=3)
             for g in range(2):
                 nc.tensor.matmul_mx(
                     out=ps[:],
-                    lhsT=codes[:, g, :].bitcast(E4M3X4),
-                    lhsT_scale=scales[:, g, :],
-                    rhs=ww[:, g, 1024 * u : 1024 * (u + 1)].bitcast(E2M1X4),
-                    rhs_scale=wsc[:, g, 512 * u : 512 * (u + 1)],
+                    lhsT=ww[:, g, 2 * P * j : 2 * P * (j + 1)].bitcast(E2M1X4),
+                    lhsT_scale=wsc[:, g, P * j : P * (j + 1)],
+                    rhs=xcodes[b, g][:].bitcast(E4M3X4),
+                    rhs_scale=xscales[b, g][:],
                     start=(g == 0),
                     stop=(g == 1),
                 )
-            vps[b, u, t] = ps
+            vps[q] = ps
 
-        def subtract(b, u, t):
-            if (b, u) not in t1s:
-                t1 = work.tile([P, 8, DH // RUN, PACK, RUN], F32, align_bytes=64, name="t1", bufs=3)
-                t1s[b, u] = t1
+        def copy_values(q):
+            vt = work.tile([P, PACK, P], F32, align_bytes=64, name="vt", bufs=4)
+            nc.scalar.copy(out=vt[:].rearrange("p t r -> p (t r)"), in_=vps[q][:])
+            vts[q] = vt
+
+        def lay_vo(q):
+            ps = psum.tile([P, 2, DH // 2, PACK, 2], F32, name="diff", bufs=3)
+            for i in range(2):
+                nc.tensor.matmul(
+                    ps[:, i].rearrange("p c t e -> p t c e"),
+                    lhsT=minus_ident[:],
+                    rhs=vos[q // 2][:, 2 * (q % 2) + i].rearrange("p t (c e) -> p t c e", e=2),
+                    start=(i == 0),
+                    stop=False,
+                )
+            diffs[q] = ps
+
+        def add_values(q):
+            for t in range(PACK):
+                nc.tensor.matmul(
+                    diffs[q][:, :, :, t, :],
+                    lhsT=vts[q][:, t, :],
+                    rhs=ident[:],
+                    start=False,
+                    stop=(t == PACK - 1),
+                    is_transpose=True,
+                )
+
+        def scale_dv(q):
+            if q % 2 == 0:
+                dvg[q // 2] = work.tile([P, 4, DH, PACK], BF16, align_bytes=64, name="dvg", bufs=3)
+            heads = slice(2 * (q % 2), 2 * (q % 2) + 2)
             nc.vector.tensor_tensor(
-                out=t1s[b, u][:, :, :, t, :],
-                in0=vps[b, u, t][:].rearrange("p (h c i) -> p h c i", h=8, i=RUN),
-                in1=vos[b, u][:, :, t, :].rearrange("p h (c i) -> p h c i", i=RUN),
-                op=ALU.subtract,
-            )
-
-        def scale_dv(b, u, j):
-            name = "dvg_last" if (b, u, j) == (1, 1, 1) else "dvg"
-            dg = work.tile([P, 4, DH, PACK], BF16, align_bytes=64, name="dvg", tag=name, bufs=1)
-            engine = nc.gpsimd if j == 1 and (b, u) != (1, 1) else nc.vector
-            r0 = 16 * b + 8 * u + 4 * j
-            engine.tensor_tensor(
-                out=dg[:].rearrange("p h (c i) t -> p h c t i", i=RUN),
-                in0=t1s[b, u][:, 4 * j : 4 * j + 4, :, :, :],
-                in1=beta_t[:, r0 : r0 + 4, :, :].unsqueeze(2).to_broadcast([P, 4, DH // RUN, PACK, RUN]),
+                out=dvg[q // 2][:, heads].rearrange("p h (c e) t -> p h c t e", e=2),
+                in0=diffs[q][:],
+                in1=beta2[:, 2 * q : 2 * q + 2].unsqueeze(2).to_broadcast([P, 2, DH // 2, PACK, 2]),
                 op=ALU.mult,
             )
-            dvg[b, u, j] = dg
 
-        def quant_dv(b, u, j):
-            codes = work.tile([P, 4, DH], U32, align_bytes=64, name="dvc", bufs=4)
-            scales = work.tile([P, 4, DH], U8, align_bytes=64, name="dvsc", bufs=4)
-            nc.vector.quantize_mx(
-                out=codes[:].rearrange("p h d -> p (h d)").bitcast(E4M3X4),
-                scales=scales[:].rearrange("p h d -> p (h d)"),
-                in_=dvg[b, u, j][:].rearrange("p h d t -> p (h d t)"),
-            )
-            dvc[b, u, j] = (codes, scales)
+        def quant_dv(q0, nq):
+            codes = work.tile([P, 2 * nq * DH], U32, align_bytes=64, name="dvc", bufs=4)
+            scales = work.tile([P, 2 * nq * DH], U8, align_bytes=64, name="dvsc", bufs=4)
+            heads = slice(2 * (q0 % 2), 2 * (q0 % 2 + nq))
+            nc.vector.quantize_mx(out=codes[:].bitcast(E4M3X4), scales=scales[:], in_=dvg[q0 // 2][:, heads].rearrange("p h d t -> p (h d t)"))
+            dvc[q0] = (codes, scales)
 
-        ops = {}
-
-        def update(b, u, j):
-            ps = psum.tile([P, 4, DH], F32, name="o", bufs=2)
-            dcodes, dscales = dvc[b, u, j]
-            for i in range(4):
-                kcodes, kscales = kc[b, 8 * u + 4 * j + i // 2 * 2 + i % 2]
+        def update(q0, nq):
+            ps = psum.tile([P, 2 * nq, DH], F32, name="o", bufs=2)
+            dcodes, dscales = dvc[q0]
+            for i in range(2 * nq):
+                kcodes, kscales = kc[q0 + i // 2]
+                cols = slice(S * (i % 2), S * (i % 2 + 1))
                 nc.tensor.matmul_mx(
                     out=ps[:, i, :],
-                    lhsT=kcodes.bitcast(E4M3X4),
-                    lhsT_scale=kscales,
-                    rhs=dcodes[:, i, :].bitcast(E4M3X4),
-                    rhs_scale=dscales[:, i, :],
+                    lhsT=kcodes[:, cols].bitcast(E4M3X4),
+                    lhsT_scale=kscales[:, cols],
+                    rhs=dcodes[:, DH * i : DH * (i + 1)].bitcast(E4M3X4),
+                    rhs_scale=dscales[:, DH * i : DH * (i + 1)],
                     start=True,
                     stop=True,
                 )
-            ops[b, u, j] = ps
+            ops[q0] = ps
 
-        def finish(b, u, j):
-            h0 = 8 * u + 4 * j
-            ot = work.tile([P, 4, DH], F32, align_bytes=64, name="ot", bufs=4)
-            nc.vector.tensor_tensor(out=ot[:], in0=ops[b, u, j][:], in1=ws[b][:, h0 : h0 + 4, :], op=ALU.add)
-            nc.sync.dma_start(out=out[b, h0 : h0 + 4].rearrange("h s d -> s h d"), in_=ot[:])
+        def finish(q0, nq):
+            b, h0 = divmod(2 * q0, H)
+            ot = work.tile([P, 2 * nq, DH], F32, align_bytes=64, name="ot", bufs=4)
+            nc.vector.tensor_tensor(out=ot[:], in0=ops[q0][:], in1=ws[b][:, h0 : h0 + 2 * nq, :], op=ALU.add)
+            nc.sync.dma_start(out=out[b, h0 : h0 + 2 * nq].rearrange("h s d -> s h d"), in_=ot[:])
 
-        with tc.manual_schedule():
-            widen(0, 0)
-            widen(0, 6)
-            widen(0, 2)
-            interleave(0, 0)
-            widen(0, 4)
-            interleave(0, 2)
-            quant_k(0, 0)
-            turn_x(0, 0)
-            copy_x(0, 0)
-            turn_x(0, 1)
-            interleave(0, 6)
-            copy_x(0, 1)
-            widen(0, 12)
-            interleave(0, 4)
-            quant_k(0, 2)
-            quant_x(0, 0)
-            quant_x(0, 1)
-            turn_x(0, 2)
-            copy_x(0, 2)
-            turn_x(0, 3)
-            copy_x(0, 3)
-            quant_k(0, 4)
-            widen(0, 8)
-            quant_x(0, 2)
-            quant_x(0, 3)
-            turn_beta()
-            copy_beta()
-            widen(0, 14)
-            interleave(0, 12)
-            values(0, 0, 0)
-            values(0, 0, 1)
-            values(0, 0, 2)
-            values(0, 0, 3)
-            widen(0, 10)
-            interleave(0, 8)
-            quant_k(0, 6)
-            interleave(0, 10)
-            quant_k(0, 8)
-            subtract(0, 0, 0)
-            subtract(0, 0, 1)
-            subtract(0, 0, 2)
-            subtract(0, 0, 3)
-            values(0, 1, 0)
-            values(0, 1, 1)
-            values(0, 1, 2)
-            values(0, 1, 3)
-            quant_k(0, 10)
-            scale_dv(0, 0, 0)
-            quant_k(0, 12)
-            quant_dv(0, 0, 0)
-            widen(1, 0)
-            interleave(0, 14)
-            widen(1, 2)
-            interleave(1, 0)
-            turn_x(1, 0)
-            copy_x(1, 0)
-            turn_x(1, 1)
-            copy_x(1, 1)
-            update(0, 0, 0)
-            scale_dv(0, 0, 1)
-            subtract(0, 1, 0)
-            subtract(0, 1, 1)
-            subtract(0, 1, 2)
-            subtract(0, 1, 3)
-            quant_dv(0, 0, 1)
-            quant_k(0, 14)
-            turn_x(1, 2)
-            copy_x(1, 2)
-            turn_x(1, 3)
-            copy_x(1, 3)
-            interleave(1, 2)
-            update(0, 0, 1)
-            scale_dv(0, 1, 0)
-            quant_x(1, 0)
-            quant_x(1, 1)
-            quant_x(1, 2)
-            quant_x(1, 3)
-            values(1, 0, 0)
-            values(1, 0, 1)
-            values(1, 0, 2)
-            values(1, 0, 3)
-            finish(0, 0, 0)
-            quant_dv(0, 1, 0)
-            update(0, 1, 0)
-            widen(1, 4)
-            widen(1, 6)
-            interleave(1, 4)
-            scale_dv(0, 1, 1)
-            subtract(1, 0, 0)
-            subtract(1, 0, 1)
-            subtract(1, 0, 2)
-            subtract(1, 0, 3)
-            values(1, 1, 0)
-            values(1, 1, 1)
-            values(1, 1, 2)
-            values(1, 1, 3)
-            finish(0, 0, 1)
-            finish(0, 1, 0)
-            widen(1, 8)
-            interleave(1, 6)
-            quant_dv(0, 1, 1)
-            quant_k(1, 0)
-            update(0, 1, 1)
-            quant_k(1, 2)
-            scale_dv(1, 0, 0)
-            quant_k(1, 4)
-            quant_dv(1, 0, 0)
-            update(1, 0, 0)
-            widen(1, 10)
-            interleave(1, 8)
-            widen(1, 12)
-            interleave(1, 10)
-            widen(1, 14)
-            interleave(1, 12)
-            interleave(1, 14)
-            scale_dv(1, 0, 1)
-            subtract(1, 1, 0)
-            subtract(1, 1, 1)
-            subtract(1, 1, 2)
-            subtract(1, 1, 3)
-            finish(0, 1, 1)
-            finish(1, 0, 0)
-            quant_dv(1, 0, 1)
-            quant_k(1, 6)
-            update(1, 0, 1)
-            scale_dv(1, 1, 0)
-            quant_k(1, 8)
-            scale_dv(1, 1, 1)
-            quant_dv(1, 1, 0)
-            finish(1, 0, 1)
-            quant_k(1, 10)
-            update(1, 1, 0)
-            quant_dv(1, 1, 1)
-            quant_k(1, 12)
-            finish(1, 1, 0)
-            quant_k(1, 14)
-            update(1, 1, 1)
-            finish(1, 1, 1)
+
+        widen(0)
+        widen(1)
+        interleave(0)
+        turn_x(0, 0, 0)
+        copy_x(0, 0, 0)
+        turn_x(0, 0, 1)
+        copy_x(0, 0, 1)
+        widen(2)
+        quant_k(0)
+        interleave(1)
+        interleave(2)
+        turn_x(0, 1, 0)
+        copy_x(0, 1, 0)
+        widen(3, (0,))
+        turn_x(0, 1, 1)
+        copy_x(0, 1, 1)
+        quant_x(0, 0, 0)
+        quant_x(0, 0, 1)
+        turn_beta()
+        first_values(0)
+        quant_k(1)
+        quant_x(0, 1, 0)
+        quant_k(2)
+        quant_x(0, 1, 1)
+        widen(3, (1,))
+        copy_beta()
+        widen(4)
+        widen(5)
+        values(2)
+        first_values(1)
+        values(3)
+        interleave(3)
+        copy_values(2)
+        copy_values(3)
+        widened = (4, 5)
+        for r in range(QUADS - 1):
+            q0, q1 = 2 * r, 2 * r + 1
+            quarters = [(r, g) for g in range(2)] if r < 2 else []
+            to_widen = WIDEN_IN[r]
+            if q0 + 4 < PAIRS:
+                values(q0 + 4)
+                copy_values(q0 + 4)
+            for quarter in quarters:
+                turn_x(1, *quarter)
+                copy_x(1, *quarter)
+            for k in widened:
+                if k in ON_SIDE:
+                    interleave(k)
+            if r == 0:
+                first_subtract(0)
+                first_subtract(1)
+                quant_k(3)
+                lay_vo(2)
+            else:
+                lay_vo(q0 + 2)
+                scale_dv(q0)
+                scale_dv(q1)
+                finish(q0 - 2, 2)
+            add_values(q0 + 2)
+            lay_vo(q1 + 2)
+            add_values(q1 + 2)
+            for k in to_widen[:1]:
+                widen(k)
+            if q1 + 4 < PAIRS:
+                values(q1 + 4)
+                copy_values(q1 + 4)
+            for k in to_widen[1:]:
+                widen(k)
+            if r == 0:
+                first_scale()
+            mine = [k for k in widened if k not in ON_SIDE]
+            for k in mine[:1]:
+                interleave(k)
+            quant_dv(q0, 2)
+            for k in mine[1:]:
+                interleave(k)
+            for quarter in quarters:
+                quant_x(1, *quarter)
+            for k in mine[:1]:
+                quant_k(k)
+            for k in widened:
+                if k in ON_SIDE:
+                    quant_k(k)
+            for k in mine[1:]:
+                quant_k(k)
+            update(q0, 2)
+            widened = to_widen
+        q0, q1 = PAIRS - 2, PAIRS - 1
+        for k in widened:
+            if k in ON_SIDE:
+                interleave(k)
+        scale_dv(q0)
+        scale_dv(q1)
+        for k in widened:
+            if k not in ON_SIDE:
+                interleave(k)
+        quant_dv(q0, 1)
+        for k in widened:
+            quant_k(k)
+        quant_dv(q1, 1)
+        update(q0, 1)
+        finish(q0 - 2, 2)
+        update(q1, 1)
+        finish(q0, 1)
+        finish(q1, 1)

@@ -23,10 +23,7 @@ PAIRS = B * H // 2
 QUADS = PAIRS // 2
 FLOPS = 2 * B * N * D * H * DH + 2 * B * H * N * S * DH
 
-WIDEN_ON_VECTOR = (0, 2, 4)
-INTERLEAVE_ON_SCALAR = (15,)
-WIDEN_IN = ((6,), (7,), (8, 9), (10, 11), (12, 13), (14,), (15,))
-ON_SIDE = (15,)
+STRIDE = 3
 
 
 def tile_dpfpattention_pb_w4_kernel(tc, x, wv_words, wv_scales, beta, vo, k_phi_bytes, k_phi_scale, W, out):
@@ -47,15 +44,14 @@ def tile_dpfpattention_pb_w4_kernel(tc, x, wv_words, wv_scales, beta, vo, k_phi_
         nc.gpsimd.memset(beta_rows[:].bitcast(I32), 0)
         nc.gpsimd.dma_start(out=beta_rows[0 : B * H, :], in_=beta.rearrange("b h n -> (b h) n"))
         kscale = keep.tile([P, PACK], F32, name="kscale")
-        ww = keep.tile([P, 2, 2 * D], U8, align_bytes=64, name="ww")
-        kb, xs, vos, ws = {}, {}, {}, {}
+        kb, xs, vos, ws, ww = {}, {}, {}, {}, {}
 
         def load_kphi(q0, nq):
             b, h0 = divmod(2 * q0, H)
             kbt = keep.tile([P, 2 * nq, PACK * S], U8, align_bytes=64, name=f"kb_{q0}")
             nc.sync.dma_start(out=kbt[:], in_=k_phi_bytes[b, h0 : h0 + 2 * nq].rearrange("h (p t) s -> p h (t s)", t=PACK))
-            for q in range(nq):
-                kb[q0 + q] = kbt[:, 2 * q : 2 * q + 2, :]
+            for i in range(2 * nq):
+                kb[2 * q0 + i] = kbt[:, i, :]
 
         def load_x(b, tp):
             xt = keep.tile([P, 2, D], BF16, align_bytes=64, name=f"x_{b}_{tp}")
@@ -71,10 +67,16 @@ def tile_dpfpattention_pb_w4_kernel(tc, x, wv_words, wv_scales, beta, vo, k_phi_
             )
             vos[r] = v
 
-        def load_W(b):
-            w = keep.tile([P, H, DH], BF16, align_bytes=64, name=f"W_{b}")
-            nc.sync.dma_start(out=w[:], in_=W[b].rearrange("h s d -> s h d"))
-            ws[b] = w
+        def load_W(u):
+            b, h0 = divmod(8 * u, H)
+            w = keep.tile([P, 8, DH], BF16, align_bytes=64, name=f"W_{u}")
+            nc.sync.dma_start(out=w[:], in_=W[b, h0 : h0 + 8].rearrange("h s d -> s h d"))
+            ws[u] = w
+
+        def load_weight(half):
+            w = keep.tile([P, 2, D], U8, align_bytes=64, name=f"ww_{half}")
+            nc.sync.dma_start(out=w[:], in_=wv_words[:, :, D * half : D * (half + 1)].rearrange("g p n -> p g n"))
+            ww[half] = w
 
         def load_weight_scales():
             for q in range(4):
@@ -91,25 +93,29 @@ def tile_dpfpattention_pb_w4_kernel(tc, x, wv_words, wv_scales, beta, vo, k_phi_
         load_x(0, 1)
         load_kphi(3, 1)
         load_weight_scales()
-        nc.sync.dma_start(out=ww[:], in_=wv_words.rearrange("g p n -> p g n"))
-        load_kphi(4, 2)
+        load_weight(0)
+        load_kphi(4, 1)
         load_vo(0)
-        load_vo(1)
+        load_kphi(5, 1)
+        load_weight(1)
         load_x(1, 0)
+        load_vo(1)
         load_kphi(6, 2)
         load_x(1, 1)
-        load_vo(2)
         load_W(0)
+        load_vo(2)
         load_kphi(8, 2)
         load_vo(3)
         load_kphi(10, 2)
+        load_W(1)
         load_vo(4)
         load_kphi(12, 2)
-        load_W(1)
         load_vo(5)
+        load_W(2)
         load_kphi(14, 2)
         load_vo(6)
         load_vo(7)
+        load_W(3)
 
         beta2 = keep.tile([P, B * H, PACK, 2], BF16, align_bytes=64, name="beta2")
         beta4 = keep.tile([P, 4, PACK, RUN], BF16, align_bytes=64, name="beta4")
@@ -161,33 +167,42 @@ def tile_dpfpattention_pb_w4_kernel(tc, x, wv_words, wv_scales, beta, vo, k_phi_
 
         planes, inter, kc = {}, {}, {}
 
-        def widen(q, heads=(0, 1)):
-            if q not in planes:
-                planes[q] = work.tile([P, PACK, 2, S], BF16, align_bytes=64, name="planes", bufs=16)
-            pl = planes[q]
-            for i in heads:
+        def widen(h0, nh, engine):
+            pl = work.tile([P, PACK, nh, S], BF16, align_bytes=64, name="planes", bufs=12)
+            for i in range(nh):
                 for t in range(PACK):
-                    src = kb[q][:, i, S * t : S * (t + 1)].bitcast(FP8)
-                    if q in WIDEN_ON_VECTOR:
+                    src = kb[h0 + i][:, S * t : S * (t + 1)].bitcast(FP8)
+                    if engine is nc.vector:
                         nc.vector.tensor_scalar(out=pl[:, t, i, :], in0=src, scalar1=kscale[:, t : t + 1], scalar2=None, op0=ALU.mult)
                     else:
                         nc.scalar.activation(out=pl[:, t, i, :], in_=src, func=ACT.Copy, scale=kscale[:, t : t + 1])
+                planes[h0 + i] = (pl, i)
 
-        def interleave(q):
-            it = work.tile([P, 2 * S, PACK], BF16, align_bytes=64, name="inter", bufs=8)
-            dst = it[:].rearrange("p (c i) t -> p c t i", i=RUN)
-            src = planes[q][:].rearrange("p t h (c i) -> p (h c) t i", i=RUN)
-            if q in INTERLEAVE_ON_SCALAR:
+        def interleave(h0, nh, engine):
+            on_gpsimd = engine is nc.gpsimd
+            it = work.tile([P, nh, S, PACK], BF16, align_bytes=64, name="inter", tag="inter_g" if on_gpsimd else "inter", bufs=1 if on_gpsimd else 8)
+            pl, i = planes[h0]
+            dst = it[:].rearrange("p h (c i) t -> p h c t i", i=RUN)
+            src = pl[:, :, i : i + nh].rearrange("p t h (c i) -> p h c t i", i=RUN)
+            if on_gpsimd:
+                nc.gpsimd.tensor_scalar(out=dst, in0=src, scalar1=1.0, scalar2=0.0, op0=ALU.mult, op1=ALU.add)
+            elif engine is nc.scalar:
                 nc.scalar.copy(out=dst, in_=src)
             else:
                 nc.vector.tensor_copy(out=dst, in_=src)
-            inter[q] = it
+            inter[h0] = (it, nh)
 
-        def quant_k(q):
-            codes = keep.tile([P, 2 * S], U32, align_bytes=64, name=f"kc_{q}")
-            scales = keep.tile([P, 2 * S], U8, align_bytes=64, name=f"ksc_{q}")
-            nc.vector.quantize_mx(out=codes[:].bitcast(E4M3X4), scales=scales[:], in_=inter[q][:].rearrange("p c t -> p (c t)"))
-            kc[q] = (codes, scales)
+        def quant_k(h0):
+            it, nh = inter[h0]
+            codes = keep.tile([P, nh, S], U32, align_bytes=64, name=f"kc_{h0}")
+            scales = keep.tile([P, nh, S], U8, align_bytes=64, name=f"ksc_{h0}")
+            nc.vector.quantize_mx(
+                out=codes[:].rearrange("p h s -> p (h s)").bitcast(E4M3X4),
+                scales=scales[:].rearrange("p h s -> p (h s)"),
+                in_=it[:].rearrange("p h s t -> p (h s t)"),
+            )
+            for i in range(nh):
+                kc[h0 + i] = (codes[:, i, :], scales[:, i, :])
 
         vps, vts, diffs, dvg, dvc, ops = {}, {}, {}, {}, {}, {}
 
@@ -200,7 +215,7 @@ def tile_dpfpattention_pb_w4_kernel(tc, x, wv_words, wv_scales, beta, vo, k_phi_
                         out=ps[:, t, :],
                         lhsT=xcodes[0, g][:, cols].bitcast(E4M3X4),
                         lhsT_scale=xscales[0, g][:, cols],
-                        rhs=ww[:, g, 0 : 8 * DH].bitcast(E2M1X4),
+                        rhs=ww[0][:, g, 0 : 8 * DH].bitcast(E2M1X4),
                         rhs_scale=wsc[:, g, 0 : 4 * DH],
                         start=(g == 0),
                         stop=(g == 1),
@@ -234,7 +249,7 @@ def tile_dpfpattention_pb_w4_kernel(tc, x, wv_words, wv_scales, beta, vo, k_phi_
             for g in range(2):
                 nc.tensor.matmul_mx(
                     out=ps[:],
-                    lhsT=ww[:, g, 2 * P * j : 2 * P * (j + 1)].bitcast(E2M1X4),
+                    lhsT=ww[j // 4][:, g, 2 * P * (j % 4) : 2 * P * (j % 4 + 1)].bitcast(E2M1X4),
                     lhsT_scale=wsc[:, g, P * j : P * (j + 1)],
                     rhs=xcodes[b, g][:].bitcast(E4M3X4),
                     rhs_scale=xscales[b, g][:],
@@ -293,12 +308,11 @@ def tile_dpfpattention_pb_w4_kernel(tc, x, wv_words, wv_scales, beta, vo, k_phi_
             ps = psum.tile([P, 2 * nq, DH], F32, name="o", bufs=2)
             dcodes, dscales = dvc[q0]
             for i in range(2 * nq):
-                kcodes, kscales = kc[q0 + i // 2]
-                cols = slice(S * (i % 2), S * (i % 2 + 1))
+                kcodes, kscales = kc[2 * q0 + i]
                 nc.tensor.matmul_mx(
                     out=ps[:, i, :],
-                    lhsT=kcodes[:, cols].bitcast(E4M3X4),
-                    lhsT_scale=kscales[:, cols],
+                    lhsT=kcodes.bitcast(E4M3X4),
+                    lhsT_scale=kscales,
                     rhs=dcodes[:, DH * i : DH * (i + 1)].bitcast(E4M3X4),
                     rhs_scale=dscales[:, DH * i : DH * (i + 1)],
                     start=True,
@@ -309,62 +323,67 @@ def tile_dpfpattention_pb_w4_kernel(tc, x, wv_words, wv_scales, beta, vo, k_phi_
         def finish(q0, nq):
             b, h0 = divmod(2 * q0, H)
             ot = work.tile([P, 2 * nq, DH], F32, align_bytes=64, name="ot", bufs=4)
-            nc.vector.tensor_tensor(out=ot[:], in0=ops[q0][:], in1=ws[b][:, h0 : h0 + 2 * nq, :], op=ALU.add)
+            nc.vector.tensor_tensor(out=ot[:], in0=ops[q0][:], in1=ws[q0 // 4][:, h0 % 8 : h0 % 8 + 2 * nq, :], op=ALU.add)
             nc.sync.dma_start(out=out[b, h0 : h0 + 2 * nq].rearrange("h s d -> s h d"), in_=ot[:])
 
 
-        widen(0)
-        widen(1)
-        interleave(0)
+        widen(0, 2, nc.vector)
+        widen(2, 2, nc.scalar)
+        interleave(0, 1, nc.vector)
+        interleave(1, 1, nc.vector)
+        interleave(2, 1, nc.scalar)
+        interleave(3, 1, nc.scalar)
         turn_x(0, 0, 0)
         copy_x(0, 0, 0)
         turn_x(0, 0, 1)
         copy_x(0, 0, 1)
-        widen(2)
         quant_k(0)
-        interleave(1)
-        interleave(2)
+        quant_k(1)
+        widen(4, 2, nc.vector)
+        quant_k(2)
+        interleave(4, 2, nc.vector)
+        quant_k(3)
         turn_x(0, 1, 0)
         copy_x(0, 1, 0)
-        widen(3, (0,))
         turn_x(0, 1, 1)
         copy_x(0, 1, 1)
         quant_x(0, 0, 0)
         quant_x(0, 0, 1)
         turn_beta()
         first_values(0)
-        quant_k(1)
+        widen(6, 2, nc.vector)
         quant_x(0, 1, 0)
-        quant_k(2)
+        quant_k(4)
         quant_x(0, 1, 1)
-        widen(3, (1,))
         copy_beta()
-        widen(4)
-        widen(5)
-        values(2)
         first_values(1)
+        values(2)
         values(3)
-        interleave(3)
+        interleave(6, 2, nc.vector)
+        widen(8, 2, nc.scalar)
+        widen(10, 1, nc.scalar)
+        widen(11, 1, nc.scalar)
+        quant_k(6)
+        interleave(8, 2, nc.vector)
         copy_values(2)
         copy_values(3)
-        widened = (4, 5)
+        ready = (10, 2)
         for r in range(QUADS - 1):
             q0, q1 = 2 * r, 2 * r + 1
             quarters = [(r, g) for g in range(2)] if r < 2 else []
-            to_widen = WIDEN_IN[r]
+            h0, nh = ready
             if q0 + 4 < PAIRS:
                 values(q0 + 4)
                 copy_values(q0 + 4)
+            if r > 0:
+                update(q0 - 2, 2)
             for quarter in quarters:
                 turn_x(1, *quarter)
                 copy_x(1, *quarter)
-            for k in widened:
-                if k in ON_SIDE:
-                    interleave(k)
+            interleave(h0, 1, nc.gpsimd)
             if r == 0:
                 first_subtract(0)
                 first_subtract(1)
-                quant_k(3)
                 lay_vo(2)
             else:
                 lay_vo(q0 + 2)
@@ -374,47 +393,34 @@ def tile_dpfpattention_pb_w4_kernel(tc, x, wv_words, wv_scales, beta, vo, k_phi_
             add_values(q0 + 2)
             lay_vo(q1 + 2)
             add_values(q1 + 2)
-            for k in to_widen[:1]:
-                widen(k)
+            ready = (h0 + nh, min(STRIDE, B * H - h0 - nh))
+            widen(ready[0], 1, nc.scalar)
+            widen(ready[0] + 1, ready[1] - 1, nc.scalar)
             if q1 + 4 < PAIRS:
                 values(q1 + 4)
                 copy_values(q1 + 4)
-            for k in to_widen[1:]:
-                widen(k)
             if r == 0:
+                quant_k(8)
                 first_scale()
-            mine = [k for k in widened if k not in ON_SIDE]
-            for k in mine[:1]:
-                interleave(k)
+            interleave(h0 + 1, nh - 1, nc.vector)
             quant_dv(q0, 2)
-            for k in mine[1:]:
-                interleave(k)
             for quarter in quarters:
                 quant_x(1, *quarter)
-            for k in mine[:1]:
-                quant_k(k)
-            for k in widened:
-                if k in ON_SIDE:
-                    quant_k(k)
-            for k in mine[1:]:
-                quant_k(k)
-            update(q0, 2)
-            widened = to_widen
+            quant_k(h0)
+            quant_k(h0 + 1)
         q0, q1 = PAIRS - 2, PAIRS - 1
-        for k in widened:
-            if k in ON_SIDE:
-                interleave(k)
+        h0, nh = ready
+        update(q0 - 2, 2)
+        interleave(h0, 1, nc.gpsimd)
+        interleave(h0 + 1, 1, nc.scalar)
         scale_dv(q0)
         scale_dv(q1)
-        for k in widened:
-            if k not in ON_SIDE:
-                interleave(k)
-        quant_dv(q0, 1)
-        for k in widened:
-            quant_k(k)
-        quant_dv(q1, 1)
-        update(q0, 1)
         finish(q0 - 2, 2)
+        quant_dv(q0, 1)
+        quant_k(h0)
+        quant_dv(q1, 1)
+        quant_k(h0 + 1)
+        update(q0, 1)
         update(q1, 1)
         finish(q0, 1)
         finish(q1, 1)

@@ -185,7 +185,8 @@ def tile_dpfpattention_pb_w4_kernel(tc, x, wv_words, wv_scales, beta, vo, k_phi_
             dst = it[:].rearrange("p h (c i) t -> p h c t i", i=RUN)
             src = pl[:, :, i : i + nh].rearrange("p t h (c i) -> p h c t i", i=RUN)
             if on_gpsimd:
-                nc.gpsimd.tensor_scalar(out=dst, in0=src, scalar1=1.0, scalar2=0.0, op0=ALU.mult, op1=ALU.add)
+                by_column = pl[:, :, i : i + nh].rearrange("p t h s -> p h s t")
+                nc.gpsimd.tensor_scalar(out=it[:], in0=by_column, scalar1=1.0, scalar2=0.0, op0=ALU.mult, op1=ALU.add)
             elif engine is nc.scalar:
                 nc.scalar.copy(out=dst, in_=src)
             else:
@@ -265,14 +266,13 @@ def tile_dpfpattention_pb_w4_kernel(tc, x, wv_words, wv_scales, beta, vo, k_phi_
 
         def lay_vo(q):
             ps = psum.tile([P, 2, DH // 2, PACK, 2], F32, name="diff", bufs=3)
-            for i in range(2):
-                nc.tensor.matmul(
-                    ps[:, i].rearrange("p c t e -> p t c e"),
-                    lhsT=minus_ident[:],
-                    rhs=vos[q // 2][:, 2 * (q % 2) + i].rearrange("p t (c e) -> p t c e", e=2),
-                    start=(i == 0),
-                    stop=False,
-                )
+            nc.tensor.matmul(
+                ps[:].rearrange("p h c t e -> p t h c e"),
+                lhsT=minus_ident[:],
+                rhs=vos[q // 2][:, 2 * (q % 2) : 2 * (q % 2) + 2].rearrange("p h t (c e) -> p t h c e", e=2),
+                start=True,
+                stop=False,
+            )
             diffs[q] = ps
 
         def add_values(q):
@@ -305,16 +305,17 @@ def tile_dpfpattention_pb_w4_kernel(tc, x, wv_words, wv_scales, beta, vo, k_phi_
             dvc[q0] = (codes, scales)
 
         def update(q0, nq):
-            ps = psum.tile([P, 2 * nq, DH], F32, name="o", bufs=2)
+            ps = psum.tile([P, 2 * nq, 2 * DH], F32, name="o", bufs=2)
             dcodes, dscales = dvc[q0]
             for i in range(2 * nq):
                 kcodes, kscales = kc[2 * q0 + i]
+                pair = slice(2 * DH * (i // 2), 2 * DH * (i // 2 + 1))
                 nc.tensor.matmul_mx(
                     out=ps[:, i, :],
                     lhsT=kcodes.bitcast(E4M3X4),
                     lhsT_scale=kscales,
-                    rhs=dcodes[:, DH * i : DH * (i + 1)].bitcast(E4M3X4),
-                    rhs_scale=dscales[:, DH * i : DH * (i + 1)],
+                    rhs=dcodes[:, pair].bitcast(E4M3X4),
+                    rhs_scale=dscales[:, pair],
                     start=True,
                     stop=True,
                 )
@@ -323,7 +324,13 @@ def tile_dpfpattention_pb_w4_kernel(tc, x, wv_words, wv_scales, beta, vo, k_phi_
         def finish(q0, nq):
             b, h0 = divmod(2 * q0, H)
             ot = work.tile([P, 2 * nq, DH], F32, align_bytes=64, name="ot", bufs=4)
-            nc.vector.tensor_tensor(out=ot[:], in0=ops[q0][:], in1=ws[q0 // 4][:, h0 % 8 : h0 % 8 + 2 * nq, :], op=ALU.add)
+            own = ops[q0][:].rearrange("p (j i) (k d) -> p j (i k) d", i=2, k=2)[:, :, 0:4:3, :]
+            nc.vector.tensor_tensor(
+                out=ot[:].rearrange("p (j i) d -> p j i d", i=2),
+                in0=own,
+                in1=ws[q0 // 4][:, h0 % 8 : h0 % 8 + 2 * nq, :].rearrange("p (j i) d -> p j i d", i=2),
+                op=ALU.add,
+            )
             nc.sync.dma_start(out=out[b, h0 : h0 + 2 * nq].rearrange("h s d -> s h d"), in_=ot[:])
 
 

@@ -67,11 +67,11 @@ def tile_dpfpattention_pb_w4_kernel(tc, x, wv_words, wv_scales, beta, vo, k_phi_
             )
             vos[r] = v
 
-        def load_W(u):
-            b, h0 = divmod(8 * u, H)
-            w = keep.tile([P, 8, DH], BF16, align_bytes=64, name=f"W_{u}")
-            nc.sync.dma_start(out=w[:], in_=W[b, h0 : h0 + 8].rearrange("h s d -> s h d"))
-            ws[u] = w
+        def load_W(r):
+            b, h0 = divmod(4 * r, H)
+            w = keep.tile([P, 4, DH], BF16, align_bytes=64, name=f"W_{r}")
+            nc.sync.dma_start(out=w[:], in_=W[b, h0 : h0 + 4].rearrange("h s d -> s h d"))
+            ws[r] = w
 
         def load_weight(half):
             w = keep.tile([P, 2, D], U8, align_bytes=64, name=f"ww_{half}")
@@ -101,21 +101,25 @@ def tile_dpfpattention_pb_w4_kernel(tc, x, wv_words, wv_scales, beta, vo, k_phi_
         load_x(1, 0)
         load_vo(1)
         load_kphi(6, 2)
-        load_x(1, 1)
         load_W(0)
+        load_x(1, 1)
         load_vo(2)
         load_kphi(8, 2)
+        load_W(1)
         load_vo(3)
         load_kphi(10, 2)
-        load_W(1)
+        load_W(2)
         load_vo(4)
         load_kphi(12, 2)
-        load_vo(5)
-        load_W(2)
-        load_kphi(14, 2)
-        load_vo(6)
-        load_vo(7)
         load_W(3)
+        load_vo(5)
+        load_kphi(14, 2)
+        load_W(4)
+        load_vo(6)
+        load_W(5)
+        load_vo(7)
+        load_W(6)
+        load_W(7)
 
         beta2 = keep.tile([P, B * H, PACK, 2], BF16, align_bytes=64, name="beta2")
         beta4 = keep.tile([P, 4, PACK, RUN], BF16, align_bytes=64, name="beta4")
@@ -323,12 +327,12 @@ def tile_dpfpattention_pb_w4_kernel(tc, x, wv_words, wv_scales, beta, vo, k_phi_
 
         def finish(q0, nq):
             b, h0 = divmod(2 * q0, H)
-            ot = work.tile([P, 2 * nq, DH], F32, align_bytes=64, name="ot", bufs=4)
+            ot = work.tile([P, 2 * nq, DH], F32, align_bytes=64, name="ot", bufs=9)
             own = ops[q0][:].rearrange("p (j i) (k d) -> p j (i k) d", i=2, k=2)[:, :, 0:4:3, :]
             nc.vector.tensor_tensor(
                 out=ot[:].rearrange("p (j i) d -> p j i d", i=2),
                 in0=own,
-                in1=ws[q0 // 4][:, h0 % 8 : h0 % 8 + 2 * nq, :].rearrange("p (j i) d -> p j i d", i=2),
+                in1=ws[q0 // 2][:, h0 % 4 : h0 % 4 + 2 * nq, :].rearrange("p (j i) d -> p j i d", i=2),
                 op=ALU.add,
             )
             nc.sync.dma_start(out=out[b, h0 : h0 + 2 * nq].rearrange("h s d -> s h d"), in_=ot[:])

@@ -23,8 +23,6 @@ PAIRS = B * H // 2
 QUADS = PAIRS // 2
 FLOPS = 2 * B * N * D * H * DH + 2 * B * H * N * S * DH
 
-STRIDE = 3
-
 
 def tile_dpfpattention_pb_w4_kernel(tc, x, wv_words, wv_scales, beta, vo, k_phi_bytes, k_phi_scale, W, out):
     nc = tc.nc
@@ -34,6 +32,7 @@ def tile_dpfpattention_pb_w4_kernel(tc, x, wv_words, wv_scales, beta, vo, k_phi_
         psum = ctx.enter_context(tc.psum_pool(name="psum", bufs=2))
         ctx.enter_context(tc.manual_schedule())
 
+        kscale = keep.tile([P, PACK], F32, name="kscale")
         ident = keep.tile([P, P], F32, name="ident")
         make_identity(nc, ident[:])
         minus_ident = keep.tile([P, P], BF16, name="minus_ident")
@@ -41,22 +40,21 @@ def tile_dpfpattention_pb_w4_kernel(tc, x, wv_words, wv_scales, beta, vo, k_phi_
         wsc = keep.tile([P, 2, D], U8, align_bytes=64, name="wsc")
         nc.gpsimd.memset(wsc[:].rearrange("p g n -> p (g n)").bitcast(I32), 0)
         beta_rows = keep.tile([P, N], BF16, align_bytes=64, name="beta_rows")
-        nc.gpsimd.memset(beta_rows[:].bitcast(I32), 0)
-        nc.gpsimd.dma_start(out=beta_rows[0 : B * H, :], in_=beta.rearrange("b h n -> (b h) n"))
-        kscale = keep.tile([P, PACK], F32, name="kscale")
+        nc.vector.memset(beta_rows[:].bitcast(I32), 0)
         kb, xs, vos, ws, ww = {}, {}, {}, {}, {}
 
-        def load_kphi(q0, nq):
-            b, h0 = divmod(2 * q0, H)
-            kbt = keep.tile([P, 2 * nq, PACK * S], U8, align_bytes=64, name=f"kb_{q0}")
-            nc.sync.dma_start(out=kbt[:], in_=k_phi_bytes[b, h0 : h0 + 2 * nq].rearrange("h (p t) s -> p h (t s)", t=PACK))
-            for i in range(2 * nq):
-                kb[2 * q0 + i] = kbt[:, i, :]
+        def load_kphi(first, nh):
+            b, h0 = divmod(first, H)
+            kbt = keep.tile([P, nh, PACK * S], U8, align_bytes=64, name=f"kb_{first}")
+            nc.sync.dma_start(out=kbt[:], in_=k_phi_bytes[b, h0 : h0 + nh].rearrange("h (p t) s -> p h (t s)", t=PACK))
+            for i in range(nh):
+                kb[first + i] = kbt[:, i, :]
 
-        def load_x(b, tp):
-            xt = keep.tile([P, 2, D], BF16, align_bytes=64, name=f"x_{b}_{tp}")
-            nc.sync.dma_start(out=xt[:], in_=x[b].rearrange("(p t) k -> p t k", t=PACK)[:, 2 * tp : 2 * tp + 2, :])
-            xs[b, tp] = xt
+        def load_x(b, t0, nt):
+            xt = keep.tile([P, nt, D], BF16, align_bytes=64, name=f"x_{b}_{t0}")
+            nc.sync.dma_start(out=xt[:], in_=x[b].rearrange("(p t) k -> p t k", t=PACK)[:, t0 : t0 + nt, :])
+            for t in range(nt):
+                xs[b, t0 + t] = xt[:, t, :]
 
         def load_vo(r):
             b, h0 = divmod(4 * r, H)
@@ -88,36 +86,40 @@ def tile_dpfpattention_pb_w4_kernel(tc, x, wv_words, wv_scales, beta, vo, k_phi_
         nc.sync.dma_start(out=kscale[:], in_=k_phi_scale.rearrange("a c (p t) f -> p (a c t f)", t=PACK))
         load_kphi(0, 1)
         load_kphi(1, 1)
-        load_x(0, 0)
-        load_kphi(2, 1)
-        load_x(0, 1)
-        load_kphi(3, 1)
+        load_kphi(2, 2)
+        nc.sync.dma_start(out=beta_rows[0 : B * H, :], in_=beta.rearrange("b h n -> (b h) n"))
+        load_x(0, 0, 1)
+        load_x(0, 1, 1)
+        load_kphi(4, 2)
+        load_x(0, 2, 1)
+        load_x(0, 3, 1)
+        load_kphi(6, 2)
         load_weight_scales()
         load_weight(0)
-        load_kphi(4, 1)
+        load_kphi(8, 4)
         load_vo(0)
-        load_kphi(5, 1)
-        load_weight(1)
-        load_x(1, 0)
         load_vo(1)
-        load_kphi(6, 2)
-        load_W(0)
-        load_x(1, 1)
-        load_vo(2)
-        load_kphi(8, 2)
-        load_W(1)
-        load_vo(3)
-        load_kphi(10, 2)
-        load_W(2)
-        load_vo(4)
+        load_weight(1)
         load_kphi(12, 2)
-        load_W(3)
-        load_vo(5)
+        load_x(1, 0, 2)
+        load_vo(2)
         load_kphi(14, 2)
-        load_W(4)
+        load_x(1, 2, 2)
+        load_W(0)
+        load_kphi(16, 4)
+        load_vo(3)
+        load_W(1)
+        load_kphi(20, 4)
+        load_vo(4)
+        load_W(2)
+        load_kphi(24, 4)
+        load_vo(5)
+        load_W(3)
+        load_kphi(28, 4)
         load_vo(6)
-        load_W(5)
+        load_W(4)
         load_vo(7)
+        load_W(5)
         load_W(6)
         load_W(7)
 
@@ -149,13 +151,14 @@ def tile_dpfpattention_pb_w4_kernel(tc, x, wv_words, wv_scales, beta, vo, k_phi_
                 xcodes[b, g] = keep.tile([P, N], U32, align_bytes=64, name=f"xc_{b}_{g}")
                 xscales[b, g] = keep.tile([P, N], U8, align_bytes=64, name=f"xsc_{b}_{g}")
 
-        def turn_x(b, tp, g):
-            ps = psum.tile([P, 2, 2, P], F32, name="turn", bufs=3)
+        def turn_x(b, tp):
+            for g in range(2):
+                turned[b, tp, g] = psum.tile([P, 2, 2, P], F32, name="turn", bufs=3)
             for t in range(2):
-                words = xs[b, tp][:, t, :].bitcast(F32)
-                for u in range(2):
-                    nc.tensor.transpose(ps[:, t, u, :], words[:, 256 * g + u : 256 * (g + 1) : 2], ident[:])
-            turned[b, tp, g] = ps
+                words = xs[b, 2 * tp + t].bitcast(F32)
+                for g in range(2):
+                    for u in range(2):
+                        nc.tensor.transpose(turned[b, tp, g][:, t, u, :], words[:, 256 * g + u : 256 * (g + 1) : 2], ident[:])
 
         def copy_x(b, tp, g):
             gt = work.tile([P, 2 * P * PACK], BF16, align_bytes=64, name="xg", bufs=8)
@@ -338,100 +341,119 @@ def tile_dpfpattention_pb_w4_kernel(tc, x, wv_words, wv_scales, beta, vo, k_phi_
             nc.sync.dma_start(out=out[b, h0 : h0 + 2 * nq].rearrange("h s d -> s h d"), in_=ot[:])
 
 
-        widen(0, 2, nc.vector)
-        widen(2, 2, nc.scalar)
+        widen(0, 1, nc.vector)
+        widen(1, 1, nc.scalar)
+        widen(2, 2, nc.vector)
         interleave(0, 1, nc.vector)
-        interleave(1, 1, nc.vector)
-        interleave(2, 1, nc.scalar)
-        interleave(3, 1, nc.scalar)
-        turn_x(0, 0, 0)
+        interleave(1, 1, nc.scalar)
+        interleave(2, 2, nc.vector)
+        turn_beta()
+        copy_beta()
+        turn_x(0, 0)
         copy_x(0, 0, 0)
-        turn_x(0, 0, 1)
         copy_x(0, 0, 1)
         quant_k(0)
         quant_k(1)
-        widen(4, 2, nc.vector)
         quant_k(2)
-        interleave(4, 2, nc.vector)
-        quant_k(3)
-        turn_x(0, 1, 0)
-        copy_x(0, 1, 0)
-        turn_x(0, 1, 1)
-        copy_x(0, 1, 1)
+        widen(4, 2, nc.vector)
         quant_x(0, 0, 0)
         quant_x(0, 0, 1)
-        turn_beta()
+        interleave(4, 2, nc.vector)
+        widen(6, 1, nc.scalar)
+        turn_x(0, 1)
+        copy_x(0, 1, 0)
+        copy_x(0, 1, 1)
         first_values(0)
-        widen(6, 2, nc.vector)
         quant_x(0, 1, 0)
         quant_k(4)
         quant_x(0, 1, 1)
-        copy_beta()
+        widen(7, 1, nc.scalar)
+        widen(10, 1, nc.scalar)
+        widen(11, 1, nc.scalar)
         first_values(1)
         values(2)
         values(3)
-        interleave(6, 2, nc.vector)
-        widen(8, 2, nc.scalar)
-        widen(10, 1, nc.scalar)
-        widen(11, 1, nc.scalar)
+        interleave(6, 1, nc.vector)
+        widen(8, 1, nc.vector)
+        interleave(7, 1, nc.vector)
         quant_k(6)
-        interleave(8, 2, nc.vector)
+        interleave(8, 1, nc.vector)
+        quant_k(7)
+        widen(9, 1, nc.vector)
+        quant_k(8)
         copy_values(2)
         copy_values(3)
-        ready = (10, 2)
+        for_gpsimd = [9, 10]
+        for_vector = (11, 1)
+        h0 = 12
         for r in range(QUADS - 1):
             q0, q1 = 2 * r, 2 * r + 1
-            quarters = [(r, g) for g in range(2)] if r < 2 else []
-            h0, nh = ready
             if q0 + 4 < PAIRS:
                 values(q0 + 4)
                 copy_values(q0 + 4)
             if r > 0:
                 update(q0 - 2, 2)
-            for quarter in quarters:
-                turn_x(1, *quarter)
-                copy_x(1, *quarter)
-            interleave(h0, 1, nc.gpsimd)
+            if r == 1:
+                turn_x(1, 1)
+                copy_x(1, 1, 0)
+                copy_x(1, 1, 1)
+            lay_vo(q0 + 2)
+            interleave(for_gpsimd[r], 1, nc.gpsimd)
             if r == 0:
                 first_subtract(0)
                 first_subtract(1)
-                lay_vo(2)
             else:
-                lay_vo(q0 + 2)
                 scale_dv(q0)
                 scale_dv(q1)
                 finish(q0 - 2, 2)
-            add_values(q0 + 2)
             lay_vo(q1 + 2)
+            add_values(q0 + 2)
             add_values(q1 + 2)
-            ready = (h0 + nh, min(STRIDE, B * H - h0 - nh))
-            widen(ready[0], 1, nc.scalar)
-            widen(ready[0] + 1, ready[1] - 1, nc.scalar)
+            if r == 0:
+                turn_x(1, 0)
+            widened = (h0, 2)
+            widen(h0, 2, nc.scalar)
+            if r == 0:
+                copy_x(1, 0, 0)
+                copy_x(1, 0, 1)
             if q1 + 4 < PAIRS:
                 values(q1 + 4)
                 copy_values(q1 + 4)
+            h0 = h0 + 2
+            if h0 < B * H:
+                widen(h0, 1, nc.scalar)
+                for_gpsimd.append(h0)
+                h0 = h0 + 1
+            interleave(*for_vector, nc.vector)
             if r == 0:
-                quant_k(8)
                 first_scale()
-            interleave(h0 + 1, nh - 1, nc.vector)
-            quant_dv(q0, 2)
-            for quarter in quarters:
-                quant_x(1, *quarter)
-            quant_k(h0)
-            quant_k(h0 + 1)
+                quant_k(for_vector[0])
+            if r > 0:
+                quant_dv(q0, 2)
+            if r == 1:
+                for tp in range(2):
+                    quant_x(1, tp, 0)
+                    quant_x(1, tp, 1)
+            quant_k(for_gpsimd[r])
+            if r > 0:
+                quant_k(for_vector[0])
+            else:
+                quant_dv(0, 2)
+            for_vector = widened
         q0, q1 = PAIRS - 2, PAIRS - 1
-        h0, nh = ready
         update(q0 - 2, 2)
-        interleave(h0, 1, nc.gpsimd)
-        interleave(h0 + 1, 1, nc.scalar)
+        interleave(for_gpsimd[-1], 1, nc.gpsimd)
+        interleave(for_vector[0], 1, nc.scalar)
         scale_dv(q0)
         scale_dv(q1)
         finish(q0 - 2, 2)
+        interleave(for_vector[0] + 1, 1, nc.vector)
         quant_dv(q0, 1)
-        quant_k(h0)
-        quant_dv(q1, 1)
-        quant_k(h0 + 1)
+        quant_k(for_gpsimd[-1])
         update(q0, 1)
+        quant_dv(q1, 1)
+        quant_k(for_vector[0])
+        quant_k(for_vector[0] + 1)
         update(q1, 1)
         finish(q0, 1)
         finish(q1, 1)

@@ -56,12 +56,12 @@ def tile_dpfpattention_pb_w4_kernel(tc, x, wv_words, wv_scales, beta, vo, k_phi_
             for t in range(nt):
                 xs[b, t0 + t] = xt[:, t, :]
 
-        def load_vo(r):
+        def load_vo(r, nr=1):
             b, h0 = divmod(4 * r, H)
-            v = keep.tile([P, 4, PACK, DH], BF16, align_bytes=64, name=f"vo_{r}")
+            v = keep.tile([P, 4 * nr, PACK, DH], BF16, align_bytes=64, name=f"vo_{r}")
             nc.sync.dma_start(
                 out=v[:].rearrange("p h t d -> p h (t d)"),
-                in_=vo[b, h0 : h0 + 4].rearrange("h (p t) d -> p h (t d)", t=PACK),
+                in_=vo[b, h0 : h0 + 4 * nr].rearrange("h (p t) d -> p h (t d)", t=PACK),
             )
             vos[r] = v
 
@@ -97,8 +97,7 @@ def tile_dpfpattention_pb_w4_kernel(tc, x, wv_words, wv_scales, beta, vo, k_phi_
         load_weight_scales()
         load_weight(0)
         load_kphi(8, 4)
-        load_vo(0)
-        load_vo(1)
+        load_vo(0, 2)
         load_weight(1)
         load_kphi(12, 2)
         load_x(1, 0, 2)
@@ -123,8 +122,8 @@ def tile_dpfpattention_pb_w4_kernel(tc, x, wv_words, wv_scales, beta, vo, k_phi_
         load_W(6)
         load_W(7)
 
-        beta2 = keep.tile([P, B * H, PACK, 2], BF16, align_bytes=64, name="beta2")
-        beta4 = keep.tile([P, 4, PACK, RUN], BF16, align_bytes=64, name="beta4")
+        beta1 = keep.tile([P, B * H, 2, PACK], BF16, align_bytes=64, name="beta1")
+        beta4 = keep.tile([P, 8, PACK, RUN], BF16, align_bytes=64, name="beta4")
         turned = {}
 
         def turn_beta():
@@ -138,11 +137,11 @@ def tile_dpfpattention_pb_w4_kernel(tc, x, wv_words, wv_scales, beta, vo, k_phi_
             by_slot = turned["beta"][:, :, 0 : B * H].bitcast(BF16).rearrange("p u (r e) -> p r u e", e=2)
             nc.scalar.copy(
                 out=beta4[:].rearrange("p r (u e) i -> p r u e i", e=2),
-                in_=by_slot[:, 0:4].unsqueeze(4).to_broadcast([P, 4, 2, 2, RUN]),
+                in_=by_slot[:, 0:8].unsqueeze(4).to_broadcast([P, 8, 2, 2, RUN]),
             )
             nc.scalar.copy(
-                out=beta2[:].rearrange("p r (u e) i -> p r u e i", e=2),
-                in_=by_slot.unsqueeze(4).to_broadcast([P, B * H, 2, 2, 2]),
+                out=beta1[:].rearrange("p r i (u e) -> p r i u e", e=2),
+                in_=by_slot.unsqueeze(2).to_broadcast([P, B * H, 2, 2, 2]),
             )
 
         xg, xcodes, xscales = {}, {}, {}
@@ -185,9 +184,10 @@ def tile_dpfpattention_pb_w4_kernel(tc, x, wv_words, wv_scales, beta, vo, k_phi_
                         nc.scalar.activation(out=pl[:, t, i, :], in_=src, func=ACT.Copy, scale=kscale[:, t : t + 1])
                 planes[h0 + i] = (pl, i)
 
-        def interleave(h0, nh, engine):
+        def interleave(h0, nh, engine, gate=False):
             on_gpsimd = engine is nc.gpsimd
-            it = work.tile([P, nh, S, PACK], BF16, align_bytes=64, name="inter", tag="inter_g" if on_gpsimd else "inter", bufs=1 if on_gpsimd else 8)
+            gated = on_gpsimd or gate
+            it = work.tile([P, nh, S, PACK], BF16, align_bytes=64, name="inter", tag="inter_g" if gated else "inter", bufs=1 if gated else 8)
             pl, i = planes[h0]
             dst = it[:].rearrange("p h (c i) t -> p h c t i", i=RUN)
             src = pl[:, :, i : i + nh].rearrange("p t h (c i) -> p h c t i", i=RUN)
@@ -214,42 +214,41 @@ def tile_dpfpattention_pb_w4_kernel(tc, x, wv_words, wv_scales, beta, vo, k_phi_
 
         vps, vts, diffs, dvg, dvc, ops = {}, {}, {}, {}, {}, {}
 
-        def first_values(tp):
-            ps = psum.tile([P, 2, 4 * DH], F32, name="diff", bufs=3)
-            for t in range(2):
-                cols = slice(P * (2 * tp + t), P * (2 * tp + t + 1))
-                for g in range(2):
-                    nc.tensor.matmul_mx(
-                        out=ps[:, t, :],
-                        lhsT=xcodes[0, g][:, cols].bitcast(E4M3X4),
-                        lhsT_scale=xscales[0, g][:, cols],
-                        rhs=ww[0][:, g, 0 : 8 * DH].bitcast(E2M1X4),
-                        rhs_scale=wsc[:, g, 0 : 4 * DH],
-                        start=(g == 0),
-                        stop=(g == 1),
-                    )
-            vps["first", tp] = ps
-
-        first_diff = keep.tile([P, 4, DH // RUN, PACK, RUN], F32, align_bytes=64, name="first_diff")
-
-        def first_subtract(tp):
-            for t in range(2):
-                nc.vector.tensor_tensor(
-                    out=first_diff[:, :, :, 2 * tp + t, :],
-                    in0=vps["first", tp][:, t, :].rearrange("p (h c i) -> p h c i", h=4, i=RUN),
-                    in1=vos[0][:, :, 2 * tp + t, :].rearrange("p h (c i) -> p h c i", i=RUN),
-                    op=ALU.subtract,
+        def first_values(t):
+            tag, bufs = ("diff", 3) if t < 3 else ("o", 2)
+            ps = psum.tile([P, 8 * DH], F32, name="first", tag=tag, bufs=bufs)
+            cols = slice(P * t, P * (t + 1))
+            for g in range(2):
+                nc.tensor.matmul_mx(
+                    out=ps[:],
+                    lhsT=xcodes[0, g][:, cols].bitcast(E4M3X4),
+                    lhsT_scale=xscales[0, g][:, cols],
+                    rhs=ww[0][:, g, :].bitcast(E2M1X4),
+                    rhs_scale=wsc[:, g, 0 : 8 * DH],
+                    start=(g == 0),
+                    stop=(g == 1),
                 )
+            vps["first", t] = ps
 
-        def first_scale():
+        first_diff = keep.tile([P, 8, DH // RUN, PACK, RUN], F32, align_bytes=64, name="first_diff")
+
+        def first_subtract(t):
+            nc.vector.tensor_tensor(
+                out=first_diff[:, :, :, t, :],
+                in0=vps["first", t][:].rearrange("p (h c i) -> p h c i", h=8, i=RUN),
+                in1=vos[0][:, :, t, :].rearrange("p h (c i) -> p h c i", i=RUN),
+                op=ALU.subtract,
+            )
+
+        def first_scale(r):
             dg = work.tile([P, 4, DH, PACK], BF16, align_bytes=64, name="dvg", bufs=3)
             nc.vector.tensor_tensor(
                 out=dg[:].rearrange("p h (c i) t -> p h c t i", i=RUN),
-                in0=first_diff[:],
-                in1=beta4[:].unsqueeze(2).to_broadcast([P, 4, DH // RUN, PACK, RUN]),
+                in0=first_diff[:, 4 * r : 4 * r + 4],
+                in1=beta4[:, 4 * r : 4 * r + 4].unsqueeze(2).to_broadcast([P, 4, DH // RUN, PACK, RUN]),
                 op=ALU.mult,
             )
-            dvg[0] = dg
+            dvg[r] = dg
 
         def values(q):
             b, j = divmod(q, H // 2)
@@ -298,9 +297,9 @@ def tile_dpfpattention_pb_w4_kernel(tc, x, wv_words, wv_scales, beta, vo, k_phi_
                 dvg[q // 2] = work.tile([P, 4, DH, PACK], BF16, align_bytes=64, name="dvg", bufs=3)
             heads = slice(2 * (q % 2), 2 * (q % 2) + 2)
             nc.vector.tensor_tensor(
-                out=dvg[q // 2][:, heads].rearrange("p h (c e) t -> p h c t e", e=2),
-                in0=diffs[q][:],
-                in1=beta2[:, 2 * q : 2 * q + 2].unsqueeze(2).to_broadcast([P, 2, DH // 2, PACK, 2]),
+                out=dvg[q // 2][:, heads].rearrange("p h (c e) t -> p h c e t", e=2),
+                in0=diffs[q][:].rearrange("p h c t e -> p h c e t"),
+                in1=beta1[:, 2 * q : 2 * q + 2].unsqueeze(2).to_broadcast([P, 2, DH // 2, 2, PACK]),
                 op=ALU.mult,
             )
 
@@ -311,8 +310,8 @@ def tile_dpfpattention_pb_w4_kernel(tc, x, wv_words, wv_scales, beta, vo, k_phi_
             nc.vector.quantize_mx(out=codes[:].bitcast(E4M3X4), scales=scales[:], in_=dvg[q0 // 2][:, heads].rearrange("p h d t -> p (h d t)"))
             dvc[q0] = (codes, scales)
 
-        def update(q0, nq):
-            ps = psum.tile([P, 2 * nq, 2 * DH], F32, name="o", bufs=2)
+        def update(q0, nq, tag="o", bufs=2):
+            ps = psum.tile([P, 2 * nq, 2 * DH], F32, name="o", tag=tag, bufs=bufs)
             dcodes, dscales = dvc[q0]
             for i in range(2 * nq):
                 kcodes, kscales = kc[2 * q0 + i]
@@ -353,8 +352,8 @@ def tile_dpfpattention_pb_w4_kernel(tc, x, wv_words, wv_scales, beta, vo, k_phi_
         copy_x(0, 0, 0)
         copy_x(0, 0, 1)
         quant_k(0)
-        quant_k(1)
         quant_k(2)
+        quant_k(1)
         widen(4, 2, nc.vector)
         quant_x(0, 0, 0)
         quant_x(0, 0, 1)
@@ -364,96 +363,106 @@ def tile_dpfpattention_pb_w4_kernel(tc, x, wv_words, wv_scales, beta, vo, k_phi_
         copy_x(0, 1, 0)
         copy_x(0, 1, 1)
         first_values(0)
-        quant_x(0, 1, 0)
-        quant_k(4)
-        quant_x(0, 1, 1)
-        widen(7, 1, nc.scalar)
-        widen(10, 1, nc.scalar)
-        widen(11, 1, nc.scalar)
         first_values(1)
-        values(2)
-        values(3)
+        widen(7, 1, nc.vector)
+        quant_k(4)
+        quant_x(0, 1, 0)
         interleave(6, 1, nc.vector)
-        widen(8, 1, nc.vector)
-        interleave(7, 1, nc.vector)
+        quant_x(0, 1, 1)
+        widen(9, 2, nc.scalar)
+        widen(8, 1, nc.scalar)
+        widen(11, 1, nc.scalar)
+        interleave(8, 1, nc.scalar)
+        first_values(2)
+        first_values(3)
+        interleave(7, 1, nc.vector, True)
         quant_k(6)
-        interleave(8, 1, nc.vector)
         quant_k(7)
-        widen(9, 1, nc.vector)
+        interleave(9, 2, nc.gpsimd)
+        first_subtract(0)
+        first_subtract(1)
+        first_subtract(2)
+        first_subtract(3)
+        values(4)
+        copy_values(4)
+        values(5)
+        copy_values(5)
+        widen(12, 2, nc.scalar)
+        turn_x(1, 0)
+        copy_x(1, 0, 0)
+        copy_x(1, 0, 1)
+        lay_vo(4)
+        lay_vo(5)
+        add_values(4)
+        add_values(5)
+        widen(14, 1, nc.scalar)
+        turn_x(1, 1)
+        copy_x(1, 1, 0)
+        copy_x(1, 1, 1)
+        interleave(11, 1, nc.vector)
+        first_scale(0)
         quant_k(8)
-        copy_values(2)
-        copy_values(3)
-        for_gpsimd = [9, 10]
-        for_vector = (11, 1)
-        h0 = 12
-        for r in range(QUADS - 1):
+        quant_dv(0, 2)
+        first_scale(1)
+        quant_k(11)
+        quant_x(1, 0, 0)
+        quant_x(1, 0, 1)
+        values(6)
+        copy_values(6)
+        widen(15, 2, nc.scalar)
+        values(7)
+        update(0, 2)
+        copy_values(7)
+        widen(17, 1, nc.scalar)
+        interleave(12, 2, nc.vector)
+        quant_dv(2, 2)
+        quant_x(1, 1, 0)
+        quant_x(1, 1, 1)
+        quant_k(9)
+        quant_k(12)
+        for_gpsimd = 14
+        for_vector = 15
+        for r in range(2, QUADS - 1):
             q0, q1 = 2 * r, 2 * r + 1
             if q0 + 4 < PAIRS:
                 values(q0 + 4)
                 copy_values(q0 + 4)
-            if r > 0:
-                update(q0 - 2, 2)
-            if r == 1:
-                turn_x(1, 1)
-                copy_x(1, 1, 0)
-                copy_x(1, 1, 1)
+            update(q0 - 2, 2)
             lay_vo(q0 + 2)
-            interleave(for_gpsimd[r], 1, nc.gpsimd)
-            if r == 0:
-                first_subtract(0)
-                first_subtract(1)
-            else:
-                scale_dv(q0)
-                scale_dv(q1)
-                finish(q0 - 2, 2)
+            interleave(for_gpsimd, 1, nc.gpsimd)
+            scale_dv(q0)
+            scale_dv(q1)
+            finish(q0 - 4, 2)
             lay_vo(q1 + 2)
             add_values(q0 + 2)
             add_values(q1 + 2)
-            if r == 0:
-                turn_x(1, 0)
-            widened = (h0, 2)
-            widen(h0, 2, nc.scalar)
-            if r == 0:
-                copy_x(1, 0, 0)
-                copy_x(1, 0, 1)
+            widen(for_vector + 3, 2, nc.scalar)
             if q1 + 4 < PAIRS:
                 values(q1 + 4)
                 copy_values(q1 + 4)
-            h0 = h0 + 2
-            if h0 < B * H:
-                widen(h0, 1, nc.scalar)
-                for_gpsimd.append(h0)
-                h0 = h0 + 1
-            interleave(*for_vector, nc.vector)
-            if r == 0:
-                first_scale()
-                quant_k(for_vector[0])
-            if r > 0:
-                quant_dv(q0, 2)
-            if r == 1:
-                for tp in range(2):
-                    quant_x(1, tp, 0)
-                    quant_x(1, tp, 1)
-            quant_k(for_gpsimd[r])
-            if r > 0:
-                quant_k(for_vector[0])
-            else:
-                quant_dv(0, 2)
-            for_vector = widened
+            if for_vector + 5 < B * H:
+                widen(for_vector + 5, 1, nc.scalar)
+            interleave(for_vector, 2, nc.vector)
+            quant_dv(q0, 2)
+            quant_k(for_gpsimd)
+            quant_k(for_vector)
+            for_gpsimd = for_gpsimd + 3
+            for_vector = for_vector + 3
         q0, q1 = PAIRS - 2, PAIRS - 1
         update(q0 - 2, 2)
-        interleave(for_gpsimd[-1], 1, nc.gpsimd)
-        interleave(for_vector[0], 1, nc.scalar)
+        interleave(for_gpsimd, 1, nc.gpsimd)
+        interleave(for_vector, 1, nc.scalar)
         scale_dv(q0)
+        finish(q0 - 4, 2)
         scale_dv(q1)
-        finish(q0 - 2, 2)
-        interleave(for_vector[0] + 1, 1, nc.vector)
+        interleave(for_vector + 1, 1, nc.vector)
         quant_dv(q0, 1)
-        quant_k(for_gpsimd[-1])
+        quant_k(for_gpsimd)
         update(q0, 1)
         quant_dv(q1, 1)
-        quant_k(for_vector[0])
-        quant_k(for_vector[0] + 1)
-        update(q1, 1)
+        quant_k(for_vector)
+        quant_k(for_vector + 1)
+        update(q1, 1, "turn", 3)
+        finish(q0 - 2, 2)
         finish(q0, 1)
         finish(q1, 1)

@@ -19,8 +19,9 @@ S = 2 * DH
 P = 128
 PACK = 4
 RUN = 4
-PAIRS = B * H // 2
-QUADS = PAIRS // 2
+HEADS = B * H
+PAIRS = HEADS // 2
+FIRST = 8
 FLOPS = 2 * B * N * D * H * DH + 2 * B * H * N * S * DH
 
 
@@ -31,6 +32,11 @@ def tile_dpfpattention_pb_w4_kernel(tc, x, wv_words, wv_scales, beta, vo, k_phi_
         work = ctx.enter_context(tc.tile_pool(name="work", bufs=4))
         psum = ctx.enter_context(tc.psum_pool(name="psum", bufs=2))
         ctx.enter_context(tc.manual_schedule())
+
+        k_heads = k_phi_bytes.rearrange("b h (p t) s -> p (b h) (t s)", t=PACK)
+        vo_heads = vo.rearrange("b h (p t) d -> p (b h) (t d)", t=PACK)
+        w_heads = W.rearrange("b h s d -> s (b h) d")
+        out_heads = out.rearrange("b h s d -> s (b h) d")
 
         kscale = keep.tile([P, PACK], F32, name="kscale")
         ident = keep.tile([P, P], F32, name="ident")
@@ -43,12 +49,17 @@ def tile_dpfpattention_pb_w4_kernel(tc, x, wv_words, wv_scales, beta, vo, k_phi_
         nc.vector.memset(beta_rows[:].bitcast(I32), 0)
         kb, xs, vos, ws, ww = {}, {}, {}, {}, {}
 
-        def load_kphi(first, nh):
-            b, h0 = divmod(first, H)
-            kbt = keep.tile([P, nh, PACK * S], U8, align_bytes=64, name=f"kb_{first}")
-            nc.sync.dma_start(out=kbt[:], in_=k_phi_bytes[b, h0 : h0 + nh].rearrange("h (p t) s -> p h (t s)", t=PACK))
+        def load_kscale():
+            nc.sync.dma_start(out=kscale[:], in_=k_phi_scale.rearrange("a c (p t) f -> p (a c t f)", t=PACK))
+
+        def load_beta():
+            nc.sync.dma_start(out=beta_rows[0:HEADS, :], in_=beta.rearrange("b h n -> (b h) n"))
+
+        def load_kphi(h0, nh):
+            kbt = keep.tile([P, nh, PACK * S], U8, align_bytes=64, name=f"kb_{h0}")
+            nc.sync.dma_start(out=kbt[:], in_=k_heads[:, h0 : h0 + nh, :])
             for i in range(nh):
-                kb[first + i] = kbt[:, i, :]
+                kb[h0 + i] = kbt[:, i, :]
 
         def load_x(b, t0, nt):
             xt = keep.tile([P, nt, D], BF16, align_bytes=64, name=f"x_{b}_{t0}")
@@ -56,20 +67,17 @@ def tile_dpfpattention_pb_w4_kernel(tc, x, wv_words, wv_scales, beta, vo, k_phi_
             for t in range(nt):
                 xs[b, t0 + t] = xt[:, t, :]
 
-        def load_vo(r, nr=1):
-            b, h0 = divmod(4 * r, H)
-            v = keep.tile([P, 4 * nr, PACK, DH], BF16, align_bytes=64, name=f"vo_{r}")
-            nc.sync.dma_start(
-                out=v[:].rearrange("p h t d -> p h (t d)"),
-                in_=vo[b, h0 : h0 + 4 * nr].rearrange("h (p t) d -> p h (t d)", t=PACK),
-            )
-            vos[r] = v
+        def load_vo(h0, nh):
+            v = keep.tile([P, nh, PACK * DH], BF16, align_bytes=64, name=f"vo_{h0}")
+            nc.sync.dma_start(out=v[:], in_=vo_heads[:, h0 : h0 + nh, :])
+            for i in range(0, nh, 2):
+                vos[h0 + i] = (v, i)
 
-        def load_W(r):
-            b, h0 = divmod(4 * r, H)
-            w = keep.tile([P, 4, DH], BF16, align_bytes=64, name=f"W_{r}")
-            nc.sync.dma_start(out=w[:], in_=W[b, h0 : h0 + 4].rearrange("h s d -> s h d"))
-            ws[r] = w
+        def load_W(h0, nh):
+            w = keep.tile([P, nh, DH], BF16, align_bytes=64, name=f"W_{h0}")
+            nc.sync.dma_start(out=w[:], in_=w_heads[:, h0 : h0 + nh, :])
+            for i in range(nh):
+                ws[h0 + i] = (w, i)
 
         def load_weight(half):
             w = keep.tile([P, 2, D], U8, align_bytes=64, name=f"ww_{half}")
@@ -77,53 +85,14 @@ def tile_dpfpattention_pb_w4_kernel(tc, x, wv_words, wv_scales, beta, vo, k_phi_
             ww[half] = w
 
         def load_weight_scales():
-            for q in range(4):
+            for r in range(4):
                 nc.sync.dma_start(
-                    out=wsc[32 * q : 32 * q + 4, :, :].bitcast(I32),
-                    in_=wv_scales[:, 4 * q : 4 * q + 4, :].rearrange("g q n -> q g n").bitcast(I32),
+                    out=wsc[r:P:32, :, :].bitcast(I32),
+                    in_=wv_scales[:, r:16:4, :].rearrange("g q n -> q g n").bitcast(I32),
                 )
 
-        nc.sync.dma_start(out=kscale[:], in_=k_phi_scale.rearrange("a c (p t) f -> p (a c t f)", t=PACK))
-        load_kphi(0, 1)
-        load_kphi(1, 1)
-        load_kphi(2, 2)
-        nc.sync.dma_start(out=beta_rows[0 : B * H, :], in_=beta.rearrange("b h n -> (b h) n"))
-        load_x(0, 0, 1)
-        load_x(0, 1, 1)
-        load_kphi(4, 2)
-        load_x(0, 2, 1)
-        load_x(0, 3, 1)
-        load_kphi(6, 2)
-        load_weight_scales()
-        load_weight(0)
-        load_kphi(8, 4)
-        load_vo(0, 2)
-        load_weight(1)
-        load_kphi(12, 2)
-        load_x(1, 0, 2)
-        load_vo(2)
-        load_kphi(14, 2)
-        load_x(1, 2, 2)
-        load_W(0)
-        load_kphi(16, 4)
-        load_vo(3)
-        load_W(1)
-        load_kphi(20, 4)
-        load_vo(4)
-        load_W(2)
-        load_kphi(24, 4)
-        load_vo(5)
-        load_W(3)
-        load_kphi(28, 4)
-        load_vo(6)
-        load_W(4)
-        load_vo(7)
-        load_W(5)
-        load_W(6)
-        load_W(7)
-
-        beta1 = keep.tile([P, B * H, 2, PACK], BF16, align_bytes=64, name="beta1")
-        beta4 = keep.tile([P, 8, PACK, RUN], BF16, align_bytes=64, name="beta4")
+        beta1 = keep.tile([P, HEADS, 2, PACK], BF16, align_bytes=64, name="beta1")
+        beta4 = keep.tile([P, FIRST, PACK, RUN], BF16, align_bytes=64, name="beta4")
         turned = {}
 
         def turn_beta():
@@ -134,14 +103,14 @@ def tile_dpfpattention_pb_w4_kernel(tc, x, wv_words, wv_scales, beta, vo, k_phi_
             turned["beta"] = bt
 
         def copy_beta():
-            by_slot = turned["beta"][:, :, 0 : B * H].bitcast(BF16).rearrange("p u (r e) -> p r u e", e=2)
+            by_slot = turned["beta"][:, :, 0:HEADS].bitcast(BF16).rearrange("p u (r e) -> p r u e", e=2)
             nc.scalar.copy(
                 out=beta4[:].rearrange("p r (u e) i -> p r u e i", e=2),
-                in_=by_slot[:, 0:8].unsqueeze(4).to_broadcast([P, 8, 2, 2, RUN]),
+                in_=by_slot[:, 0:FIRST].unsqueeze(4).to_broadcast([P, FIRST, 2, 2, RUN]),
             )
             nc.scalar.copy(
                 out=beta1[:].rearrange("p r i (u e) -> p r i u e", e=2),
-                in_=by_slot.unsqueeze(2).to_broadcast([P, B * H, 2, 2, 2]),
+                in_=by_slot.unsqueeze(2).to_broadcast([P, HEADS, 2, 2, 2]),
             )
 
         xg, xcodes, xscales = {}, {}, {}
@@ -149,55 +118,58 @@ def tile_dpfpattention_pb_w4_kernel(tc, x, wv_words, wv_scales, beta, vo, k_phi_
             for g in range(2):
                 xcodes[b, g] = keep.tile([P, N], U32, align_bytes=64, name=f"xc_{b}_{g}")
                 xscales[b, g] = keep.tile([P, N], U8, align_bytes=64, name=f"xsc_{b}_{g}")
+            for tp in range(2):
+                xg[b, tp] = keep.tile([P, 2, 2 * P * PACK], BF16, align_bytes=64, name=f"xg_{b}_{tp}")
 
-        def turn_x(b, tp):
+        def turn_x(b, t):
+            turned[b, t] = psum.tile([P, 2, 2, P], F32, name="turn", bufs=3)
+            words = xs[b, t].bitcast(F32)
             for g in range(2):
-                turned[b, tp, g] = psum.tile([P, 2, 2, P], F32, name="turn", bufs=3)
-            for t in range(2):
-                words = xs[b, 2 * tp + t].bitcast(F32)
-                for g in range(2):
-                    for u in range(2):
-                        nc.tensor.transpose(turned[b, tp, g][:, t, u, :], words[:, 256 * g + u : 256 * (g + 1) : 2], ident[:])
+                for u in range(2):
+                    nc.tensor.transpose(turned[b, t][:, g, u, :], words[:, 256 * g + u : 256 * (g + 1) : 2], ident[:])
 
-        def copy_x(b, tp, g):
-            gt = work.tile([P, 2 * P * PACK], BF16, align_bytes=64, name="xg", bufs=8)
-            nc.scalar.copy(
-                out=gt[:].bitcast(F32).rearrange("p (t r u) -> p t r u", t=2, u=2),
-                in_=turned[b, tp, g][:].rearrange("p t u r -> p t r u"),
-            )
-            xg[b, tp, g] = gt
+        def copy_x(b, t):
+            tp, i = divmod(t, 2)
+            dst = xg[b, tp][:, :, P * PACK * i : P * PACK * (i + 1)].bitcast(F32).rearrange("p g (r u) -> p g r u", u=2)
+            nc.scalar.copy(out=dst, in_=turned[b, t][:].rearrange("p g u r -> p g r u"))
 
         def quant_x(b, tp, g):
             cols = slice(2 * P * tp, 2 * P * (tp + 1))
-            nc.vector.quantize_mx(out=xcodes[b, g][:, cols].bitcast(E4M3X4), scales=xscales[b, g][:, cols], in_=xg[b, tp, g][:])
+            nc.vector.quantize_mx(out=xcodes[b, g][:, cols].bitcast(E4M3X4), scales=xscales[b, g][:, cols], in_=xg[b, tp][:, g, :])
 
         planes, inter, kc = {}, {}, {}
 
-        def widen(h0, nh, engine):
-            pl = work.tile([P, PACK, nh, S], BF16, align_bytes=64, name="planes", bufs=12)
+        def k_group(h0, nh):
+            pl = keep.tile([P, PACK, nh, S], BF16, align_bytes=64, name=f"planes_{h0}")
             for i in range(nh):
-                for t in range(PACK):
-                    src = kb[h0 + i][:, S * t : S * (t + 1)].bitcast(FP8)
+                planes[h0 + i] = (pl, i)
+
+        def widen(h0, nh, engine, t0=0, t1=PACK):
+            for h in range(h0, h0 + nh):
+                pl, i = planes[h]
+                for t in range(t0, t1):
+                    src = kb[h][:, S * t : S * (t + 1)].bitcast(FP8)
                     if engine is nc.vector:
                         nc.vector.tensor_scalar(out=pl[:, t, i, :], in0=src, scalar1=kscale[:, t : t + 1], scalar2=None, op0=ALU.mult)
                     else:
                         nc.scalar.activation(out=pl[:, t, i, :], in_=src, func=ACT.Copy, scale=kscale[:, t : t + 1])
-                planes[h0 + i] = (pl, i)
 
-        def interleave(h0, nh, engine, gate=False):
-            on_gpsimd = engine is nc.gpsimd
-            gated = on_gpsimd or gate
-            it = work.tile([P, nh, S, PACK], BF16, align_bytes=64, name="inter", tag="inter_g" if gated else "inter", bufs=1 if gated else 8)
+        def interleave(h0, nh, engine, gated=False):
+            if gated:
+                it = work.tile([P, nh, S, PACK], BF16, align_bytes=64, name="inter_gated", bufs=1)
+            else:
+                it = keep.tile([P, nh, S, PACK], BF16, align_bytes=64, name=f"inter_{h0}")
             pl, i = planes[h0]
-            dst = it[:].rearrange("p h (c i) t -> p h c t i", i=RUN)
-            src = pl[:, :, i : i + nh].rearrange("p t h (c i) -> p h c t i", i=RUN)
-            if on_gpsimd:
+            if engine is nc.gpsimd:
                 by_column = pl[:, :, i : i + nh].rearrange("p t h s -> p h s t")
                 nc.gpsimd.tensor_scalar(out=it[:], in0=by_column, scalar1=1.0, scalar2=0.0, op0=ALU.mult, op1=ALU.add)
-            elif engine is nc.scalar:
-                nc.scalar.copy(out=dst, in_=src)
             else:
-                nc.vector.tensor_copy(out=dst, in_=src)
+                dst = it[:].rearrange("p h (c i) t -> p h c t i", i=RUN)
+                src = pl[:, :, i : i + nh].rearrange("p t h (c i) -> p h c t i", i=RUN)
+                if engine is nc.scalar:
+                    nc.scalar.copy(out=dst, in_=src)
+                else:
+                    nc.vector.tensor_copy(out=dst, in_=src)
             inter[h0] = (it, nh)
 
         def quant_k(h0):
@@ -216,7 +188,7 @@ def tile_dpfpattention_pb_w4_kernel(tc, x, wv_words, wv_scales, beta, vo, k_phi_
 
         def first_values(t):
             tag, bufs = ("diff", 3) if t < 3 else ("o", 2)
-            ps = psum.tile([P, 8 * DH], F32, name="first", tag=tag, bufs=bufs)
+            ps = psum.tile([P, FIRST * DH], F32, name="first", tag=tag, bufs=bufs)
             cols = slice(P * t, P * (t + 1))
             for g in range(2):
                 nc.tensor.matmul_mx(
@@ -224,31 +196,36 @@ def tile_dpfpattention_pb_w4_kernel(tc, x, wv_words, wv_scales, beta, vo, k_phi_
                     lhsT=xcodes[0, g][:, cols].bitcast(E4M3X4),
                     lhsT_scale=xscales[0, g][:, cols],
                     rhs=ww[0][:, g, :].bitcast(E2M1X4),
-                    rhs_scale=wsc[:, g, 0 : 8 * DH],
+                    rhs_scale=wsc[:, g, 0 : FIRST * DH],
                     start=(g == 0),
                     stop=(g == 1),
                 )
             vps["first", t] = ps
 
-        first_diff = keep.tile([P, 8, DH // RUN, PACK, RUN], F32, align_bytes=64, name="first_diff")
+        first_diff = keep.tile([P, FIRST, DH // RUN, PACK, RUN], F32, align_bytes=64, name="first_diff")
 
         def first_subtract(t):
+            v, i = vos[0]
             nc.vector.tensor_tensor(
                 out=first_diff[:, :, :, t, :],
-                in0=vps["first", t][:].rearrange("p (h c i) -> p h c i", h=8, i=RUN),
-                in1=vos[0][:, :, t, :].rearrange("p h (c i) -> p h c i", i=RUN),
+                in0=vps["first", t][:].rearrange("p (h c i) -> p h c i", h=FIRST, i=RUN),
+                in1=v[:, :, DH * t : DH * (t + 1)].rearrange("p h (c i) -> p h c i", i=RUN),
                 op=ALU.subtract,
             )
 
-        def first_scale(r):
-            dg = work.tile([P, 4, DH, PACK], BF16, align_bytes=64, name="dvg", bufs=3)
+        def dv_group(h0, nh):
+            dg = keep.tile([P, nh, DH, PACK], BF16, align_bytes=64, name=f"dvg_{h0}")
+            for i in range(nh):
+                dvg[h0 + i] = (dg, i)
+
+        def first_scale(h0, nh):
+            dg, i = dvg[h0]
             nc.vector.tensor_tensor(
-                out=dg[:].rearrange("p h (c i) t -> p h c t i", i=RUN),
-                in0=first_diff[:, 4 * r : 4 * r + 4],
-                in1=beta4[:, 4 * r : 4 * r + 4].unsqueeze(2).to_broadcast([P, 4, DH // RUN, PACK, RUN]),
+                out=dg[:, i : i + nh].rearrange("p h (c i) t -> p h c t i", i=RUN),
+                in0=first_diff[:, h0 : h0 + nh],
+                in1=beta4[:, h0 : h0 + nh].unsqueeze(2).to_broadcast([P, nh, DH // RUN, PACK, RUN]),
                 op=ALU.mult,
             )
-            dvg[r] = dg
 
         def values(q):
             b, j = divmod(q, H // 2)
@@ -265,17 +242,21 @@ def tile_dpfpattention_pb_w4_kernel(tc, x, wv_words, wv_scales, beta, vo, k_phi_
                 )
             vps[q] = ps
 
-        def copy_values(q):
-            vt = work.tile([P, PACK, P], F32, align_bytes=64, name="vt", bufs=4)
-            nc.scalar.copy(out=vt[:].rearrange("p t r -> p (t r)"), in_=vps[q][:])
+        def copy_values(q, engine):
+            vt = work.tile([P, N], F32, align_bytes=64, name="vt", bufs=6)
+            if engine is nc.vector:
+                nc.vector.tensor_copy(out=vt[:], in_=vps[q][:])
+            else:
+                nc.scalar.copy(out=vt[:], in_=vps[q][:])
             vts[q] = vt
 
         def lay_vo(q):
             ps = psum.tile([P, 2, DH // 2, PACK, 2], F32, name="diff", bufs=3)
+            v, i = vos[2 * q]
             nc.tensor.matmul(
                 ps[:].rearrange("p h c t e -> p t h c e"),
                 lhsT=minus_ident[:],
-                rhs=vos[q // 2][:, 2 * (q % 2) : 2 * (q % 2) + 2].rearrange("p h t (c e) -> p t h c e", e=2),
+                rhs=v[:, i : i + 2].rearrange("p h (t c e) -> p t h c e", t=PACK, e=2),
                 start=True,
                 stop=False,
             )
@@ -285,7 +266,7 @@ def tile_dpfpattention_pb_w4_kernel(tc, x, wv_words, wv_scales, beta, vo, k_phi_
             for t in range(PACK):
                 nc.tensor.matmul(
                     diffs[q][:, :, :, t, :],
-                    lhsT=vts[q][:, t, :],
+                    lhsT=vts[q][:, P * t : P * (t + 1)],
                     rhs=ident[:],
                     start=False,
                     stop=(t == PACK - 1),
@@ -293,176 +274,241 @@ def tile_dpfpattention_pb_w4_kernel(tc, x, wv_words, wv_scales, beta, vo, k_phi_
                 )
 
         def scale_dv(q):
-            if q % 2 == 0:
-                dvg[q // 2] = work.tile([P, 4, DH, PACK], BF16, align_bytes=64, name="dvg", bufs=3)
-            heads = slice(2 * (q % 2), 2 * (q % 2) + 2)
+            dg, i = dvg[2 * q]
             nc.vector.tensor_tensor(
-                out=dvg[q // 2][:, heads].rearrange("p h (c e) t -> p h c e t", e=2),
+                out=dg[:, i : i + 2].rearrange("p h (c e) t -> p h c e t", e=2),
                 in0=diffs[q][:].rearrange("p h c t e -> p h c e t"),
                 in1=beta1[:, 2 * q : 2 * q + 2].unsqueeze(2).to_broadcast([P, 2, DH // 2, 2, PACK]),
                 op=ALU.mult,
             )
 
-        def quant_dv(q0, nq):
-            codes = work.tile([P, 2 * nq * DH], U32, align_bytes=64, name="dvc", bufs=4)
-            scales = work.tile([P, 2 * nq * DH], U8, align_bytes=64, name="dvsc", bufs=4)
-            heads = slice(2 * (q0 % 2), 2 * (q0 % 2 + nq))
-            nc.vector.quantize_mx(out=codes[:].bitcast(E4M3X4), scales=scales[:], in_=dvg[q0 // 2][:, heads].rearrange("p h d t -> p (h d t)"))
-            dvc[q0] = (codes, scales)
+        def quant_dv(h0, nh):
+            dg, i = dvg[h0]
+            codes = keep.tile([P, nh * DH], U32, align_bytes=64, name=f"dvc_{h0}")
+            scales = keep.tile([P, nh * DH], U8, align_bytes=64, name=f"dvsc_{h0}")
+            nc.vector.quantize_mx(out=codes[:].bitcast(E4M3X4), scales=scales[:], in_=dg[:, i : i + nh].rearrange("p h d t -> p (h d t)"))
+            for j in range(nh):
+                dvc[h0 + j] = (codes[:, DH * j : DH * (j + 1)], scales[:, DH * j : DH * (j + 1)])
 
-        def update(q0, nq, tag="o", bufs=2):
-            ps = psum.tile([P, 2 * nq, 2 * DH], F32, name="o", tag=tag, bufs=bufs)
-            dcodes, dscales = dvc[q0]
-            for i in range(2 * nq):
-                kcodes, kscales = kc[2 * q0 + i]
-                pair = slice(2 * DH * (i // 2), 2 * DH * (i // 2 + 1))
+        def update(h0, nh, tag="o", bufs=2):
+            ps = psum.tile([P, nh, DH], F32, name="o", tag=tag, bufs=bufs)
+            for i in range(nh):
+                kcodes, kscales = kc[h0 + i]
+                dcodes, dscales = dvc[h0 + i]
                 nc.tensor.matmul_mx(
                     out=ps[:, i, :],
                     lhsT=kcodes.bitcast(E4M3X4),
                     lhsT_scale=kscales,
-                    rhs=dcodes[:, pair].bitcast(E4M3X4),
-                    rhs_scale=dscales[:, pair],
+                    rhs=dcodes.bitcast(E4M3X4),
+                    rhs_scale=dscales,
                     start=True,
                     stop=True,
                 )
-            ops[q0] = ps
+            ops[h0] = (ps, nh)
 
-        def finish(q0, nq):
-            b, h0 = divmod(2 * q0, H)
-            ot = work.tile([P, 2 * nq, DH], F32, align_bytes=64, name="ot", bufs=9)
-            own = ops[q0][:].rearrange("p (j i) (k d) -> p j (i k) d", i=2, k=2)[:, :, 0:4:3, :]
-            nc.vector.tensor_tensor(
-                out=ot[:].rearrange("p (j i) d -> p j i d", i=2),
-                in0=own,
-                in1=ws[q0 // 2][:, h0 % 4 : h0 % 4 + 2 * nq, :].rearrange("p (j i) d -> p j i d", i=2),
-                op=ALU.add,
-            )
-            nc.sync.dma_start(out=out[b, h0 : h0 + 2 * nq].rearrange("h s d -> s h d"), in_=ot[:])
+        def finish(h0):
+            ps, nh = ops[h0]
+            w, i = ws[h0]
+            ot = keep.tile([P, nh, DH], F32, align_bytes=64, name=f"ot_{h0}")
+            nc.vector.tensor_tensor(out=ot[:], in0=ps[:], in1=w[:, i : i + nh, :], op=ALU.add)
+            nc.sync.dma_start(out=out_heads[:, h0 : h0 + nh, :], in_=ot[:])
 
+        V, A, G = nc.vector, nc.scalar, nc.gpsimd
 
-        widen(0, 1, nc.vector)
-        widen(1, 1, nc.scalar)
-        widen(2, 2, nc.vector)
-        interleave(0, 1, nc.vector)
-        interleave(1, 1, nc.scalar)
-        interleave(2, 2, nc.vector)
-        turn_beta()
-        copy_beta()
-        turn_x(0, 0)
-        copy_x(0, 0, 0)
-        copy_x(0, 0, 1)
+        load_kscale()
+        load_kphi(0, 1)
+        load_kphi(1, 1)
+        load_kphi(2, 2)
+        load_x(0, 0, 1)
+        load_x(0, 1, 1)
+        load_kphi(4, 2)
+        load_x(0, 2, 1)
+        load_x(0, 3, 1)
+        load_kphi(6, 2)
+        load_x(1, 0, 2)
+        load_kphi(8, 2)
+        load_weight_scales()
+        load_weight(0)
+        load_kphi(10, 2)
+        load_kphi(12, 3)
+        load_x(1, 2, 2)
+        load_vo(0, 8)
+        load_weight(1)
+        load_beta()
+        load_kphi(15, 3)
+        load_vo(8, 6)
+        load_kphi(18, 5)
+        load_vo(14, 6)
+        load_W(0, 8)
+        load_kphi(23, 5)
+        load_vo(20, 6)
+        load_kphi(28, 4)
+        load_W(8, 6)
+        load_vo(26, 6)
+        load_W(14, 6)
+        load_W(20, 6)
+        load_W(26, 6)
+
+        for h0, nh in [(0, 1), (1, 1), (2, 2), (4, 2), (6, 2), (8, 2), (10, 2), (12, 3), (15, 3), (18, 2), (20, 3), (23, 3), (26, 2), (28, 2), (30, 2)]:
+            k_group(h0, nh)
+        dv_group(0, 8)
+        for h0 in range(FIRST, HEADS, 6):
+            dv_group(h0, 6)
+
+        widen(0, 1, V)
+        widen(1, 1, A)
+        widen(2, 1, V)
+        widen(3, 1, A)
+        interleave(0, 1, V)
+        interleave(1, 1, V)
         quant_k(0)
-        quant_k(2)
+        interleave(2, 2, V)
         quant_k(1)
-        widen(4, 2, nc.vector)
+        turn_x(0, 0)
+        copy_x(0, 0)
+        turn_x(0, 1)
+        copy_x(0, 1)
+        widen(4, 1, V)
+        widen(5, 1, A)
+        quant_k(2)
+        turn_x(0, 2)
+        copy_x(0, 2)
+        turn_x(0, 3)
+        copy_x(0, 3)
         quant_x(0, 0, 0)
         quant_x(0, 0, 1)
-        interleave(4, 2, nc.vector)
-        widen(6, 1, nc.scalar)
-        turn_x(0, 1)
-        copy_x(0, 1, 0)
-        copy_x(0, 1, 1)
+        widen(6, 1, V)
+        interleave(4, 2, V)
+        widen(7, 1, A)
+        quant_x(0, 1, 0)
+        quant_k(4)
+        quant_x(0, 1, 1)
+        turn_x(1, 0)
+        turn_x(1, 1)
+        widen(8, 1, V)
+        interleave(6, 2, V)
+        copy_x(1, 0)
+        copy_x(1, 1)
+        widen(9, 1, A)
+        widen(11, 1, A)
         first_values(0)
         first_values(1)
-        widen(7, 1, nc.vector)
-        quant_k(4)
-        quant_x(0, 1, 0)
-        interleave(6, 1, nc.vector)
-        quant_x(0, 1, 1)
-        widen(9, 2, nc.scalar)
-        widen(8, 1, nc.scalar)
-        widen(11, 1, nc.scalar)
-        interleave(8, 1, nc.scalar)
-        first_values(2)
-        first_values(3)
-        interleave(7, 1, nc.vector, True)
+        widen(10, 1, V)
         quant_k(6)
-        quant_k(7)
-        interleave(9, 2, nc.gpsimd)
-        first_subtract(0)
-        first_subtract(1)
-        first_subtract(2)
-        first_subtract(3)
-        values(4)
-        copy_values(4)
-        values(5)
-        copy_values(5)
-        widen(12, 2, nc.scalar)
-        turn_x(1, 0)
-        copy_x(1, 0, 0)
-        copy_x(1, 0, 1)
-        lay_vo(4)
-        lay_vo(5)
-        add_values(4)
-        add_values(5)
-        widen(14, 1, nc.scalar)
-        turn_x(1, 1)
-        copy_x(1, 1, 0)
-        copy_x(1, 1, 1)
-        interleave(11, 1, nc.vector)
-        first_scale(0)
-        quant_k(8)
-        quant_dv(0, 2)
-        first_scale(1)
-        quant_k(11)
+        interleave(8, 2, V)
         quant_x(1, 0, 0)
+        first_values(2)
+        turn_x(1, 2)
+        turn_x(1, 3)
+        first_values(3)
+        widen(12, 3, A)
+        interleave(10, 2, V, True)
+        quant_k(8)
+        quant_k(10)
         quant_x(1, 0, 1)
+        interleave(12, 3, G, True)
+        copy_x(1, 2)
+        copy_x(1, 3)
+        for t in range(PACK):
+            first_subtract(t)
+        values(4)
+        turn_beta()
+        copy_values(4, A)
+        copy_beta()
+        widen(15, 1, A)
+        values(5)
         values(6)
-        copy_values(6)
-        widen(15, 2, nc.scalar)
-        values(7)
-        update(0, 2)
-        copy_values(7)
-        widen(17, 1, nc.scalar)
-        interleave(12, 2, nc.vector)
-        quant_dv(2, 2)
+        copy_values(5, A)
+        copy_values(6, A)
         quant_x(1, 1, 0)
         quant_x(1, 1, 1)
-        quant_k(9)
+        widen(16, 2, A)
+        values(7)
+        values(8)
+        for q in range(4, 7):
+            lay_vo(q)
+        for q in range(4, 7):
+            add_values(q)
+        first_scale(0, 4)
+        first_scale(4, 4)
         quant_k(12)
-        for_gpsimd = 14
-        for_vector = 15
-        for r in range(2, QUADS - 1):
-            q0, q1 = 2 * r, 2 * r + 1
-            if q0 + 4 < PAIRS:
-                values(q0 + 4)
-                copy_values(q0 + 4)
-            update(q0 - 2, 2)
-            lay_vo(q0 + 2)
-            interleave(for_gpsimd, 1, nc.gpsimd)
-            scale_dv(q0)
-            scale_dv(q1)
-            finish(q0 - 4, 2)
-            lay_vo(q1 + 2)
-            add_values(q0 + 2)
-            add_values(q1 + 2)
-            widen(for_vector + 3, 2, nc.scalar)
-            if q1 + 4 < PAIRS:
-                values(q1 + 4)
-                copy_values(q1 + 4)
-            if for_vector + 5 < B * H:
-                widen(for_vector + 5, 1, nc.scalar)
-            interleave(for_vector, 2, nc.vector)
-            quant_dv(q0, 2)
-            quant_k(for_gpsimd)
-            quant_k(for_vector)
-            for_gpsimd = for_gpsimd + 3
-            for_vector = for_vector + 3
-        q0, q1 = PAIRS - 2, PAIRS - 1
-        update(q0 - 2, 2)
-        interleave(for_gpsimd, 1, nc.gpsimd)
-        interleave(for_vector, 1, nc.scalar)
-        scale_dv(q0)
-        finish(q0 - 4, 2)
-        scale_dv(q1)
-        interleave(for_vector + 1, 1, nc.vector)
-        quant_dv(q0, 1)
-        quant_k(for_gpsimd)
-        update(q0, 1)
-        quant_dv(q1, 1)
-        quant_k(for_vector)
-        quant_k(for_vector + 1)
-        update(q1, 1, "turn", 3)
-        finish(q0 - 2, 2)
-        finish(q0, 1)
-        finish(q1, 1)
+        quant_dv(0, 8)
+        copy_values(7, A)
+        copy_values(8, A)
+        values(9)
+        update(0, 8)
+        interleave(15, 3, G, True)
+        widen(19, 1, A)
+        widen(20, 1, A)
+        copy_values(9, A)
+        widen(21, 2, A)
+        for q in range(4, 7):
+            scale_dv(q)
+        finish(0)
+        widen(18, 1, V)
+        values(10)
+        values(11)
+        for q in range(7, 10):
+            lay_vo(q)
+        for q in range(7, 10):
+            add_values(q)
+        quant_dv(8, 6)
+        interleave(18, 2, V)
+        quant_k(15)
+        quant_k(18)
+        copy_values(10, A)
+        copy_values(11, A)
+        update(8, 6)
+        values(12)
+        values(13)
+        interleave(20, 3, G, True)
+        widen(23, 2, A)
+        copy_values(12, A)
+        widen(25, 1, A)
+        copy_values(13, A)
+        for q in range(7, 10):
+            scale_dv(q)
+        finish(8)
+        for q in range(10, 13):
+            lay_vo(q)
+        for q in range(10, 13):
+            add_values(q)
+        quant_dv(14, 4)
+        quant_k(20)
+        quant_dv(18, 2)
+        update(14, 6)
+        values(14)
+        values(15)
+        interleave(23, 3, G, True)
+        widen(26, 2, A)
+        widen(28, 1, A)
+        copy_values(14, A)
+        widen(29, 1, A)
+        copy_values(15, A)
+        for q in range(10, 13):
+            scale_dv(q)
+        finish(14)
+        for q in range(13, 16):
+            lay_vo(q)
+        for q in range(13, 16):
+            add_values(q)
+        interleave(26, 2, V)
+        quant_dv(20, 6)
+        quant_k(23)
+        quant_k(26)
+        update(20, 6)
+        interleave(28, 2, G, True)
+        widen(30, 2, A)
+        interleave(30, 2, A)
+        scale_dv(13)
+        scale_dv(14)
+        finish(20)
+        quant_dv(26, 4)
+        quant_k(28)
+        scale_dv(15)
+        update(26, 4)
+        quant_k(30)
+        quant_dv(30, 2)
+        update(30, 2)
+        finish(26)
+        finish(30)

@@ -184,7 +184,7 @@ def tile_dpfpattention_pb_w4_kernel(tc, x, wv_words, wv_scales, beta, vo, k_phi_
             for i in range(nh):
                 kc[h0 + i] = (codes[:, i, :], scales[:, i, :])
 
-        vps, vts, diffs, dvg, dvc, ops = {}, {}, {}, {}, {}, {}
+        vps, vts, diffs, dvg, ops = {}, {}, {}, {}, {}
 
         def first_values(t):
             tag, bufs = ("diff", 3) if t < 3 else ("o", 2)
@@ -282,35 +282,36 @@ def tile_dpfpattention_pb_w4_kernel(tc, x, wv_words, wv_scales, beta, vo, k_phi_
                 op=ALU.mult,
             )
 
+        dcodes = keep.tile([P, HEADS * DH], U32, align_bytes=64, name="dcodes")
+        dscales = keep.tile([P, HEADS * DH], U8, align_bytes=64, name="dscales")
+
         def quant_dv(h0, nh):
             dg, i = dvg[h0]
-            codes = keep.tile([P, nh * DH], U32, align_bytes=64, name=f"dvc_{h0}")
-            scales = keep.tile([P, nh * DH], U8, align_bytes=64, name=f"dvsc_{h0}")
-            nc.vector.quantize_mx(out=codes[:].bitcast(E4M3X4), scales=scales[:], in_=dg[:, i : i + nh].rearrange("p h d t -> p (h d t)"))
-            for j in range(nh):
-                dvc[h0 + j] = (codes[:, DH * j : DH * (j + 1)], scales[:, DH * j : DH * (j + 1)])
+            cols = slice(DH * h0, DH * (h0 + nh))
+            nc.vector.quantize_mx(out=dcodes[:, cols].bitcast(E4M3X4), scales=dscales[:, cols], in_=dg[:, i : i + nh].rearrange("p h d t -> p (h d t)"))
 
-        def update(h0, nh, tag="o", bufs=2):
-            ps = psum.tile([P, nh, DH], F32, name="o", tag=tag, bufs=bufs)
-            for i in range(nh):
-                kcodes, kscales = kc[h0 + i]
-                dcodes, dscales = dvc[h0 + i]
+        def update(h0, nh):
+            spare = 0 if h0 == 0 else 1
+            ps = psum.tile([P, (spare + nh) * DH], F32, name="o", bufs=2)
+            for h in reversed(range(h0, h0 + nh)):
+                kcodes, kscales = kc[h]
+                first = max(h - 1, 0)
                 nc.tensor.matmul_mx(
-                    out=ps[:, i, :],
+                    out=ps[:, DH * (first - h0 + spare) : DH * (h + 1 - h0 + spare)],
                     lhsT=kcodes.bitcast(E4M3X4),
                     lhsT_scale=kscales,
-                    rhs=dcodes.bitcast(E4M3X4),
-                    rhs_scale=dscales,
+                    rhs=dcodes[:, DH * first : DH * (h + 1)].bitcast(E4M3X4),
+                    rhs_scale=dscales[:, DH * first : DH * (h + 1)],
                     start=True,
                     stop=True,
                 )
-            ops[h0] = (ps, nh)
+            ops[h0] = (ps[:, spare * DH :].rearrange("p (h d) -> p h d", d=DH), nh)
 
         def finish(h0):
             ps, nh = ops[h0]
             w, i = ws[h0]
             ot = keep.tile([P, nh, DH], F32, align_bytes=64, name=f"ot_{h0}")
-            nc.vector.tensor_tensor(out=ot[:], in0=ps[:], in1=w[:, i : i + nh, :], op=ALU.add)
+            nc.vector.tensor_tensor(out=ot[:], in0=ps, in1=w[:, i : i + nh, :], op=ALU.add)
             nc.sync.dma_start(out=out_heads[:, h0 : h0 + nh, :], in_=ot[:])
 
         V, A, G = nc.vector, nc.scalar, nc.gpsimd
@@ -324,6 +325,7 @@ def tile_dpfpattention_pb_w4_kernel(tc, x, wv_words, wv_scales, beta, vo, k_phi_
         load_kphi(4, 2)
         load_x(0, 2, 1)
         load_x(0, 3, 1)
+        load_beta()
         load_kphi(6, 2)
         load_x(1, 0, 2)
         load_kphi(8, 2)
@@ -333,9 +335,9 @@ def tile_dpfpattention_pb_w4_kernel(tc, x, wv_words, wv_scales, beta, vo, k_phi_
         load_kphi(12, 3)
         load_x(1, 2, 2)
         load_vo(0, 8)
+        load_kphi(15, 1)
         load_weight(1)
-        load_beta()
-        load_kphi(15, 3)
+        load_kphi(16, 2)
         load_vo(8, 6)
         load_kphi(18, 5)
         load_vo(14, 6)
@@ -383,6 +385,8 @@ def tile_dpfpattention_pb_w4_kernel(tc, x, wv_words, wv_scales, beta, vo, k_phi_
         quant_x(0, 1, 0)
         quant_k(4)
         quant_x(0, 1, 1)
+        turn_beta()
+        copy_beta()
         turn_x(1, 0)
         turn_x(1, 1)
         widen(8, 1, V)
@@ -409,20 +413,18 @@ def tile_dpfpattention_pb_w4_kernel(tc, x, wv_words, wv_scales, beta, vo, k_phi_
         interleave(12, 3, G, True)
         copy_x(1, 2)
         copy_x(1, 3)
+        widen(15, 1, A)
         for t in range(PACK):
             first_subtract(t)
         values(4)
-        turn_beta()
-        copy_values(4, A)
-        copy_beta()
-        widen(15, 1, A)
         values(5)
         values(6)
+        copy_values(4, A)
         copy_values(5, A)
         copy_values(6, A)
         quant_x(1, 1, 0)
         quant_x(1, 1, 1)
-        widen(16, 2, A)
+        widen(16, 3, A)
         values(7)
         values(8)
         for q in range(4, 7):
@@ -445,7 +447,6 @@ def tile_dpfpattention_pb_w4_kernel(tc, x, wv_words, wv_scales, beta, vo, k_phi_
         for q in range(4, 7):
             scale_dv(q)
         finish(0)
-        widen(18, 1, V)
         values(10)
         values(11)
         for q in range(7, 10):

@@ -394,22 +394,20 @@ def tile_dpfpattention_pb_w4_kernel(tc, x, wv_words, wv_scales, beta, vo, k_phi_
         copy_x(1, 0)
         copy_x(1, 1)
         widen(9, 1, A)
-        widen(11, 1, A)
         first_values(0)
         first_values(1)
-        widen(10, 1, V)
+        widen(10, 2, V)
         quant_k(6)
-        interleave(8, 2, V)
+        interleave(8, 2, V, True)
         quant_x(1, 0, 0)
         first_values(2)
         turn_x(1, 2)
         turn_x(1, 3)
         first_values(3)
         widen(12, 3, A)
-        interleave(10, 2, V, True)
-        quant_k(8)
-        quant_k(10)
         quant_x(1, 0, 1)
+        quant_k(8)
+        interleave(10, 2, V)
         interleave(12, 3, G, True)
         copy_x(1, 2)
         copy_x(1, 3)
@@ -424,6 +422,7 @@ def tile_dpfpattention_pb_w4_kernel(tc, x, wv_words, wv_scales, beta, vo, k_phi_
         copy_values(6, A)
         quant_x(1, 1, 0)
         quant_x(1, 1, 1)
+        quant_k(10)
         widen(16, 3, A)
         values(7)
         values(8)
@@ -438,32 +437,31 @@ def tile_dpfpattention_pb_w4_kernel(tc, x, wv_words, wv_scales, beta, vo, k_phi_
         copy_values(7, A)
         copy_values(8, A)
         values(9)
+        values(10)
         update(0, 8)
         interleave(15, 3, G, True)
         widen(19, 1, A)
         widen(20, 1, A)
         copy_values(9, A)
-        widen(21, 2, A)
+        widen(21, 3, A)
         for q in range(4, 7):
             scale_dv(q)
         finish(0)
-        values(10)
         values(11)
         for q in range(7, 10):
             lay_vo(q)
         for q in range(7, 10):
             add_values(q)
         quant_dv(8, 6)
-        interleave(18, 2, V)
         quant_k(15)
-        quant_k(18)
+        interleave(18, 2, V)
         copy_values(10, A)
         copy_values(11, A)
-        update(8, 6)
         values(12)
+        update(8, 6)
         values(13)
         interleave(20, 3, G, True)
-        widen(23, 2, A)
+        widen(24, 1, A)
         copy_values(12, A)
         widen(25, 1, A)
         copy_values(13, A)
@@ -474,11 +472,11 @@ def tile_dpfpattention_pb_w4_kernel(tc, x, wv_words, wv_scales, beta, vo, k_phi_
             lay_vo(q)
         for q in range(10, 13):
             add_values(q)
-        quant_dv(14, 4)
+        quant_k(18)
         quant_k(20)
-        quant_dv(18, 2)
-        update(14, 6)
+        quant_dv(14, 6)
         values(14)
+        update(14, 6)
         values(15)
         interleave(23, 3, G, True)
         widen(26, 2, A)
@@ -491,19 +489,20 @@ def tile_dpfpattention_pb_w4_kernel(tc, x, wv_words, wv_scales, beta, vo, k_phi_
         finish(14)
         for q in range(13, 16):
             lay_vo(q)
-        for q in range(13, 16):
-            add_values(q)
-        interleave(26, 2, V)
+        add_values(13)
+        add_values(14)
         quant_dv(20, 6)
         quant_k(23)
-        quant_k(26)
+        interleave(26, 2, V)
         update(20, 6)
+        add_values(15)
         interleave(28, 2, G, True)
         widen(30, 2, A)
         interleave(30, 2, A)
         scale_dv(13)
         scale_dv(14)
         finish(20)
+        quant_k(26)
         quant_dv(26, 4)
         quant_k(28)
         scale_dv(15)

@@ -47,6 +47,8 @@ def tile_dpfpattention_pb_w4_kernel(tc, x, wv_words, wv_scales, beta, vo, k_phi_
         nc.gpsimd.memset(wsc[:].rearrange("p g n -> p (g n)").bitcast(I32), 0)
         beta_rows = keep.tile([P, N], BF16, align_bytes=64, name="beta_rows")
         nc.vector.memset(beta_rows[:].bitcast(I32), 0)
+        zeros = keep.tile([P, 2 * P], F32, name="zeros")
+        nc.vector.memset(zeros[:], 0.0)
         kb, xs, vos, ws, ww = {}, {}, {}, {}, {}
 
         def load_kscale():
@@ -314,6 +316,10 @@ def tile_dpfpattention_pb_w4_kernel(tc, x, wv_words, wv_scales, beta, vo, k_phi_
             nc.vector.tensor_tensor(out=ot[:], in0=ps, in1=w[:, i : i + nh, :], op=ALU.add)
             nc.sync.dma_start(out=out_heads[:, h0 : h0 + nh, :], in_=ot[:])
 
+        def warm_up():
+            ps = psum.tile([P, 2 * P], F32, name="o", bufs=2)
+            nc.tensor.matmul(ps[:], lhsT=zeros[:, 0:P], rhs=zeros[:], start=True, stop=True)
+
         V, A, G = nc.vector, nc.scalar, nc.gpsimd
 
         load_kscale()
@@ -366,6 +372,8 @@ def tile_dpfpattention_pb_w4_kernel(tc, x, wv_words, wv_scales, beta, vo, k_phi_
         quant_k(0)
         interleave(2, 2, V)
         quant_k(1)
+        warm_up()
+        warm_up()
         turn_x(0, 0)
         copy_x(0, 0)
         turn_x(0, 1)
@@ -373,6 +381,7 @@ def tile_dpfpattention_pb_w4_kernel(tc, x, wv_words, wv_scales, beta, vo, k_phi_
         widen(4, 1, V)
         widen(5, 1, A)
         quant_k(2)
+        warm_up()
         turn_x(0, 2)
         copy_x(0, 2)
         turn_x(0, 3)
@@ -385,6 +394,7 @@ def tile_dpfpattention_pb_w4_kernel(tc, x, wv_words, wv_scales, beta, vo, k_phi_
         quant_x(0, 1, 0)
         quant_k(4)
         quant_x(0, 1, 1)
+        warm_up()
         turn_beta()
         copy_beta()
         turn_x(1, 0)

@@ -43,8 +43,10 @@ def tile_dpfpattention_pb_w4_kernel(tc, x, wv_words, wv_scales, beta, vo, k_phi_
         make_identity(nc, ident[:])
         minus_ident = keep.tile([P, P], BF16, name="minus_ident")
         nc.scalar.activation(out=minus_ident[:], in_=ident[:], func=ACT.Copy, scale=-1.0)
-        wsc = keep.tile([P, 2, D], U8, align_bytes=64, name="wsc")
-        nc.gpsimd.memset(wsc[:].rearrange("p g n -> p (g n)").bitcast(I32), 0)
+        wsc = {}
+        for half in range(2):
+            wsc[half] = keep.tile([P, 2, N], U8, align_bytes=64, name=f"wsc_{half}")
+            nc.gpsimd.memset(wsc[half][:].rearrange("p g n -> p (g n)").bitcast(I32), 0)
         beta_rows = keep.tile([P, N], BF16, align_bytes=64, name="beta_rows")
         nc.vector.memset(beta_rows[:].bitcast(I32), 0)
         zeros = keep.tile([P, 2 * P], F32, name="zeros")
@@ -86,11 +88,12 @@ def tile_dpfpattention_pb_w4_kernel(tc, x, wv_words, wv_scales, beta, vo, k_phi_
             nc.sync.dma_start(out=w[:], in_=wv_words[:, :, D * half : D * (half + 1)].rearrange("g p n -> p g n"))
             ww[half] = w
 
-        def load_weight_scales():
+        def load_weight_scales(half):
+            cols = slice(N * half, N * (half + 1))
             for r in range(4):
                 nc.sync.dma_start(
-                    out=wsc[r:P:32, :, :].bitcast(I32),
-                    in_=wv_scales[:, r:16:4, :].rearrange("g q n -> q g n").bitcast(I32),
+                    out=wsc[half][r:P:32, :, :].bitcast(I32),
+                    in_=wv_scales[:, r:16:4, cols].rearrange("g q n -> q g n").bitcast(I32),
                 )
 
         beta1 = keep.tile([P, HEADS, 2, PACK], BF16, align_bytes=64, name="beta1")
@@ -198,7 +201,7 @@ def tile_dpfpattention_pb_w4_kernel(tc, x, wv_words, wv_scales, beta, vo, k_phi_
                     lhsT=xcodes[0, g][:, cols].bitcast(E4M3X4),
                     lhsT_scale=xscales[0, g][:, cols],
                     rhs=ww[0][:, g, :].bitcast(E2M1X4),
-                    rhs_scale=wsc[:, g, 0 : FIRST * DH],
+                    rhs_scale=wsc[0][:, g, :],
                     start=(g == 0),
                     stop=(g == 1),
                 )
@@ -206,11 +209,11 @@ def tile_dpfpattention_pb_w4_kernel(tc, x, wv_words, wv_scales, beta, vo, k_phi_
 
         first_diff = keep.tile([P, FIRST, DH // RUN, PACK, RUN], F32, align_bytes=64, name="first_diff")
 
-        def first_subtract(t):
-            v, i = vos[0]
+        def first_subtract(h0, nh, t):
+            v, i = vos[h0]
             nc.vector.tensor_tensor(
-                out=first_diff[:, :, :, t, :],
-                in0=vps["first", t][:].rearrange("p (h c i) -> p h c i", h=FIRST, i=RUN),
+                out=first_diff[:, h0 : h0 + nh, :, t, :],
+                in0=vps["first", t][:, DH * h0 : DH * (h0 + nh)].rearrange("p (h c i) -> p h c i", h=nh, i=RUN),
                 in1=v[:, :, DH * t : DH * (t + 1)].rearrange("p h (c i) -> p h c i", i=RUN),
                 op=ALU.subtract,
             )
@@ -229,14 +232,14 @@ def tile_dpfpattention_pb_w4_kernel(tc, x, wv_words, wv_scales, beta, vo, k_phi_
                 op=ALU.mult,
             )
 
-        def values(q):
+        def values(q, tag="turn", bufs=3):
             b, j = divmod(q, H // 2)
-            ps = psum.tile([P, N], F32, name="turn", bufs=3)
+            ps = psum.tile([P, N], F32, name="values", tag=tag, bufs=bufs)
             for g in range(2):
                 nc.tensor.matmul_mx(
                     out=ps[:],
                     lhsT=ww[j // 4][:, g, 2 * P * (j % 4) : 2 * P * (j % 4 + 1)].bitcast(E2M1X4),
-                    lhsT_scale=wsc[:, g, P * j : P * (j + 1)],
+                    lhsT_scale=wsc[j // 4][:, g, P * (j % 4) : P * (j % 4 + 1)],
                     rhs=xcodes[b, g][:].bitcast(E4M3X4),
                     rhs_scale=xscales[b, g][:],
                     start=(g == 0),
@@ -244,13 +247,14 @@ def tile_dpfpattention_pb_w4_kernel(tc, x, wv_words, wv_scales, beta, vo, k_phi_
                 )
             vps[q] = ps
 
-        def copy_values(q, engine):
-            vt = work.tile([P, N], F32, align_bytes=64, name="vt", bufs=6)
+        def copy_values(q, engine, t0=0, t1=PACK):
+            if q not in vts:
+                vts[q] = work.tile([P, N], F32, align_bytes=64, name="vt", bufs=6)
+            cols = slice(P * t0, P * t1)
             if engine is nc.vector:
-                nc.vector.tensor_copy(out=vt[:], in_=vps[q][:])
+                nc.vector.tensor_copy(out=vts[q][:, cols], in_=vps[q][:, cols])
             else:
-                nc.scalar.copy(out=vt[:], in_=vps[q][:])
-            vts[q] = vt
+                nc.scalar.copy(out=vts[q][:, cols], in_=vps[q][:, cols])
 
         def lay_vo(q):
             ps = psum.tile([P, 2, DH // 2, PACK, 2], F32, name="diff", bufs=3)
@@ -323,27 +327,27 @@ def tile_dpfpattention_pb_w4_kernel(tc, x, wv_words, wv_scales, beta, vo, k_phi_
         V, A, G = nc.vector, nc.scalar, nc.gpsimd
 
         load_kscale()
-        load_kphi(0, 1)
-        load_kphi(1, 1)
+        load_kphi(0, 2)
         load_kphi(2, 2)
         load_x(0, 0, 1)
-        load_x(0, 1, 1)
         load_kphi(4, 2)
+        load_x(0, 1, 1)
         load_x(0, 2, 1)
         load_x(0, 3, 1)
-        load_beta()
         load_kphi(6, 2)
+        load_beta()
         load_x(1, 0, 2)
         load_kphi(8, 2)
-        load_weight_scales()
+        load_weight_scales(0)
         load_weight(0)
         load_kphi(10, 2)
         load_kphi(12, 3)
         load_x(1, 2, 2)
-        load_vo(0, 8)
-        load_kphi(15, 1)
+        load_vo(0, 4)
+        load_weight_scales(1)
         load_weight(1)
-        load_kphi(16, 2)
+        load_vo(4, 4)
+        load_kphi(15, 3)
         load_vo(8, 6)
         load_kphi(18, 5)
         load_vo(14, 6)
@@ -357,42 +361,33 @@ def tile_dpfpattention_pb_w4_kernel(tc, x, wv_words, wv_scales, beta, vo, k_phi_
         load_W(20, 6)
         load_W(26, 6)
 
-        for h0, nh in [(0, 1), (1, 1), (2, 2), (4, 2), (6, 2), (8, 2), (10, 2), (12, 3), (15, 3), (18, 2), (20, 3), (23, 3), (26, 2), (28, 2), (30, 2)]:
+        for h0, nh in [(0, 2), (2, 2), (4, 2), (6, 2), (8, 2), (10, 2), (12, 3), (15, 3), (18, 2), (20, 3), (23, 3), (26, 2), (28, 2), (30, 2)]:
             k_group(h0, nh)
         dv_group(0, 8)
         for h0 in range(FIRST, HEADS, 6):
             dv_group(h0, 6)
 
-        widen(0, 1, V)
-        widen(1, 1, A)
-        widen(2, 1, V)
-        widen(3, 1, A)
-        interleave(0, 1, V)
-        interleave(1, 1, V)
-        quant_k(0)
+        widen(0, 3, V)
+        widen(3, 3, A)
+        interleave(0, 2, V)
         interleave(2, 2, V)
-        quant_k(1)
+        quant_k(0)
+        quant_k(2)
         warm_up()
         warm_up()
         turn_x(0, 0)
         copy_x(0, 0)
-        turn_x(0, 1)
-        copy_x(0, 1)
-        widen(4, 1, V)
-        widen(5, 1, A)
-        quant_k(2)
         warm_up()
-        turn_x(0, 2)
-        copy_x(0, 2)
-        turn_x(0, 3)
-        copy_x(0, 3)
+        for t in range(1, PACK):
+            turn_x(0, t)
+            copy_x(0, t)
+        interleave(4, 2, V)
+        widen(6, 1, V)
         quant_x(0, 0, 0)
         quant_x(0, 0, 1)
-        widen(6, 1, V)
-        interleave(4, 2, V)
         widen(7, 1, A)
-        quant_x(0, 1, 0)
         quant_k(4)
+        quant_x(0, 1, 0)
         quant_x(0, 1, 1)
         warm_up()
         turn_beta()
@@ -411,9 +406,9 @@ def tile_dpfpattention_pb_w4_kernel(tc, x, wv_words, wv_scales, beta, vo, k_phi_
         interleave(8, 2, V, True)
         quant_x(1, 0, 0)
         first_values(2)
+        first_values(3)
         turn_x(1, 2)
         turn_x(1, 3)
-        first_values(3)
         widen(12, 3, A)
         quant_x(1, 0, 1)
         quant_k(8)
@@ -421,9 +416,9 @@ def tile_dpfpattention_pb_w4_kernel(tc, x, wv_words, wv_scales, beta, vo, k_phi_
         interleave(12, 3, G, True)
         copy_x(1, 2)
         copy_x(1, 3)
-        widen(15, 1, A)
-        for t in range(PACK):
-            first_subtract(t)
+        for h0 in range(0, FIRST, 4):
+            for t in range(PACK):
+                first_subtract(h0, 4, t)
         values(4)
         values(5)
         values(6)
@@ -433,7 +428,7 @@ def tile_dpfpattention_pb_w4_kernel(tc, x, wv_words, wv_scales, beta, vo, k_phi_
         quant_x(1, 1, 0)
         quant_x(1, 1, 1)
         quant_k(10)
-        widen(16, 3, A)
+        widen(15, 4, A)
         values(7)
         values(8)
         for q in range(4, 7):
@@ -456,8 +451,9 @@ def tile_dpfpattention_pb_w4_kernel(tc, x, wv_words, wv_scales, beta, vo, k_phi_
         widen(21, 3, A)
         for q in range(4, 7):
             scale_dv(q)
-        finish(0)
         values(11)
+        finish(0)
+        copy_values(11, V, 0, 1)
         for q in range(7, 10):
             lay_vo(q)
         for q in range(7, 10):
@@ -466,7 +462,7 @@ def tile_dpfpattention_pb_w4_kernel(tc, x, wv_words, wv_scales, beta, vo, k_phi_
         quant_k(15)
         interleave(18, 2, V)
         copy_values(10, A)
-        copy_values(11, A)
+        copy_values(11, A, 1, 4)
         values(12)
         update(8, 6)
         values(13)
@@ -474,10 +470,10 @@ def tile_dpfpattention_pb_w4_kernel(tc, x, wv_words, wv_scales, beta, vo, k_phi_
         widen(24, 1, A)
         copy_values(12, A)
         widen(25, 1, A)
-        copy_values(13, A)
         for q in range(7, 10):
             scale_dv(q)
         finish(8)
+        copy_values(13, V, 0, 2)
         for q in range(10, 13):
             lay_vo(q)
         for q in range(10, 13):
@@ -485,36 +481,35 @@ def tile_dpfpattention_pb_w4_kernel(tc, x, wv_words, wv_scales, beta, vo, k_phi_
         quant_k(18)
         quant_k(20)
         quant_dv(14, 6)
+        copy_values(13, A, 2, 4)
         values(14)
         update(14, 6)
         values(15)
         interleave(23, 3, G, True)
-        widen(26, 2, A)
-        widen(28, 1, A)
+        widen(26, 3, A)
         copy_values(14, A)
-        widen(29, 1, A)
-        copy_values(15, A)
+        widen(29, 3, A)
+        interleave(26, 2, A)
         for q in range(10, 13):
             scale_dv(q)
         finish(14)
+        copy_values(15, V)
         for q in range(13, 16):
             lay_vo(q)
-        add_values(13)
-        add_values(14)
-        quant_dv(20, 6)
+        for q in range(13, 16):
+            add_values(q)
+        quant_dv(20, 2)
         quant_k(23)
-        interleave(26, 2, V)
+        quant_dv(22, 4)
         update(20, 6)
-        add_values(15)
         interleave(28, 2, G, True)
-        widen(30, 2, A)
         interleave(30, 2, A)
         scale_dv(13)
         scale_dv(14)
         finish(20)
-        quant_k(26)
         quant_dv(26, 4)
         quant_k(28)
+        quant_k(26)
         scale_dv(15)
         update(26, 4)
         quant_k(30)

@@ -165,16 +165,15 @@ def tile_dpfpattention_pb_w4_kernel(tc, x, wv_words, wv_scales, beta, vo, k_phi_
             else:
                 it = keep.tile([P, nh, S, PACK], BF16, align_bytes=64, name=f"inter_{h0}")
             pl, i = planes[h0]
+            by_column = pl[:, :, i : i + nh].rearrange("p t h s -> p h s t")
             if engine is nc.gpsimd:
-                by_column = pl[:, :, i : i + nh].rearrange("p t h s -> p h s t")
                 nc.gpsimd.tensor_scalar(out=it[:], in0=by_column, scalar1=1.0, scalar2=0.0, op0=ALU.mult, op1=ALU.add)
+            elif engine is nc.scalar:
+                nc.scalar.copy(out=it[:], in_=by_column)
             else:
                 dst = it[:].rearrange("p h (c i) t -> p h c t i", i=RUN)
                 src = pl[:, :, i : i + nh].rearrange("p t h (c i) -> p h c t i", i=RUN)
-                if engine is nc.scalar:
-                    nc.scalar.copy(out=dst, in_=src)
-                else:
-                    nc.vector.tensor_copy(out=dst, in_=src)
+                nc.vector.tensor_copy(out=dst, in_=src)
             inter[h0] = (it, nh)
 
         def quant_k(h0):

@@ -452,7 +452,6 @@ def tile_dpfpattention_pb_w4_kernel(tc, x, wv_words, wv_scales, beta, vo, k_phi_
             scale_dv(q)
         values(11)
         finish(0)
-        copy_values(11, V, 0, 1)
         for q in range(7, 10):
             lay_vo(q)
         for q in range(7, 10):
@@ -461,7 +460,7 @@ def tile_dpfpattention_pb_w4_kernel(tc, x, wv_words, wv_scales, beta, vo, k_phi_
         quant_k(15)
         interleave(18, 2, V)
         copy_values(10, A)
-        copy_values(11, A, 1, 4)
+        copy_values(11, A)
         values(12)
         update(8, 6)
         values(13)
@@ -493,14 +492,16 @@ def tile_dpfpattention_pb_w4_kernel(tc, x, wv_words, wv_scales, beta, vo, k_phi_
             scale_dv(q)
         finish(14)
         copy_values(15, V)
-        for q in range(13, 16):
-            lay_vo(q)
-        for q in range(13, 16):
-            add_values(q)
+        lay_vo(13)
+        lay_vo(14)
+        add_values(13)
+        add_values(14)
         quant_dv(20, 2)
         quant_k(23)
         quant_dv(22, 4)
         update(20, 6)
+        lay_vo(15)
+        add_values(15)
         interleave(28, 2, G, True)
         interleave(30, 2, A)
         scale_dv(13)

@@ -20,7 +20,6 @@ P = 128
 PACK = 4
 RUN = 4
 HEADS = B * H
-PAIRS = HEADS // 2
 FIRST = 8
 FLOPS = 2 * B * N * D * H * DH + 2 * B * H * N * S * DH
 
@@ -30,7 +29,7 @@ def tile_dpfpattention_pb_w4_kernel(tc, x, wv_words, wv_scales, beta, vo, k_phi_
     with ExitStack() as ctx:
         keep = ctx.enter_context(tc.tile_pool(name="keep", bufs=1))
         work = ctx.enter_context(tc.tile_pool(name="work", bufs=4))
-        psum = ctx.enter_context(tc.psum_pool(name="psum", bufs=2))
+        psum = ctx.enter_context(tc.psum_pool(name="psum", bufs=1))
         ctx.enter_context(tc.manual_schedule())
 
         k_heads = k_phi_bytes.rearrange("b h (p t) s -> p (b h) (t s)", t=PACK)
@@ -38,11 +37,12 @@ def tile_dpfpattention_pb_w4_kernel(tc, x, wv_words, wv_scales, beta, vo, k_phi_
         w_heads = W.rearrange("b h s d -> s (b h) d")
         out_heads = out.rearrange("b h s d -> s (b h) d")
 
+        def bank(i, shape):
+            return psum.tile([P] + shape, F32, name="bank", tag=f"bank_{i}", bufs=1)
+
         kscale = keep.tile([P, PACK], F32, name="kscale")
         ident = keep.tile([P, P], F32, name="ident")
         make_identity(nc, ident[:])
-        minus_ident = keep.tile([P, P], BF16, name="minus_ident")
-        nc.scalar.activation(out=minus_ident[:], in_=ident[:], func=ACT.Copy, scale=-1.0)
         wsc = {}
         for half in range(2):
             wsc[half] = keep.tile([P, 2, N], U8, align_bytes=64, name=f"wsc_{half}")
@@ -51,6 +51,8 @@ def tile_dpfpattention_pb_w4_kernel(tc, x, wv_words, wv_scales, beta, vo, k_phi_
         nc.vector.memset(beta_rows[:].bitcast(I32), 0)
         zeros = keep.tile([P, 2 * P], F32, name="zeros")
         nc.vector.memset(zeros[:], 0.0)
+        minus_ident = keep.tile([P, P], BF16, name="minus_ident")
+        nc.scalar.activation(out=minus_ident[:], in_=ident[:], func=ACT.Copy, scale=-1.0)
         kb, xs, vos, ws, ww = {}, {}, {}, {}, {}
 
         def load_kscale():
@@ -60,10 +62,10 @@ def tile_dpfpattention_pb_w4_kernel(tc, x, wv_words, wv_scales, beta, vo, k_phi_
             nc.sync.dma_start(out=beta_rows[0:HEADS, :], in_=beta.rearrange("b h n -> (b h) n"))
 
         def load_kphi(h0, nh):
-            kbt = keep.tile([P, nh, PACK * S], U8, align_bytes=64, name=f"kb_{h0}")
-            nc.sync.dma_start(out=kbt[:], in_=k_heads[:, h0 : h0 + nh, :])
+            kbt = keep.tile([P, nh * PACK * S], U8, align_bytes=64, name=f"kb_{h0}")
+            nc.sync.dma_start(out=kbt[:].rearrange("p (h c) -> p h c", h=nh), in_=k_heads[:, h0 : h0 + nh, :])
             for i in range(nh):
-                kb[h0 + i] = kbt[:, i, :]
+                kb[h0 + i] = (kbt, i)
 
         def load_x(b, t0, nt):
             xt = keep.tile([P, nt, D], BF16, align_bytes=64, name=f"x_{b}_{t0}")
@@ -96,38 +98,27 @@ def tile_dpfpattention_pb_w4_kernel(tc, x, wv_words, wv_scales, beta, vo, k_phi_
                     in_=wv_scales[:, r:16:4, cols].rearrange("g q n -> q g n").bitcast(I32),
                 )
 
-        beta1 = keep.tile([P, HEADS, 2, PACK], BF16, align_bytes=64, name="beta1")
-        beta4 = keep.tile([P, FIRST, PACK, RUN], BF16, align_bytes=64, name="beta4")
+        beta2 = keep.tile([P, HEADS - FIRST, 2, PACK], BF16, align_bytes=64, name="beta2")
         turned = {}
 
-        def turn_beta():
-            bt = psum.tile([P, 2, P], F32, name="turn", bufs=3)
+        def turn_beta(i):
+            bt = bank(i, [P, 2])
             words = beta_rows[:].bitcast(F32)
             for u in range(2):
-                nc.tensor.transpose(bt[:, u, :], words[:, u : 2 * P : 2], ident[:])
-            turned["beta"] = bt
+                nc.tensor.transpose(bt[:, :, u], words[:, u : 2 * P : 2], ident[:])
+            turned["beta"] = bt[:].rearrange("p r u -> p (r u)").bitcast(BF16).rearrange("p (r t) -> p r t", t=PACK)
 
         def copy_beta():
-            by_slot = turned["beta"][:, :, 0:HEADS].bitcast(BF16).rearrange("p u (r e) -> p r u e", e=2)
-            nc.scalar.copy(
-                out=beta4[:].rearrange("p r (u e) i -> p r u e i", e=2),
-                in_=by_slot[:, 0:FIRST].unsqueeze(4).to_broadcast([P, FIRST, 2, 2, RUN]),
-            )
-            nc.scalar.copy(
-                out=beta1[:].rearrange("p r i (u e) -> p r i u e", e=2),
-                in_=by_slot.unsqueeze(2).to_broadcast([P, HEADS, 2, 2, 2]),
-            )
+            nc.scalar.copy(out=beta2[:], in_=turned["beta"][:, FIRST:HEADS].unsqueeze(2).to_broadcast([P, HEADS - FIRST, 2, PACK]))
 
         xg, xcodes, xscales = {}, {}, {}
         for b in range(B):
             for g in range(2):
                 xcodes[b, g] = keep.tile([P, N], U32, align_bytes=64, name=f"xc_{b}_{g}")
                 xscales[b, g] = keep.tile([P, N], U8, align_bytes=64, name=f"xsc_{b}_{g}")
-            for tp in range(2):
-                xg[b, tp] = keep.tile([P, 2, 2 * P * PACK], BF16, align_bytes=64, name=f"xg_{b}_{tp}")
 
-        def turn_x(b, t):
-            turned[b, t] = psum.tile([P, 2, 2, P], F32, name="turn", bufs=3)
+        def turn_x(b, t, i):
+            turned[b, t] = bank(i, [2, 2, P])
             words = xs[b, t].bitcast(F32)
             for g in range(2):
                 for u in range(2):
@@ -135,32 +126,53 @@ def tile_dpfpattention_pb_w4_kernel(tc, x, wv_words, wv_scales, beta, vo, k_phi_
 
         def copy_x(b, t):
             tp, i = divmod(t, 2)
+            if i == 0:
+                xg[b, tp] = work.tile([P, 2, 2 * P * PACK], BF16, align_bytes=64, name="xg", bufs=3)
             dst = xg[b, tp][:, :, P * PACK * i : P * PACK * (i + 1)].bitcast(F32).rearrange("p g (r u) -> p g r u", u=2)
             nc.scalar.copy(out=dst, in_=turned[b, t][:].rearrange("p g u r -> p g r u"))
 
-        def quant_x(b, tp, g):
+        def quant_x(b, tp):
             cols = slice(2 * P * tp, 2 * P * (tp + 1))
-            nc.vector.quantize_mx(out=xcodes[b, g][:, cols].bitcast(E4M3X4), scales=xscales[b, g][:, cols], in_=xg[b, tp][:, g, :])
+            for g in range(2):
+                nc.vector.quantize_mx(out=xcodes[b, g][:, cols].bitcast(E4M3X4), scales=xscales[b, g][:, cols], in_=xg[b, tp][:, g, :])
 
-        planes, inter, kc = {}, {}, {}
+        casts, planes, members, inter, kc = {}, {}, {}, {}, {}
 
-        def k_group(h0, nh):
-            pl = keep.tile([P, PACK, nh, S], BF16, align_bytes=64, name=f"planes_{h0}")
-            for i in range(nh):
-                planes[h0 + i] = (pl, i)
+        def k_group(heads):
+            pl = keep.tile([P, PACK, len(heads), S], BF16, align_bytes=64, name=f"planes_{heads[0]}")
+            for i, h in enumerate(heads):
+                planes[h] = (pl, i)
+                members[h] = heads
 
-        def widen(h0, nh, engine, t0=0, t1=PACK):
+        def widen_k(h0, nh, engine):
             for h in range(h0, h0 + nh):
+                kbt, j = kb[h]
                 pl, i = planes[h]
-                for t in range(t0, t1):
-                    src = kb[h][:, S * t : S * (t + 1)].bitcast(FP8)
+                for t in range(PACK):
+                    src = kbt[:, S * (PACK * j + t) : S * (PACK * j + t + 1)].bitcast(FP8)
                     if engine is nc.vector:
                         nc.vector.tensor_scalar(out=pl[:, t, i, :], in0=src, scalar1=kscale[:, t : t + 1], scalar2=None, op0=ALU.mult)
                     else:
                         nc.scalar.activation(out=pl[:, t, i, :], in_=src, func=ACT.Copy, scale=kscale[:, t : t + 1])
 
-        def interleave(h0, nh, engine, gated=False):
-            if gated:
+        def cast_k(h0, nh):
+            kbt, j = kb[h0]
+            if h0 not in casts:
+                heads = members[h0][planes[h0][1] :]
+                tile = work.tile([P, len(heads), PACK, S], BF16, align_bytes=64, name="cast", bufs=3)
+                for i, h in enumerate(heads):
+                    casts[h] = (tile, i)
+            cast, i = casts[h0]
+            nc.scalar.copy(out=cast[:, i : i + nh].rearrange("p h t s -> p (h t s)"), in_=kbt[:, PACK * S * j : PACK * S * (j + nh)].bitcast(FP8))
+
+        def scale_k(h0, nh):
+            cast, j = casts[h0]
+            pl, i = planes[h0]
+            for t in range(PACK):
+                nc.vector.tensor_scalar(out=pl[:, t, i : i + nh], in0=cast[:, j : j + nh, t, :], scalar1=kscale[:, t : t + 1], scalar2=None, op0=ALU.mult)
+
+        def interleave(h0, nh, engine):
+            if engine is nc.gpsimd:
                 it = work.tile([P, nh, S, PACK], BF16, align_bytes=64, name="inter_gated", bufs=1)
             else:
                 it = keep.tile([P, nh, S, PACK], BF16, align_bytes=64, name=f"inter_{h0}")
@@ -174,46 +186,49 @@ def tile_dpfpattention_pb_w4_kernel(tc, x, wv_words, wv_scales, beta, vo, k_phi_
                 dst = it[:].rearrange("p h (c i) t -> p h c t i", i=RUN)
                 src = pl[:, :, i : i + nh].rearrange("p t h (c i) -> p h c t i", i=RUN)
                 nc.vector.tensor_copy(out=dst, in_=src)
-            inter[h0] = (it, nh)
+            for j in range(nh):
+                inter[members[h0][i + j]] = (it, j)
 
-        def quant_k(h0):
-            it, nh = inter[h0]
+        def quant_k(h0, nh):
+            it, j = inter[h0]
             codes = keep.tile([P, nh, S], U32, align_bytes=64, name=f"kc_{h0}")
             scales = keep.tile([P, nh, S], U8, align_bytes=64, name=f"ksc_{h0}")
             nc.vector.quantize_mx(
                 out=codes[:].rearrange("p h s -> p (h s)").bitcast(E4M3X4),
                 scales=scales[:].rearrange("p h s -> p (h s)"),
-                in_=it[:].rearrange("p h s t -> p (h s t)"),
+                in_=it[:, j : j + nh].rearrange("p h s t -> p (h s t)"),
             )
+            first = planes[h0][1]
             for i in range(nh):
-                kc[h0 + i] = (codes[:, i, :], scales[:, i, :])
+                kc[members[h0][first + i]] = (codes[:, i, :], scales[:, i, :])
 
         vps, vts, diffs, dvg, ops = {}, {}, {}, {}, {}
 
-        def first_values(t):
-            tag, bufs = ("diff", 3) if t < 3 else ("o", 2)
-            ps = psum.tile([P, FIRST * DH], F32, name="first", tag=tag, bufs=bufs)
+        def first_values(h0, t, i):
+            b, half = divmod(h0 // 8, 2)
+            ps = bank(i, [8 * DH])
             cols = slice(P * t, P * (t + 1))
             for g in range(2):
                 nc.tensor.matmul_mx(
                     out=ps[:],
-                    lhsT=xcodes[0, g][:, cols].bitcast(E4M3X4),
-                    lhsT_scale=xscales[0, g][:, cols],
-                    rhs=ww[0][:, g, :].bitcast(E2M1X4),
-                    rhs_scale=wsc[0][:, g, :],
+                    lhsT=xcodes[b, g][:, cols].bitcast(E4M3X4),
+                    lhsT_scale=xscales[b, g][:, cols],
+                    rhs=ww[half][:, g, :].bitcast(E2M1X4),
+                    rhs_scale=wsc[half][:, g, :],
                     start=(g == 0),
                     stop=(g == 1),
                 )
-            vps["first", t] = ps
+            vps["first", h0, t] = ps
 
         first_diff = keep.tile([P, FIRST, DH // RUN, PACK, RUN], F32, align_bytes=64, name="first_diff")
 
         def first_subtract(h0, nh, t):
             v, i = vos[h0]
+            j = h0 % 8
             nc.vector.tensor_tensor(
                 out=first_diff[:, h0 : h0 + nh, :, t, :],
-                in0=vps["first", t][:, DH * h0 : DH * (h0 + nh)].rearrange("p (h c i) -> p h c i", h=nh, i=RUN),
-                in1=v[:, :, DH * t : DH * (t + 1)].rearrange("p h (c i) -> p h c i", i=RUN),
+                in0=vps["first", h0 - j, t][:, DH * j : DH * (j + nh)].rearrange("p (h c i) -> p h c i", h=nh, i=RUN),
+                in1=v[:, i : i + nh, DH * t : DH * (t + 1)].rearrange("p h (c i) -> p h c i", i=RUN),
                 op=ALU.subtract,
             )
 
@@ -223,17 +238,18 @@ def tile_dpfpattention_pb_w4_kernel(tc, x, wv_words, wv_scales, beta, vo, k_phi_
                 dvg[h0 + i] = (dg, i)
 
         def first_scale(h0, nh):
-            dg, i = dvg[h0]
-            nc.vector.tensor_tensor(
-                out=dg[:, i : i + nh].rearrange("p h (c i) t -> p h c t i", i=RUN),
-                in0=first_diff[:, h0 : h0 + nh],
-                in1=beta4[:, h0 : h0 + nh].unsqueeze(2).to_broadcast([P, nh, DH // RUN, PACK, RUN]),
-                op=ALU.mult,
-            )
+            for h in range(h0, h0 + nh):
+                dg, i = dvg[h]
+                nc.vector.tensor_tensor(
+                    out=dg[:, i].rearrange("p (c i) t -> p c t i", i=RUN),
+                    in0=first_diff[:, h],
+                    in1=turned["beta"][:, h].unsqueeze(1).unsqueeze(3).to_broadcast([P, DH // RUN, PACK, RUN]),
+                    op=ALU.mult,
+                )
 
-        def values(q, tag="turn", bufs=3):
+        def values(q, i):
             b, j = divmod(q, H // 2)
-            ps = psum.tile([P, N], F32, name="values", tag=tag, bufs=bufs)
+            ps = bank(i, [N])
             for g in range(2):
                 nc.tensor.matmul_mx(
                     out=ps[:],
@@ -246,22 +262,17 @@ def tile_dpfpattention_pb_w4_kernel(tc, x, wv_words, wv_scales, beta, vo, k_phi_
                 )
             vps[q] = ps
 
-        def copy_values(q, engine, t0=0, t1=PACK):
-            if q not in vts:
-                vts[q] = work.tile([P, N], F32, align_bytes=64, name="vt", bufs=6)
-            cols = slice(P * t0, P * t1)
-            if engine is nc.vector:
-                nc.vector.tensor_copy(out=vts[q][:, cols], in_=vps[q][:, cols])
-            else:
-                nc.scalar.copy(out=vts[q][:, cols], in_=vps[q][:, cols])
+        def copy_values(q):
+            vts[q] = work.tile([P, N], F32, align_bytes=64, name="vt", bufs=6)
+            nc.scalar.copy(out=vts[q][:], in_=vps[q][:])
 
-        def lay_vo(q):
-            ps = psum.tile([P, 2, DH // 2, PACK, 2], F32, name="diff", bufs=3)
-            v, i = vos[2 * q]
+        def lay_vo(q, i):
+            ps = bank(i, [2, DH // 2, PACK, 2])
+            v, j = vos[2 * q]
             nc.tensor.matmul(
                 ps[:].rearrange("p h c t e -> p t h c e"),
                 lhsT=minus_ident[:],
-                rhs=v[:, i : i + 2].rearrange("p h (t c e) -> p t h c e", t=PACK, e=2),
+                rhs=v[:, j : j + 2].rearrange("p h (t c e) -> p t h c e", t=PACK, e=2),
                 start=True,
                 stop=False,
             )
@@ -283,7 +294,7 @@ def tile_dpfpattention_pb_w4_kernel(tc, x, wv_words, wv_scales, beta, vo, k_phi_
             nc.vector.tensor_tensor(
                 out=dg[:, i : i + 2].rearrange("p h (c e) t -> p h c e t", e=2),
                 in0=diffs[q][:].rearrange("p h c t e -> p h c e t"),
-                in1=beta1[:, 2 * q : 2 * q + 2].unsqueeze(2).to_broadcast([P, 2, DH // 2, 2, PACK]),
+                in1=beta2[:, 2 * q - FIRST : 2 * q - FIRST + 2].unsqueeze(2).to_broadcast([P, 2, DH // 2, 2, PACK]),
                 op=ALU.mult,
             )
 
@@ -295,14 +306,13 @@ def tile_dpfpattention_pb_w4_kernel(tc, x, wv_words, wv_scales, beta, vo, k_phi_
             cols = slice(DH * h0, DH * (h0 + nh))
             nc.vector.quantize_mx(out=dcodes[:, cols].bitcast(E4M3X4), scales=dscales[:, cols], in_=dg[:, i : i + nh].rearrange("p h d t -> p (h d t)"))
 
-        def update(h0, nh):
-            spare = 0 if h0 == 0 else 1
-            ps = psum.tile([P, (spare + nh) * DH], F32, name="o", bufs=2)
+        def update(h0, nh, i):
+            ps = bank(i, [nh * DH])
             for h in reversed(range(h0, h0 + nh)):
                 kcodes, kscales = kc[h]
-                first = max(h - 1, 0)
+                first = max(h - 1, h0)
                 nc.tensor.matmul_mx(
-                    out=ps[:, DH * (first - h0 + spare) : DH * (h + 1 - h0 + spare)],
+                    out=ps[:, DH * (first - h0) : DH * (h + 1 - h0)],
                     lhsT=kcodes.bitcast(E4M3X4),
                     lhsT_scale=kscales,
                     rhs=dcodes[:, DH * first : DH * (h + 1)].bitcast(E4M3X4),
@@ -310,7 +320,7 @@ def tile_dpfpattention_pb_w4_kernel(tc, x, wv_words, wv_scales, beta, vo, k_phi_
                     start=True,
                     stop=True,
                 )
-            ops[h0] = (ps[:, spare * DH :].rearrange("p (h d) -> p h d", d=DH), nh)
+            ops[h0] = (ps[:].rearrange("p (h d) -> p h d", d=DH), nh)
 
         def finish(h0):
             ps, nh = ops[h0]
@@ -319,201 +329,186 @@ def tile_dpfpattention_pb_w4_kernel(tc, x, wv_words, wv_scales, beta, vo, k_phi_
             nc.vector.tensor_tensor(out=ot[:], in0=ps, in1=w[:, i : i + nh, :], op=ALU.add)
             nc.sync.dma_start(out=out_heads[:, h0 : h0 + nh, :], in_=ot[:])
 
-        def warm_up():
-            ps = psum.tile([P, 2 * P], F32, name="o", bufs=2)
+        def warm_up(i):
+            ps = bank(i, [2 * P])
             nc.tensor.matmul(ps[:], lhsT=zeros[:, 0:P], rhs=zeros[:], start=True, stop=True)
 
         V, A, G = nc.vector, nc.scalar, nc.gpsimd
 
         load_kscale()
         load_kphi(0, 2)
-        load_kphi(2, 2)
         load_x(0, 0, 1)
-        load_kphi(4, 2)
+        load_kphi(2, 2)
         load_x(0, 1, 1)
+        load_kphi(4, 2)
         load_x(0, 2, 1)
         load_x(0, 3, 1)
-        load_kphi(6, 2)
+        load_kphi(6, 6)
         load_beta()
-        load_x(1, 0, 2)
-        load_kphi(8, 2)
         load_weight_scales(0)
         load_weight(0)
-        load_kphi(10, 2)
-        load_kphi(12, 3)
-        load_x(1, 2, 2)
         load_vo(0, 4)
+        load_vo(4, 4)
         load_weight_scales(1)
         load_weight(1)
-        load_vo(4, 4)
-        load_kphi(15, 3)
+        load_x(1, 0, 2)
+        load_x(1, 2, 2)
+        load_kphi(12, 6)
         load_vo(8, 6)
-        load_kphi(18, 5)
-        load_vo(14, 6)
+        load_kphi(18, 6)
         load_W(0, 8)
-        load_kphi(23, 5)
-        load_vo(20, 6)
-        load_kphi(28, 4)
+        load_vo(14, 6)
+        load_kphi(24, 8)
         load_W(8, 6)
+        load_vo(20, 6)
         load_vo(26, 6)
         load_W(14, 6)
         load_W(20, 6)
         load_W(26, 6)
 
-        for h0, nh in [(0, 2), (2, 2), (4, 2), (6, 2), (8, 2), (10, 2), (12, 3), (15, 3), (18, 2), (20, 3), (23, 3), (26, 2), (28, 2), (30, 2)]:
-            k_group(h0, nh)
         dv_group(0, 8)
         for h0 in range(FIRST, HEADS, 6):
             dv_group(h0, 6)
 
-        widen(0, 3, V)
-        widen(3, 3, A)
-        interleave(0, 2, V)
-        interleave(2, 2, V)
-        quant_k(0)
-        quant_k(2)
-        warm_up()
-        warm_up()
-        turn_x(0, 0)
+        for h0, nh in [(0, 2), (2, 2), (4, 2), (6, 6), (12, 6), (18, 6), (24, 8)]:
+            k_group(list(range(h0, h0 + nh)))
+
+        widen_k(0, 2, V)
+        warm_up(6)
+        warm_up(7)
+        turn_x(0, 0, 0)
+        cast_k(2, 2)
         copy_x(0, 0)
-        warm_up()
-        for t in range(1, PACK):
-            turn_x(0, t)
-            copy_x(0, t)
+        warm_up(6)
+        turn_x(0, 1, 1)
+        cast_k(4, 2)
+        copy_x(0, 1)
+        turn_x(0, 2, 2)
+        turn_x(0, 3, 3)
+        copy_x(0, 2)
+        copy_x(0, 3)
+        interleave(0, 2, V)
+        scale_k(2, 2)
+        quant_k(0, 2)
+        interleave(2, 2, V)
+        scale_k(4, 2)
+        quant_x(0, 0)
         interleave(4, 2, V)
-        widen(6, 1, V)
-        quant_x(0, 0, 0)
-        quant_x(0, 0, 1)
-        widen(7, 1, A)
-        quant_k(4)
-        quant_x(0, 1, 0)
-        quant_x(0, 1, 1)
-        warm_up()
-        turn_beta()
+        cast_k(6, 2)
+        cast_k(8, 4)
+        quant_k(2, 2)
+        quant_x(0, 1)
+        scale_k(6, 2)
+        quant_k(4, 2)
+        scale_k(8, 4)
+        turn_beta(7)
+        warm_up(6)
         copy_beta()
-        turn_x(1, 0)
-        turn_x(1, 1)
-        widen(8, 1, V)
-        interleave(6, 2, V)
-        copy_x(1, 0)
-        copy_x(1, 1)
-        widen(9, 1, A)
-        first_values(0)
-        first_values(1)
-        widen(10, 2, V)
-        quant_k(6)
-        interleave(8, 2, V, True)
-        quant_x(1, 0, 0)
-        first_values(2)
-        first_values(3)
-        turn_x(1, 2)
-        turn_x(1, 3)
-        widen(12, 3, A)
-        quant_x(1, 0, 1)
-        quant_k(8)
-        interleave(10, 2, V)
-        interleave(12, 3, G, True)
-        copy_x(1, 2)
-        copy_x(1, 3)
+        for t in range(PACK):
+            first_values(0, t, 3 + t)
+        interleave(6, 6, G)
         for h0 in range(0, FIRST, 4):
             for t in range(PACK):
                 first_subtract(h0, 4, t)
-        values(4)
-        values(5)
-        values(6)
-        copy_values(4, A)
-        copy_values(5, A)
-        copy_values(6, A)
-        quant_x(1, 1, 0)
-        quant_x(1, 1, 1)
-        quant_k(10)
-        widen(15, 4, A)
-        values(7)
-        values(8)
+        first_scale(0, 8)
         for q in range(4, 7):
-            lay_vo(q)
+            values(q, q - 4)
+            copy_values(q)
+        turn_x(1, 0, 3)
+        turn_x(1, 1, 4)
+        copy_x(1, 0)
+        copy_x(1, 1)
+        cast_k(12, 6)
+        turn_x(1, 2, 5)
+        turn_x(1, 3, 6)
+        copy_x(1, 2)
+        copy_x(1, 3)
+        values(7, 0)
+        copy_values(7)
+        for q in range(4, 7):
+            lay_vo(q, q - 1)
         for q in range(4, 7):
             add_values(q)
-        first_scale(0, 4)
-        first_scale(4, 4)
-        quant_k(12)
+        quant_k(6, 4)
+        quant_x(1, 0)
+        scale_k(12, 6)
+        quant_x(1, 1)
+        quant_k(10, 2)
         quant_dv(0, 8)
-        copy_values(7, A)
-        copy_values(8, A)
-        values(9)
-        values(10)
-        update(0, 8)
-        interleave(15, 3, G, True)
-        widen(19, 1, A)
-        widen(20, 1, A)
-        copy_values(9, A)
-        widen(21, 3, A)
+        cast_k(18, 6)
+        values(8, 1)
+        values(9, 2)
+        update(0, 8, 6)
+        values(10, 0)
+        copy_values(8)
+        copy_values(9)
+        copy_values(10)
+        interleave(12, 3, G)
         for q in range(4, 7):
             scale_dv(q)
-        values(11)
         finish(0)
         for q in range(7, 10):
-            lay_vo(q)
+            lay_vo(q, q - 4)
         for q in range(7, 10):
             add_values(q)
+        scale_k(18, 6)
+        quant_k(12, 3)
         quant_dv(8, 6)
-        quant_k(15)
-        interleave(18, 2, V)
-        copy_values(10, A)
-        copy_values(11, A)
-        values(12)
-        update(8, 6)
-        values(13)
-        interleave(20, 3, G, True)
-        widen(24, 1, A)
-        copy_values(12, A)
-        widen(25, 1, A)
+        cast_k(24, 4)
+        cast_k(28, 4)
+        values(11, 1)
+        values(12, 2)
+        update(8, 6, 7)
+        values(13, 0)
+        copy_values(11)
+        copy_values(12)
+        interleave(18, 2, A)
+        interleave(15, 3, G)
         for q in range(7, 10):
             scale_dv(q)
         finish(8)
-        copy_values(13, V, 0, 2)
         for q in range(10, 13):
-            lay_vo(q)
+            lay_vo(q, q - 7)
         for q in range(10, 13):
             add_values(q)
-        quant_k(18)
-        quant_k(20)
+        scale_k(24, 8)
+        quant_k(18, 2)
+        quant_k(15, 3)
         quant_dv(14, 6)
-        copy_values(13, A, 2, 4)
-        values(14)
-        update(14, 6)
-        values(15)
-        interleave(23, 3, G, True)
-        widen(26, 3, A)
-        copy_values(14, A)
-        widen(29, 3, A)
-        interleave(26, 2, A)
+        copy_values(13)
+        interleave(23, 1, A)
+        values(14, 1)
+        values(15, 2)
+        update(14, 6, 6)
+        interleave(24, 2, A)
+        copy_values(14)
+        copy_values(15)
+        interleave(20, 3, G)
         for q in range(10, 13):
             scale_dv(q)
         finish(14)
-        copy_values(15, V)
-        lay_vo(13)
-        lay_vo(14)
-        add_values(13)
-        add_values(14)
-        quant_dv(20, 2)
-        quant_k(23)
-        quant_dv(22, 4)
-        update(20, 6)
-        lay_vo(15)
-        add_values(15)
-        interleave(28, 2, G, True)
+        for q in range(13, 16):
+            lay_vo(q, q - 10)
+        for q in range(13, 16):
+            add_values(q)
+        interleave(28, 2, A)
         interleave(30, 2, A)
+        quant_k(23, 1)
+        quant_k(24, 2)
+        quant_k(20, 3)
+        quant_dv(20, 6)
+        update(20, 6, 7)
+        interleave(26, 2, G)
         scale_dv(13)
         scale_dv(14)
         finish(20)
         quant_dv(26, 4)
-        quant_k(28)
-        quant_k(26)
+        quant_k(28, 2)
+        quant_k(26, 2)
         scale_dv(15)
-        update(26, 4)
-        quant_k(30)
+        update(26, 4, 6)
+        quant_k(30, 2)
         quant_dv(30, 2)
-        update(30, 2)
+        update(30, 2, 7)
         finish(26)
         finish(30)

@@ -171,8 +171,8 @@ def tile_dpfpattention_pb_w4_kernel(tc, x, wv_words, wv_scales, beta, vo, k_phi_
             for t in range(PACK):
                 nc.vector.tensor_scalar(out=pl[:, t, i : i + nh], in0=cast[:, j : j + nh, t, :], scalar1=kscale[:, t : t + 1], scalar2=None, op0=ALU.mult)
 
-        def interleave(h0, nh, engine):
-            if engine is nc.gpsimd:
+        def interleave(h0, nh, engine, gated=False):
+            if gated:
                 it = work.tile([P, nh, S, PACK], BF16, align_bytes=64, name="inter_gated", bufs=1)
             else:
                 it = keep.tile([P, nh, S, PACK], BF16, align_bytes=64, name=f"inter_{h0}")
@@ -337,30 +337,33 @@ def tile_dpfpattention_pb_w4_kernel(tc, x, wv_words, wv_scales, beta, vo, k_phi_
 
         load_kscale()
         load_kphi(0, 2)
-        load_x(0, 0, 1)
         load_kphi(2, 2)
-        load_x(0, 1, 1)
+        load_x(0, 0, 1)
         load_kphi(4, 2)
+        load_x(0, 1, 1)
         load_x(0, 2, 1)
         load_x(0, 3, 1)
-        load_kphi(6, 6)
+        load_kphi(6, 2)
         load_beta()
+        load_x(1, 0, 2)
+        load_kphi(8, 2)
         load_weight_scales(0)
         load_weight(0)
+        load_kphi(10, 4)
         load_vo(0, 4)
-        load_vo(4, 4)
         load_weight_scales(1)
         load_weight(1)
-        load_x(1, 0, 2)
         load_x(1, 2, 2)
-        load_kphi(12, 6)
+        load_vo(4, 4)
+        load_kphi(14, 4)
         load_vo(8, 6)
-        load_kphi(18, 6)
-        load_W(0, 8)
+        load_kphi(18, 4)
         load_vo(14, 6)
-        load_kphi(24, 8)
-        load_W(8, 6)
+        load_kphi(22, 4)
+        load_W(0, 8)
+        load_kphi(26, 6)
         load_vo(20, 6)
+        load_W(8, 6)
         load_vo(26, 6)
         load_W(14, 6)
         load_W(20, 6)
@@ -369,81 +372,84 @@ def tile_dpfpattention_pb_w4_kernel(tc, x, wv_words, wv_scales, beta, vo, k_phi_
         dv_group(0, 8)
         for h0 in range(FIRST, HEADS, 6):
             dv_group(h0, 6)
-
-        for h0, nh in [(0, 2), (2, 2), (4, 2), (6, 6), (12, 6), (18, 6), (24, 8)]:
+        for h0, nh in [(0, 2), (2, 2), (4, 2), (6, 2), (8, 6), (14, 6), (20, 6), (26, 6)]:
             k_group(list(range(h0, h0 + nh)))
 
-        widen_k(0, 2, V)
+        widen_k(0, 4, V)
         warm_up(6)
-        warm_up(7)
         turn_x(0, 0, 0)
-        cast_k(2, 2)
+        cast_k(4, 2)
         copy_x(0, 0)
         warm_up(6)
         turn_x(0, 1, 1)
-        cast_k(4, 2)
         copy_x(0, 1)
         turn_x(0, 2, 2)
         turn_x(0, 3, 3)
         copy_x(0, 2)
         copy_x(0, 3)
         interleave(0, 2, V)
-        scale_k(2, 2)
-        quant_k(0, 2)
         interleave(2, 2, V)
+        quant_k(0, 2)
         scale_k(4, 2)
-        quant_x(0, 0)
-        interleave(4, 2, V)
-        cast_k(6, 2)
-        cast_k(8, 4)
         quant_k(2, 2)
-        quant_x(0, 1)
-        scale_k(6, 2)
-        quant_k(4, 2)
-        scale_k(8, 4)
-        turn_beta(7)
+        interleave(4, 2, V)
+        quant_x(0, 0)
         warm_up(6)
+        turn_beta(7)
+        turn_x(1, 0, 0)
+        turn_x(1, 1, 1)
+        cast_k(6, 2)
         copy_beta()
-        for t in range(PACK):
-            first_values(0, t, 3 + t)
-        interleave(6, 6, G)
-        for h0 in range(0, FIRST, 4):
-            for t in range(PACK):
-                first_subtract(h0, 4, t)
-        first_scale(0, 8)
-        for q in range(4, 7):
-            values(q, q - 4)
-            copy_values(q)
-        turn_x(1, 0, 3)
-        turn_x(1, 1, 4)
         copy_x(1, 0)
         copy_x(1, 1)
-        cast_k(12, 6)
-        turn_x(1, 2, 5)
-        turn_x(1, 3, 6)
+        warm_up(6)
+        cast_k(8, 2)
+        widen_k(10, 4, A)
+        quant_k(4, 2)
+        quant_x(0, 1)
+        scale_k(6, 2)
+        interleave(6, 2, V, True)
+        quant_x(1, 0)
+        scale_k(8, 2)
+        quant_k(6, 2)
+        for t in range(PACK):
+            first_values(0, t, 3 + t)
+        interleave(8, 3, G, True)
+        interleave(11, 3, G)
+        for h0 in range(0, FIRST, 4):
+            for h in range(h0, h0 + 4, 2):
+                for t in range(PACK):
+                    first_subtract(h, 2, t)
+            first_scale(h0, 4)
+        for q in range(4, 7):
+            values(q, (q - 4) % 3)
+            copy_values(q)
+        turn_x(1, 2, 0)
+        turn_x(1, 3, 1)
         copy_x(1, 2)
         copy_x(1, 3)
-        values(7, 0)
-        copy_values(7)
+        values(7, 2)
+        cast_k(14, 4)
         for q in range(4, 7):
             lay_vo(q, q - 1)
         for q in range(4, 7):
             add_values(q)
-        quant_k(6, 4)
-        quant_x(1, 0)
-        scale_k(12, 6)
         quant_x(1, 1)
-        quant_k(10, 2)
+        quant_k(11, 3)
+        scale_k(14, 4)
+        quant_k(8, 3)
         quant_dv(0, 8)
-        cast_k(18, 6)
-        values(8, 1)
-        values(9, 2)
+        copy_values(7)
+        widen_k(18, 2, A)
+        values(8, 0)
+        values(9, 1)
         update(0, 8, 6)
-        values(10, 0)
+        values(10, 2)
         copy_values(8)
         copy_values(9)
-        copy_values(10)
-        interleave(12, 3, G)
+        cast_k(22, 4)
+        widen_k(20, 2, A)
+        interleave(14, 3, G, True)
         for q in range(4, 7):
             scale_dv(q)
         finish(0)
@@ -451,19 +457,19 @@ def tile_dpfpattention_pb_w4_kernel(tc, x, wv_words, wv_scales, beta, vo, k_phi_
             lay_vo(q, q - 4)
         for q in range(7, 10):
             add_values(q)
-        scale_k(18, 6)
-        quant_k(12, 3)
+        scale_k(22, 4)
+        quant_k(14, 3)
         quant_dv(8, 6)
-        cast_k(24, 4)
-        cast_k(28, 4)
-        values(11, 1)
-        values(12, 2)
+        copy_values(10)
+        cast_k(26, 6)
+        values(11, 0)
+        values(12, 1)
         update(8, 6, 7)
-        values(13, 0)
+        values(13, 2)
         copy_values(11)
         copy_values(12)
-        interleave(18, 2, A)
-        interleave(15, 3, G)
+        interleave(23, 3, A)
+        interleave(17, 3, G, True)
         for q in range(7, 10):
             scale_dv(q)
         finish(8)
@@ -471,34 +477,32 @@ def tile_dpfpattention_pb_w4_kernel(tc, x, wv_words, wv_scales, beta, vo, k_phi_
             lay_vo(q, q - 7)
         for q in range(10, 13):
             add_values(q)
-        scale_k(24, 8)
-        quant_k(18, 2)
-        quant_k(15, 3)
+        scale_k(26, 6)
+        quant_k(17, 3)
         quant_dv(14, 6)
         copy_values(13)
-        interleave(23, 1, A)
-        values(14, 1)
-        values(15, 2)
+        values(14, 0)
+        values(15, 1)
         update(14, 6, 6)
-        interleave(24, 2, A)
         copy_values(14)
+        interleave(28, 2, A)
         copy_values(15)
-        interleave(20, 3, G)
+        interleave(20, 3, G, True)
         for q in range(10, 13):
             scale_dv(q)
         finish(14)
-        for q in range(13, 16):
+        for q in range(13, 15):
             lay_vo(q, q - 10)
-        for q in range(13, 16):
+        for q in range(13, 15):
             add_values(q)
-        interleave(28, 2, A)
-        interleave(30, 2, A)
-        quant_k(23, 1)
-        quant_k(24, 2)
+        quant_k(23, 3)
         quant_k(20, 3)
         quant_dv(20, 6)
+        interleave(30, 2, A)
         update(20, 6, 7)
-        interleave(26, 2, G)
+        lay_vo(15, 5)
+        add_values(15)
+        interleave(26, 2, G, True)
         scale_dv(13)
         scale_dv(14)
         finish(20)

@@ -262,9 +262,14 @@ def tile_dpfpattention_pb_w4_kernel(tc, x, wv_words, wv_scales, beta, vo, k_phi_
                 )
             vps[q] = ps
 
-        def copy_values(q):
-            vts[q] = work.tile([P, N], F32, align_bytes=64, name="vt", bufs=6)
-            nc.scalar.copy(out=vts[q][:], in_=vps[q][:])
+        def copy_values(q, engine=nc.scalar, t0=0, t1=PACK):
+            if q not in vts:
+                vts[q] = work.tile([P, N], F32, align_bytes=64, name="vt", bufs=6)
+            cols = slice(P * t0, P * t1)
+            if engine is nc.vector:
+                nc.vector.tensor_copy(out=vts[q][:, cols], in_=vps[q][:, cols])
+            else:
+                nc.scalar.copy(out=vts[q][:, cols], in_=vps[q][:, cols])
 
         def lay_vo(q, i):
             ps = bank(i, [2, DH // 2, PACK, 2])
@@ -349,160 +354,169 @@ def tile_dpfpattention_pb_w4_kernel(tc, x, wv_words, wv_scales, beta, vo, k_phi_
         load_kphi(8, 2)
         load_weight_scales(0)
         load_weight(0)
-        load_kphi(10, 4)
+        load_kphi(10, 2)
+        load_kphi(12, 3)
         load_vo(0, 4)
         load_weight_scales(1)
         load_weight(1)
-        load_x(1, 2, 2)
         load_vo(4, 4)
-        load_kphi(14, 4)
+        load_x(1, 2, 2)
         load_vo(8, 6)
-        load_kphi(18, 4)
+        load_kphi(15, 3)
+        load_kphi(18, 6)
         load_vo(14, 6)
-        load_kphi(22, 4)
         load_W(0, 8)
-        load_kphi(26, 6)
+        load_kphi(24, 4)
         load_vo(20, 6)
+        load_kphi(28, 4)
         load_W(8, 6)
         load_vo(26, 6)
         load_W(14, 6)
         load_W(20, 6)
         load_W(26, 6)
 
+        for h0, nh in [(0, 2), (2, 2), (4, 2), (6, 2), (8, 1), (9, 6), (15, 3), (18, 8), (26, 6)]:
+            k_group(list(range(h0, h0 + nh)))
         dv_group(0, 8)
         for h0 in range(FIRST, HEADS, 6):
             dv_group(h0, 6)
-        for h0, nh in [(0, 2), (2, 2), (4, 2), (6, 2), (8, 6), (14, 6), (20, 6), (26, 6)]:
-            k_group(list(range(h0, h0 + nh)))
 
-        widen_k(0, 4, V)
-        warm_up(6)
-        turn_x(0, 0, 0)
-        cast_k(4, 2)
-        copy_x(0, 0)
-        warm_up(6)
-        turn_x(0, 1, 1)
-        copy_x(0, 1)
-        turn_x(0, 2, 2)
-        turn_x(0, 3, 3)
-        copy_x(0, 2)
-        copy_x(0, 3)
+        widen_k(0, 3, V)
+        widen_k(3, 3, A)
         interleave(0, 2, V)
         interleave(2, 2, V)
         quant_k(0, 2)
-        scale_k(4, 2)
         quant_k(2, 2)
+        warm_up(6)
+        warm_up(7)
+        turn_x(0, 0, 0)
+        copy_x(0, 0)
+        warm_up(6)
+        for t in range(1, PACK):
+            turn_x(0, t, t % 3)
+            copy_x(0, t)
         interleave(4, 2, V)
+        widen_k(6, 1, V)
         quant_x(0, 0)
-        warm_up(6)
-        turn_beta(7)
-        turn_x(1, 0, 0)
-        turn_x(1, 1, 1)
-        cast_k(6, 2)
-        copy_beta()
-        copy_x(1, 0)
-        copy_x(1, 1)
-        warm_up(6)
-        cast_k(8, 2)
-        widen_k(10, 4, A)
+        widen_k(7, 1, A)
         quant_k(4, 2)
         quant_x(0, 1)
-        scale_k(6, 2)
-        interleave(6, 2, V, True)
-        quant_x(1, 0)
-        scale_k(8, 2)
+        warm_up(6)
+        turn_beta(7)
+        copy_beta()
+        turn_x(1, 0, 1)
+        turn_x(1, 1, 2)
+        widen_k(8, 1, A)
+        interleave(6, 2, V)
+        copy_x(1, 0)
+        copy_x(1, 1)
+        widen_k(9, 1, A)
+        first_values(0, 0, 3)
+        first_values(0, 1, 4)
         quant_k(6, 2)
-        for t in range(PACK):
-            first_values(0, t, 3 + t)
-        interleave(8, 3, G, True)
-        interleave(11, 3, G)
+        interleave(8, 1, V, True)
+        widen_k(10, 2, V)
+        first_values(0, 2, 5)
+        first_values(0, 3, 6)
+        widen_k(12, 3, A)
+        quant_x(1, 0)
+        quant_k(8, 1)
+        interleave(9, 3, G, True)
+        interleave(12, 3, G)
         for h0 in range(0, FIRST, 4):
-            for h in range(h0, h0 + 4, 2):
-                for t in range(PACK):
-                    first_subtract(h, 2, t)
+            for t in range(PACK - 1):
+                first_subtract(h0, 4, t)
+            first_subtract(h0, 2, PACK - 1)
+            first_subtract(h0 + 2, 2, PACK - 1)
             first_scale(h0, 4)
-        for q in range(4, 7):
-            values(q, (q - 4) % 3)
-            copy_values(q)
-        turn_x(1, 2, 0)
-        turn_x(1, 3, 1)
+        values(4, 0)
+        values(5, 1)
+        values(6, 2)
+        copy_values(4)
+        values(7, 0)
+        copy_values(5)
+        copy_values(6)
+        turn_x(1, 2, 1)
+        turn_x(1, 3, 2)
+        copy_values(7)
         copy_x(1, 2)
         copy_x(1, 3)
-        values(7, 2)
-        cast_k(14, 4)
+        widen_k(15, 3, A)
         for q in range(4, 7):
             lay_vo(q, q - 1)
         for q in range(4, 7):
             add_values(q)
+        quant_k(12, 3)
         quant_x(1, 1)
-        quant_k(11, 3)
-        scale_k(14, 4)
-        quant_k(8, 3)
+        quant_k(9, 3)
         quant_dv(0, 8)
-        copy_values(7)
-        widen_k(18, 2, A)
         values(8, 0)
         values(9, 1)
         update(0, 8, 6)
         values(10, 2)
+        interleave(15, 3, G, True)
+        cast_k(18, 4)
         copy_values(8)
         copy_values(9)
-        cast_k(22, 4)
-        widen_k(20, 2, A)
-        interleave(14, 3, G, True)
+        widen_k(22, 2, A)
         for q in range(4, 7):
             scale_dv(q)
         finish(0)
+        copy_values(10, V, 0, 2)
+        copy_values(10, A, 2, 4)
         for q in range(7, 10):
             lay_vo(q, q - 4)
         for q in range(7, 10):
             add_values(q)
-        scale_k(22, 4)
-        quant_k(14, 3)
-        quant_dv(8, 6)
-        copy_values(10)
-        cast_k(26, 6)
         values(11, 0)
         values(12, 1)
+        scale_k(18, 4)
+        quant_k(15, 3)
+        quant_dv(8, 6)
         update(8, 6, 7)
         values(13, 2)
+        interleave(18, 3, G, True)
+        widen_k(24, 1, A)
         copy_values(11)
+        cast_k(28, 4)
         copy_values(12)
-        interleave(23, 3, A)
-        interleave(17, 3, G, True)
+        widen_k(25, 1, A)
         for q in range(7, 10):
             scale_dv(q)
         finish(8)
+        copy_values(13, V, 0, 2)
+        copy_values(13, A, 2, 4)
         for q in range(10, 13):
             lay_vo(q, q - 7)
         for q in range(10, 13):
             add_values(q)
-        scale_k(26, 6)
-        quant_k(17, 3)
+        scale_k(28, 4)
+        quant_k(18, 3)
         quant_dv(14, 6)
-        copy_values(13)
         values(14, 0)
-        values(15, 1)
         update(14, 6, 6)
+        interleave(21, 3, G, True)
+        interleave(24, 2, A)
         copy_values(14)
-        interleave(28, 2, A)
-        copy_values(15)
-        interleave(20, 3, G, True)
+        widen_k(26, 2, A)
         for q in range(10, 13):
             scale_dv(q)
         finish(14)
-        for q in range(13, 15):
-            lay_vo(q, q - 10)
-        for q in range(13, 15):
-            add_values(q)
-        quant_k(23, 3)
-        quant_k(20, 3)
-        quant_dv(20, 6)
+        lay_vo(13, 3)
+        add_values(13)
+        values(15, 1)
+        lay_vo(14, 4)
+        add_values(14)
+        copy_values(15)
+        interleave(26, 2, A)
         interleave(30, 2, A)
+        quant_k(24, 2)
+        quant_k(21, 3)
+        quant_dv(20, 6)
         update(20, 6, 7)
         lay_vo(15, 5)
         add_values(15)
-        interleave(26, 2, G, True)
+        interleave(28, 2, G, True)
         scale_dv(13)
         scale_dv(14)
         finish(20)
@@ -513,6 +527,6 @@ def tile_dpfpattention_pb_w4_kernel(tc, x, wv_words, wv_scales, beta, vo, k_phi_
         update(26, 4, 6)
         quant_k(30, 2)
         quant_dv(30, 2)
-        update(30, 2, 7)
+        update(30, 2, 0)
         finish(26)
         finish(30)

@@ -325,13 +325,14 @@ def tile_dpfpattention_pb_w4_kernel(tc, x, wv_words, wv_scales, beta, vo, k_phi_
                     start=True,
                     stop=True,
                 )
-            ops[h0] = (ps[:].rearrange("p (h d) -> p h d", d=DH), nh)
+            for j in range(nh):
+                ops[h0 + j] = (ps[:].rearrange("p (h d) -> p h d", d=DH), j)
 
-        def finish(h0):
-            ps, nh = ops[h0]
+        def finish(h0, nh):
+            ps, j = ops[h0]
             w, i = ws[h0]
             ot = keep.tile([P, nh, DH], F32, align_bytes=64, name=f"ot_{h0}")
-            nc.vector.tensor_tensor(out=ot[:], in0=ps, in1=w[:, i : i + nh, :], op=ALU.add)
+            nc.vector.tensor_tensor(out=ot[:], in0=ps[:, j : j + nh], in1=w[:, i : i + nh, :], op=ALU.add)
             nc.sync.dma_start(out=out_heads[:, h0 : h0 + nh, :], in_=ot[:])
 
         def warm_up(i):
@@ -364,12 +365,14 @@ def tile_dpfpattention_pb_w4_kernel(tc, x, wv_words, wv_scales, beta, vo, k_phi_
         load_vo(8, 6)
         load_kphi(15, 3)
         load_kphi(18, 6)
+        load_W(0, 4)
         load_vo(14, 6)
-        load_W(0, 8)
-        load_kphi(24, 4)
-        load_vo(20, 6)
+        load_W(4, 4)
+        load_kphi(24, 2)
         load_kphi(28, 4)
         load_W(8, 6)
+        load_vo(20, 6)
+        load_kphi(26, 2)
         load_vo(26, 6)
         load_W(14, 6)
         load_W(20, 6)
@@ -461,7 +464,7 @@ def tile_dpfpattention_pb_w4_kernel(tc, x, wv_words, wv_scales, beta, vo, k_phi_
         widen_k(22, 2, A)
         for q in range(4, 7):
             scale_dv(q)
-        finish(0)
+        finish(0, 4)
         copy_values(10, V, 0, 2)
         copy_values(10, A, 2, 4)
         for q in range(7, 10):
@@ -483,9 +486,9 @@ def tile_dpfpattention_pb_w4_kernel(tc, x, wv_words, wv_scales, beta, vo, k_phi_
         widen_k(25, 1, A)
         for q in range(7, 10):
             scale_dv(q)
-        finish(8)
-        copy_values(13, V, 0, 2)
-        copy_values(13, A, 2, 4)
+        finish(4, 4)
+        finish(8, 6)
+        copy_values(13)
         for q in range(10, 13):
             lay_vo(q, q - 7)
         for q in range(10, 13):
@@ -501,7 +504,7 @@ def tile_dpfpattention_pb_w4_kernel(tc, x, wv_words, wv_scales, beta, vo, k_phi_
         widen_k(26, 2, A)
         for q in range(10, 13):
             scale_dv(q)
-        finish(14)
+        finish(14, 6)
         lay_vo(13, 3)
         add_values(13)
         values(15, 1)
@@ -519,7 +522,7 @@ def tile_dpfpattention_pb_w4_kernel(tc, x, wv_words, wv_scales, beta, vo, k_phi_
         interleave(28, 2, G, True)
         scale_dv(13)
         scale_dv(14)
-        finish(20)
+        finish(20, 6)
         quant_dv(26, 4)
         quant_k(28, 2)
         quant_k(26, 2)
@@ -528,5 +531,5 @@ def tile_dpfpattention_pb_w4_kernel(tc, x, wv_words, wv_scales, beta, vo, k_phi_
         quant_k(30, 2)
         quant_dv(30, 2)
         update(30, 2, 0)
-        finish(26)
-        finish(30)
+        finish(26, 4)
+        finish(30, 2)

@@ -180,12 +180,13 @@ def tile_dpfpattention_pb_w4_kernel(tc, x, wv_words, wv_scales, beta, vo, k_phi_
             by_column = pl[:, :, i : i + nh].rearrange("p t h s -> p h s t")
             if engine is nc.gpsimd:
                 nc.gpsimd.tensor_scalar(out=it[:], in0=by_column, scalar1=1.0, scalar2=0.0, op0=ALU.mult, op1=ALU.add)
-            elif engine is nc.scalar:
-                nc.scalar.copy(out=it[:], in_=by_column)
             else:
-                dst = it[:].rearrange("p h (c i) t -> p h c t i", i=RUN)
-                src = pl[:, :, i : i + nh].rearrange("p t h (c i) -> p h c t i", i=RUN)
-                nc.vector.tensor_copy(out=dst, in_=src)
+                dst = it[:].rearrange("p h (c i) t -> p (h c) t i", i=RUN)
+                src = pl[:, :, i : i + nh].rearrange("p t h (c i) -> p (h c) t i", i=RUN)
+                if engine is nc.scalar:
+                    nc.scalar.copy(out=dst, in_=src)
+                else:
+                    nc.vector.tensor_copy(out=dst, in_=src)
             for j in range(nh):
                 inter[members[h0][i + j]] = (it, j)
 

@@ -369,11 +369,10 @@ def tile_dpfpattention_pb_w4_kernel(tc, x, wv_words, wv_scales, beta, vo, k_phi_
         load_W(0, 4)
         load_vo(14, 6)
         load_W(4, 4)
-        load_kphi(24, 2)
-        load_kphi(28, 4)
+        load_kphi(24, 4)
         load_W(8, 6)
         load_vo(20, 6)
-        load_kphi(26, 2)
+        load_kphi(28, 4)
         load_vo(26, 6)
         load_W(14, 6)
         load_W(20, 6)
@@ -385,44 +384,46 @@ def tile_dpfpattention_pb_w4_kernel(tc, x, wv_words, wv_scales, beta, vo, k_phi_
         for h0 in range(FIRST, HEADS, 6):
             dv_group(h0, 6)
 
-        widen_k(0, 3, V)
-        widen_k(3, 3, A)
-        interleave(0, 2, V)
-        interleave(2, 2, V)
-        quant_k(0, 2)
-        quant_k(2, 2)
+        widen_k(0, 4, V)
         warm_up(6)
         warm_up(7)
         turn_x(0, 0, 0)
+        cast_k(4, 2)
         copy_x(0, 0)
+        turn_x(0, 1, 1)
         warm_up(6)
-        for t in range(1, PACK):
-            turn_x(0, t, t % 3)
-            copy_x(0, t)
+        copy_x(0, 1)
+        turn_x(0, 2, 2)
+        turn_x(0, 3, 3)
+        cast_k(6, 2)
+        copy_x(0, 2)
+        copy_x(0, 3)
+        interleave(0, 2, V)
+        interleave(2, 2, V)
+        quant_k(0, 2)
+        scale_k(4, 2)
+        quant_k(2, 2)
         interleave(4, 2, V)
-        widen_k(6, 1, V)
         quant_x(0, 0)
-        widen_k(7, 1, A)
-        quant_k(4, 2)
-        quant_x(0, 1)
-        warm_up(6)
         turn_beta(7)
-        copy_beta()
-        turn_x(1, 0, 1)
-        turn_x(1, 1, 2)
+        warm_up(6)
+        turn_x(1, 0, 0)
+        turn_x(1, 1, 1)
         widen_k(8, 1, A)
-        interleave(6, 2, V)
+        copy_beta()
         copy_x(1, 0)
         copy_x(1, 1)
-        widen_k(9, 1, A)
-        first_values(0, 0, 3)
-        first_values(0, 1, 4)
-        quant_k(6, 2)
+        scale_k(6, 2)
+        quant_k(4, 2)
+        quant_x(0, 1)
+        interleave(6, 2, V)
         interleave(8, 1, V, True)
-        widen_k(10, 2, V)
-        first_values(0, 2, 5)
-        first_values(0, 3, 6)
+        for t in range(PACK):
+            first_values(0, t, 3 + t)
+        widen_k(9, 2, A)
         widen_k(12, 3, A)
+        quant_k(6, 2)
+        widen_k(11, 1, V)
         quant_x(1, 0)
         quant_k(8, 1)
         interleave(9, 3, G, True)
@@ -450,18 +451,19 @@ def tile_dpfpattention_pb_w4_kernel(tc, x, wv_words, wv_scales, beta, vo, k_phi_
             lay_vo(q, q - 1)
         for q in range(4, 7):
             add_values(q)
-        quant_k(12, 3)
+        quant_dv(0, 8)
         quant_x(1, 1)
         quant_k(9, 3)
-        quant_dv(0, 8)
+        quant_k(12, 3)
         values(8, 0)
         values(9, 1)
         update(0, 8, 6)
         values(10, 2)
         interleave(15, 3, G, True)
-        cast_k(18, 4)
+        cast_k(20, 2)
         copy_values(8)
         copy_values(9)
+        widen_k(18, 2, A)
         widen_k(22, 2, A)
         for q in range(4, 7):
             scale_dv(q)
@@ -474,17 +476,16 @@ def tile_dpfpattention_pb_w4_kernel(tc, x, wv_words, wv_scales, beta, vo, k_phi_
             add_values(q)
         values(11, 0)
         values(12, 1)
-        scale_k(18, 4)
+        scale_k(20, 2)
         quant_k(15, 3)
         quant_dv(8, 6)
         update(8, 6, 7)
         values(13, 2)
         interleave(18, 3, G, True)
-        widen_k(24, 1, A)
+        widen_k(24, 2, A)
         copy_values(11)
-        cast_k(28, 4)
         copy_values(12)
-        widen_k(25, 1, A)
+        widen_k(26, 2, A)
         for q in range(7, 10):
             scale_dv(q)
         finish(4, 4)
@@ -494,15 +495,14 @@ def tile_dpfpattention_pb_w4_kernel(tc, x, wv_words, wv_scales, beta, vo, k_phi_
             lay_vo(q, q - 7)
         for q in range(10, 13):
             add_values(q)
-        scale_k(28, 4)
+        interleave(24, 2, V)
         quant_k(18, 3)
         quant_dv(14, 6)
         values(14, 0)
         update(14, 6, 6)
         interleave(21, 3, G, True)
-        interleave(24, 2, A)
         copy_values(14)
-        widen_k(26, 2, A)
+        widen_k(28, 4, A)
         for q in range(10, 13):
             scale_dv(q)
         finish(14, 6)
@@ -512,8 +512,8 @@ def tile_dpfpattention_pb_w4_kernel(tc, x, wv_words, wv_scales, beta, vo, k_phi_
         lay_vo(14, 4)
         add_values(14)
         copy_values(15)
-        interleave(26, 2, A)
         interleave(30, 2, A)
+        interleave(26, 2, V)
         quant_k(24, 2)
         quant_k(21, 3)
         quant_dv(20, 6)

@@ -49,8 +49,6 @@ def tile_dpfpattention_pb_w4_kernel(tc, x, wv_words, wv_scales, beta, vo, k_phi_
             nc.gpsimd.memset(wsc[half][:].rearrange("p g n -> p (g n)").bitcast(I32), 0)
         beta_rows = keep.tile([P, N], BF16, align_bytes=64, name="beta_rows")
         nc.vector.memset(beta_rows[:].bitcast(I32), 0)
-        zeros = keep.tile([P, 2 * P], F32, name="zeros")
-        nc.vector.memset(zeros[:], 0.0)
         minus_ident = keep.tile([P, P], BF16, name="minus_ident")
         nc.scalar.activation(out=minus_ident[:], in_=ident[:], func=ACT.Copy, scale=-1.0)
         kb, xs, vos, ws, ww = {}, {}, {}, {}, {}
@@ -336,10 +334,6 @@ def tile_dpfpattention_pb_w4_kernel(tc, x, wv_words, wv_scales, beta, vo, k_phi_
             nc.vector.tensor_tensor(out=ot[:], in0=ps[:, j : j + nh], in1=w[:, i : i + nh, :], op=ALU.add)
             nc.sync.dma_start(out=out_heads[:, h0 : h0 + nh, :], in_=ot[:])
 
-        def warm_up(i):
-            ps = bank(i, [2 * P])
-            nc.tensor.matmul(ps[:], lhsT=zeros[:, 0:P], rhs=zeros[:], start=True, stop=True)
-
         V, A, G = nc.vector, nc.scalar, nc.gpsimd
 
         load_kscale()
@@ -385,13 +379,10 @@ def tile_dpfpattention_pb_w4_kernel(tc, x, wv_words, wv_scales, beta, vo, k_phi_
             dv_group(h0, 6)
 
         widen_k(0, 4, V)
-        warm_up(6)
-        warm_up(7)
         turn_x(0, 0, 0)
         cast_k(4, 2)
         copy_x(0, 0)
         turn_x(0, 1, 1)
-        warm_up(6)
         copy_x(0, 1)
         turn_x(0, 2, 2)
         turn_x(0, 3, 3)
@@ -406,7 +397,6 @@ def tile_dpfpattention_pb_w4_kernel(tc, x, wv_words, wv_scales, beta, vo, k_phi_
         interleave(4, 2, V)
         quant_x(0, 0)
         turn_beta(7)
-        warm_up(6)
         turn_x(1, 0, 0)
         turn_x(1, 1, 1)
         widen_k(8, 1, A)

from contextlib import ExitStack

import concourse.mybir as mybir
from concourse.masks import make_identity

F32 = mybir.dt.float32
BF16 = mybir.dt.bfloat16
I32 = mybir.dt.int32
U32 = mybir.dt.uint32
U8 = mybir.dt.uint8
FP8 = mybir.dt.float8_e4m3fn
E4M3X4 = mybir.dt.float8_e4m3fn_x4
E2M1X4 = mybir.dt.float4_e2m1fn_x4
ALU = mybir.AluOpType
ACT = mybir.ActivationFunctionType

B, N, D, H, DH = 2, 512, 1024, 16, 64
S = 2 * DH
P = 128
PACK = 4
RUN = 4
HEADS = B * H
FIRST = 8
FLOPS = 2 * B * N * D * H * DH + 2 * B * H * N * S * DH


def tile_dpfpattention_pb_w4_kernel(tc, x, wv_words, wv_scales, beta, vo, k_phi_bytes, k_phi_scale, W, out):
    nc = tc.nc
    with ExitStack() as ctx:
        keep = ctx.enter_context(tc.tile_pool(name="keep", bufs=1))
        work = ctx.enter_context(tc.tile_pool(name="work", bufs=4))
        psum = ctx.enter_context(tc.psum_pool(name="psum", bufs=1))
        ctx.enter_context(tc.manual_schedule())

        k_heads = k_phi_bytes.rearrange("b h (p t) s -> p (b h) (t s)", t=PACK)
        vo_heads = vo.rearrange("b h (p t) d -> p (b h) (t d)", t=PACK)
        w_heads = W.rearrange("b h s d -> s (b h) d")
        out_heads = out.rearrange("b h s d -> s (b h) d")

        def bank(i, shape):
            return psum.tile([P] + shape, F32, name="bank", tag=f"bank_{i}", bufs=1)

        kscale = keep.tile([P, PACK], F32, name="kscale")
        ident = keep.tile([P, P], F32, name="ident")
        make_identity(nc, ident[:])
        wsc = {}
        for half in range(2):
            wsc[half] = keep.tile([P, 2, N], U8, align_bytes=64, name=f"wsc_{half}")
            nc.gpsimd.memset(wsc[half][:].rearrange("p g n -> p (g n)").bitcast(I32), 0)
        beta_rows = keep.tile([P, N], BF16, align_bytes=64, name="beta_rows")
        nc.vector.memset(beta_rows[:].bitcast(I32), 0)
        minus_ident = keep.tile([P, P], BF16, name="minus_ident")
        nc.scalar.activation(out=minus_ident[:], in_=ident[:], func=ACT.Copy, scale=-1.0)
        kb, xs, vos, ws, ww = {}, {}, {}, {}, {}

        def load_kscale():
            nc.sync.dma_start(out=kscale[:], in_=k_phi_scale.rearrange("a c (p t) f -> p (a c t f)", t=PACK))

        def load_beta():
            nc.sync.dma_start(out=beta_rows[0:HEADS, :], in_=beta.rearrange("b h n -> (b h) n"))

        def load_kphi(h0, nh):
            kbt = keep.tile([P, nh * PACK * S], U8, align_bytes=64, name=f"kb_{h0}")
            nc.sync.dma_start(out=kbt[:].rearrange("p (h c) -> p h c", h=nh), in_=k_heads[:, h0 : h0 + nh, :])
            for i in range(nh):
                kb[h0 + i] = (kbt, i)

        def load_x(b, t0, nt):
            xt = keep.tile([P, nt, D], BF16, align_bytes=64, name=f"x_{b}_{t0}")
            nc.sync.dma_start(out=xt[:], in_=x[b].rearrange("(p t) k -> p t k", t=PACK)[:, t0 : t0 + nt, :])
            for t in range(nt):
                xs[b, t0 + t] = xt[:, t, :]

        def load_vo(h0, nh):
            v = keep.tile([P, nh, PACK * DH], BF16, align_bytes=64, name=f"vo_{h0}")
            nc.sync.dma_start(out=v[:], in_=vo_heads[:, h0 : h0 + nh, :])
            for i in range(0, nh, 2):
                vos[h0 + i] = (v, i)

        def load_W(h0, nh):
            w = keep.tile([P, nh, DH], BF16, align_bytes=64, name=f"W_{h0}")
            nc.sync.dma_start(out=w[:], in_=w_heads[:, h0 : h0 + nh, :])
            for i in range(nh):
                ws[h0 + i] = (w, i)

        def load_weight(half):
            w = keep.tile([P, 2, D], U8, align_bytes=64, name=f"ww_{half}")
            nc.sync.dma_start(out=w[:], in_=wv_words[:, :, D * half : D * (half + 1)].rearrange("g p n -> p g n"))
            ww[half] = w

        def load_weight_scales(half):
            cols = slice(N * half, N * (half + 1))
            for r in range(4):
                nc.sync.dma_start(
                    out=wsc[half][r:P:32, :, :].bitcast(I32),
                    in_=wv_scales[:, r:16:4, cols].rearrange("g q n -> q g n").bitcast(I32),
                )

        beta2 = keep.tile([P, HEADS - FIRST, 2, PACK], BF16, align_bytes=64, name="beta2")
        turned = {}

        def turn_beta(i):
            bt = bank(i, [P, 2])
            words = beta_rows[:].bitcast(F32)
            for u in range(2):
                nc.tensor.transpose(bt[:, :, u], words[:, u : 2 * P : 2], ident[:])
            turned["beta"] = bt[:].rearrange("p r u -> p (r u)").bitcast(BF16).rearrange("p (r t) -> p r t", t=PACK)

        def copy_beta():
            nc.scalar.copy(out=beta2[:], in_=turned["beta"][:, FIRST:HEADS].unsqueeze(2).to_broadcast([P, HEADS - FIRST, 2, PACK]))

        xg, xcodes, xscales = {}, {}, {}
        for b in range(B):
            for g in range(2):
                xcodes[b, g] = keep.tile([P, N], U32, align_bytes=64, name=f"xc_{b}_{g}")
                xscales[b, g] = keep.tile([P, N], U8, align_bytes=64, name=f"xsc_{b}_{g}")

        def turn_x(b, t, i):
            turned[b, t] = bank(i, [2, 2, P])
            words = xs[b, t].bitcast(F32)
            for g in range(2):
                for u in range(2):
                    nc.tensor.transpose(turned[b, t][:, g, u, :], words[:, 256 * g + u : 256 * (g + 1) : 2], ident[:])

        def copy_x(b, t):
            tp, i = divmod(t, 2)
            if i == 0:
                xg[b, tp] = work.tile([P, 2, 2 * P * PACK], BF16, align_bytes=64, name="xg", bufs=3)
            dst = xg[b, tp][:, :, P * PACK * i : P * PACK * (i + 1)].bitcast(F32).rearrange("p g (r u) -> p g r u", u=2)
            nc.scalar.copy(out=dst, in_=turned[b, t][:].rearrange("p g u r -> p g r u"))

        def quant_x(b, tp):
            cols = slice(2 * P * tp, 2 * P * (tp + 1))
            for g in range(2):
                nc.vector.quantize_mx(out=xcodes[b, g][:, cols].bitcast(E4M3X4), scales=xscales[b, g][:, cols], in_=xg[b, tp][:, g, :])

        casts, planes, members, inter, kc = {}, {}, {}, {}, {}

        def k_group(heads):
            pl = keep.tile([P, PACK, len(heads), S], BF16, align_bytes=64, name=f"planes_{heads[0]}")
            for i, h in enumerate(heads):
                planes[h] = (pl, i)
                members[h] = heads

        def widen_k(h0, nh, engine):
            for h in range(h0, h0 + nh):
                kbt, j = kb[h]
                pl, i = planes[h]
                for t in range(PACK):
                    src = kbt[:, S * (PACK * j + t) : S * (PACK * j + t + 1)].bitcast(FP8)
                    if engine is nc.vector:
                        nc.vector.tensor_scalar(out=pl[:, t, i, :], in0=src, scalar1=kscale[:, t : t + 1], scalar2=None, op0=ALU.mult)
                    else:
                        nc.scalar.activation(out=pl[:, t, i, :], in_=src, func=ACT.Copy, scale=kscale[:, t : t + 1])

        def cast_k(h0, nh):
            kbt, j = kb[h0]
            if h0 not in casts:
                heads = members[h0][planes[h0][1] :]
                tile = work.tile([P, len(heads), PACK, S], BF16, align_bytes=64, name="cast", bufs=3)
                for i, h in enumerate(heads):
                    casts[h] = (tile, i)
            cast, i = casts[h0]
            nc.scalar.copy(out=cast[:, i : i + nh].rearrange("p h t s -> p (h t s)"), in_=kbt[:, PACK * S * j : PACK * S * (j + nh)].bitcast(FP8))

        def scale_k(h0, nh):
            cast, j = casts[h0]
            pl, i = planes[h0]
            for t in range(PACK):
                nc.vector.tensor_scalar(out=pl[:, t, i : i + nh], in0=cast[:, j : j + nh, t, :], scalar1=kscale[:, t : t + 1], scalar2=None, op0=ALU.mult)

        def interleave(h0, nh, engine, gated=False):
            if gated:
                it = work.tile([P, nh, S, PACK], BF16, align_bytes=64, name="inter_gated", bufs=1)
            else:
                it = keep.tile([P, nh, S, PACK], BF16, align_bytes=64, name=f"inter_{h0}")
            pl, i = planes[h0]
            by_column = pl[:, :, i : i + nh].rearrange("p t h s -> p h s t")
            if engine is nc.gpsimd:
                nc.gpsimd.tensor_scalar(out=it[:], in0=by_column, scalar1=1.0, scalar2=0.0, op0=ALU.mult, op1=ALU.add)
            else:
                dst = it[:].rearrange("p h (c i) t -> p (h c) t i", i=RUN)
                src = pl[:, :, i : i + nh].rearrange("p t h (c i) -> p (h c) t i", i=RUN)
                if engine is nc.scalar:
                    nc.scalar.copy(out=dst, in_=src)
                else:
                    nc.vector.tensor_copy(out=dst, in_=src)
            for j in range(nh):
                inter[members[h0][i + j]] = (it, j)

        def quant_k(h0, nh):
            it, j = inter[h0]
            codes = keep.tile([P, nh, S], U32, align_bytes=64, name=f"kc_{h0}")
            scales = keep.tile([P, nh, S], U8, align_bytes=64, name=f"ksc_{h0}")
            nc.vector.quantize_mx(
                out=codes[:].rearrange("p h s -> p (h s)").bitcast(E4M3X4),
                scales=scales[:].rearrange("p h s -> p (h s)"),
                in_=it[:, j : j + nh].rearrange("p h s t -> p (h s t)"),
            )
            first = planes[h0][1]
            for i in range(nh):
                kc[members[h0][first + i]] = (codes[:, i, :], scales[:, i, :])

        vps, vts, diffs, dvg, ops = {}, {}, {}, {}, {}

        def first_values(h0, t, i):
            b, half = divmod(h0 // 8, 2)
            ps = bank(i, [8 * DH])
            cols = slice(P * t, P * (t + 1))
            for g in range(2):
                nc.tensor.matmul_mx(
                    out=ps[:],
                    lhsT=xcodes[b, g][:, cols].bitcast(E4M3X4),
                    lhsT_scale=xscales[b, g][:, cols],
                    rhs=ww[half][:, g, :].bitcast(E2M1X4),
                    rhs_scale=wsc[half][:, g, :],
                    start=(g == 0),
                    stop=(g == 1),
                )
            vps["first", h0, t] = ps

        first_diff = keep.tile([P, FIRST, DH // RUN, PACK, RUN], F32, align_bytes=64, name="first_diff")

        def first_subtract(h0, nh, t):
            v, i = vos[h0]
            j = h0 % 8
            nc.vector.tensor_tensor(
                out=first_diff[:, h0 : h0 + nh, :, t, :],
                in0=vps["first", h0 - j, t][:, DH * j : DH * (j + nh)].rearrange("p (h c i) -> p h c i", h=nh, i=RUN),
                in1=v[:, i : i + nh, DH * t : DH * (t + 1)].rearrange("p h (c i) -> p h c i", i=RUN),
                op=ALU.subtract,
            )

        def dv_group(h0, nh):
            dg = keep.tile([P, nh, DH, PACK], BF16, align_bytes=64, name=f"dvg_{h0}")
            for i in range(nh):
                dvg[h0 + i] = (dg, i)

        def first_scale(h0, nh):
            for h in range(h0, h0 + nh):
                dg, i = dvg[h]
                nc.vector.tensor_tensor(
                    out=dg[:, i].rearrange("p (c i) t -> p c t i", i=RUN),
                    in0=first_diff[:, h],
                    in1=turned["beta"][:, h].unsqueeze(1).unsqueeze(3).to_broadcast([P, DH // RUN, PACK, RUN]),
                    op=ALU.mult,
                )

        def values(q, i):
            b, j = divmod(q, H // 2)
            ps = bank(i, [N])
            for g in range(2):
                nc.tensor.matmul_mx(
                    out=ps[:],
                    lhsT=ww[j // 4][:, g, 2 * P * (j % 4) : 2 * P * (j % 4 + 1)].bitcast(E2M1X4),
                    lhsT_scale=wsc[j // 4][:, g, P * (j % 4) : P * (j % 4 + 1)],
                    rhs=xcodes[b, g][:].bitcast(E4M3X4),
                    rhs_scale=xscales[b, g][:],
                    start=(g == 0),
                    stop=(g == 1),
                )
            vps[q] = ps

        def copy_values(q, engine=nc.scalar, t0=0, t1=PACK):
            if q not in vts:
                vts[q] = work.tile([P, N], F32, align_bytes=64, name="vt", bufs=6)
            cols = slice(P * t0, P * t1)
            if engine is nc.vector:
                nc.vector.tensor_copy(out=vts[q][:, cols], in_=vps[q][:, cols])
            else:
                nc.scalar.copy(out=vts[q][:, cols], in_=vps[q][:, cols])

        def lay_vo(q, i):
            ps = bank(i, [2, DH // 2, PACK, 2])
            v, j = vos[2 * q]
            nc.tensor.matmul(
                ps[:].rearrange("p h c t e -> p t h c e"),
                lhsT=minus_ident[:],
                rhs=v[:, j : j + 2].rearrange("p h (t c e) -> p t h c e", t=PACK, e=2),
                start=True,
                stop=False,
            )
            diffs[q] = ps

        def add_values(q):
            for t in range(PACK):
                nc.tensor.matmul(
                    diffs[q][:, :, :, t, :],
                    lhsT=vts[q][:, P * t : P * (t + 1)],
                    rhs=ident[:],
                    start=False,
                    stop=(t == PACK - 1),
                    is_transpose=True,
                )

        def scale_dv(q):
            dg, i = dvg[2 * q]
            nc.vector.tensor_tensor(
                out=dg[:, i : i + 2].rearrange("p h (c e) t -> p h c e t", e=2),
                in0=diffs[q][:].rearrange("p h c t e -> p h c e t"),
                in1=beta2[:, 2 * q - FIRST : 2 * q - FIRST + 2].unsqueeze(2).to_broadcast([P, 2, DH // 2, 2, PACK]),
                op=ALU.mult,
            )

        dcodes = keep.tile([P, HEADS * DH], U32, align_bytes=64, name="dcodes")
        dscales = keep.tile([P, HEADS * DH], U8, align_bytes=64, name="dscales")

        def quant_dv(h0, nh):
            dg, i = dvg[h0]
            cols = slice(DH * h0, DH * (h0 + nh))
            nc.vector.quantize_mx(out=dcodes[:, cols].bitcast(E4M3X4), scales=dscales[:, cols], in_=dg[:, i : i + nh].rearrange("p h d t -> p (h d t)"))

        def update(h0, nh, i):
            ps = bank(i, [nh * DH])
            for h in reversed(range(h0, h0 + nh)):
                kcodes, kscales = kc[h]
                first = max(h - 1, h0)
                nc.tensor.matmul_mx(
                    out=ps[:, DH * (first - h0) : DH * (h + 1 - h0)],
                    lhsT=kcodes.bitcast(E4M3X4),
                    lhsT_scale=kscales,
                    rhs=dcodes[:, DH * first : DH * (h + 1)].bitcast(E4M3X4),
                    rhs_scale=dscales[:, DH * first : DH * (h + 1)],
                    start=True,
                    stop=True,
                )
            for j in range(nh):
                ops[h0 + j] = (ps[:].rearrange("p (h d) -> p h d", d=DH), j)

        def finish(h0, nh):
            ps, j = ops[h0]
            w, i = ws[h0]
            ot = keep.tile([P, nh, DH], F32, align_bytes=64, name=f"ot_{h0}")
            nc.vector.tensor_tensor(out=ot[:], in0=ps[:, j : j + nh], in1=w[:, i : i + nh, :], op=ALU.add)
            nc.sync.dma_start(out=out_heads[:, h0 : h0 + nh, :], in_=ot[:])

        V, A, G = nc.vector, nc.scalar, nc.gpsimd

        load_kscale()
        load_kphi(0, 2)
        load_kphi(2, 2)
        load_x(0, 0, 1)
        load_kphi(4, 2)
        load_x(0, 1, 1)
        load_x(0, 2, 1)
        load_x(0, 3, 1)
        load_kphi(6, 2)
        load_beta()
        load_x(1, 0, 2)
        load_kphi(8, 2)
        load_weight_scales(0)
        load_weight(0)
        load_kphi(10, 2)
        load_kphi(12, 3)
        load_vo(0, 4)
        load_weight_scales(1)
        load_weight(1)
        load_vo(4, 4)
        load_x(1, 2, 2)
        load_vo(8, 6)
        load_kphi(15, 3)
        load_kphi(18, 6)
        load_W(0, 4)
        load_vo(14, 6)
        load_W(4, 4)
        load_kphi(24, 4)
        load_W(8, 6)
        load_vo(20, 6)
        load_kphi(28, 4)
        load_vo(26, 6)
        load_W(14, 6)
        load_W(20, 6)
        load_W(26, 6)

        for h0, nh in [(0, 2), (2, 2), (4, 2), (6, 2), (8, 1), (9, 6), (15, 3), (18, 8), (26, 6)]:
            k_group(list(range(h0, h0 + nh)))
        dv_group(0, 8)
        for h0 in range(FIRST, HEADS, 6):
            dv_group(h0, 6)

        widen_k(0, 4, V)
        turn_x(0, 0, 0)
        cast_k(4, 2)
        copy_x(0, 0)
        turn_x(0, 1, 1)
        copy_x(0, 1)
        turn_x(0, 2, 2)
        turn_x(0, 3, 3)
        cast_k(6, 2)
        copy_x(0, 2)
        copy_x(0, 3)
        interleave(0, 2, V)
        interleave(2, 2, V)
        quant_k(0, 2)
        scale_k(4, 2)
        quant_k(2, 2)
        interleave(4, 2, V)
        quant_x(0, 0)
        turn_beta(7)
        turn_x(1, 0, 0)
        turn_x(1, 1, 1)
        widen_k(8, 1, A)
        copy_beta()
        copy_x(1, 0)
        copy_x(1, 1)
        scale_k(6, 2)
        quant_k(4, 2)
        quant_x(0, 1)
        interleave(6, 2, V)
        interleave(8, 1, V, True)
        for t in range(PACK):
            first_values(0, t, 3 + t)
        widen_k(9, 2, A)
        widen_k(12, 3, A)
        quant_k(6, 2)
        widen_k(11, 1, V)
        quant_x(1, 0)
        quant_k(8, 1)
        interleave(9, 3, G, True)
        interleave(12, 3, G)
        for h0 in range(0, FIRST, 4):
            for t in range(PACK - 1):
                first_subtract(h0, 4, t)
            first_subtract(h0, 2, PACK - 1)
            first_subtract(h0 + 2, 2, PACK - 1)
            first_scale(h0, 4)
        values(4, 0)
        values(5, 1)
        values(6, 2)
        copy_values(4)
        values(7, 0)
        copy_values(5)
        copy_values(6)
        turn_x(1, 2, 1)
        turn_x(1, 3, 2)
        copy_values(7)
        copy_x(1, 2)
        copy_x(1, 3)
        widen_k(15, 3, A)
        for q in range(4, 7):
            lay_vo(q, q - 1)
        for q in range(4, 7):
            add_values(q)
        quant_dv(0, 8)
        quant_x(1, 1)
        quant_k(9, 3)
        quant_k(12, 3)
        values(8, 0)
        values(9, 1)
        update(0, 8, 6)
        values(10, 2)
        interleave(15, 3, G, True)
        cast_k(20, 2)
        copy_values(8)
        copy_values(9)
        widen_k(18, 2, A)
        widen_k(22, 2, A)
        for q in range(4, 7):
            scale_dv(q)
        finish(0, 4)
        copy_values(10, V, 0, 2)
        copy_values(10, A, 2, 4)
        for q in range(7, 10):
            lay_vo(q, q - 4)
        for q in range(7, 10):
            add_values(q)
        values(11, 0)
        values(12, 1)
        scale_k(20, 2)
        quant_k(15, 3)
        quant_dv(8, 6)
        update(8, 6, 7)
        values(13, 2)
        interleave(18, 3, G, True)
        widen_k(24, 2, A)
        copy_values(11)
        copy_values(12)
        widen_k(26, 2, A)
        for q in range(7, 10):
            scale_dv(q)
        finish(4, 4)
        finish(8, 6)
        copy_values(13)
        for q in range(10, 13):
            lay_vo(q, q - 7)
        for q in range(10, 13):
            add_values(q)
        interleave(24, 2, V)
        quant_k(18, 3)
        quant_dv(14, 6)
        values(14, 0)
        update(14, 6, 6)
        interleave(21, 3, G, True)
        copy_values(14)
        widen_k(28, 4, A)
        for q in range(10, 13):
            scale_dv(q)
        finish(14, 6)
        lay_vo(13, 3)
        add_values(13)
        values(15, 1)
        lay_vo(14, 4)
        add_values(14)
        copy_values(15)
        interleave(30, 2, A)
        interleave(26, 2, V)
        quant_k(24, 2)
        quant_k(21, 3)
        quant_dv(20, 6)
        update(20, 6, 7)
        lay_vo(15, 5)
        add_values(15)
        interleave(28, 2, G, True)
        scale_dv(13)
        scale_dv(14)
        finish(20, 6)
        quant_dv(26, 4)
        quant_k(28, 2)
        quant_k(26, 2)
        scale_dv(15)
        update(26, 4, 6)
        quant_k(30, 2)
        quant_dv(30, 2)
        update(30, 2, 0)
        finish(26, 4)
        finish(30, 2)
